import numpy as np
import ml_dtypes


def mxq(x, axis, fmt="e4m3"):
    dtype, down = {"e4m3": (ml_dtypes.float8_e4m3fn, 7), "e5m2": (ml_dtypes.float8_e5m2, 14)}[fmt]
    v = np.moveaxis(np.asarray(x, np.float32).astype(ml_dtypes.bfloat16).astype(np.float64), axis, -1)
    blocks = v.reshape(v.shape[:-1] + (-1, 32))
    amax = np.abs(blocks).max(-1, keepdims=True)
    byte = np.maximum(np.where(amax > 0, np.frexp(amax)[1] - 1 + 127, 0) - down, 1)
    scale = np.exp2(byte - 127.0)
    codes = (blocks / scale).astype(np.float32).astype(dtype).astype(np.float64)
    return np.moveaxis((codes * scale).reshape(v.shape), -1, axis)


WIDE = False


def mx_kscale(k):
    if not WIDE:
        return np.ones(k)
    levels = np.array([10, -10, 5, -5, 0])
    a = np.random.permutation(np.resize(levels, k // 512 * 4)).reshape(k // 512, 4)
    idx = np.arange(k)
    return np.exp2(a[idx // 512, idx % 128 // 32])


BF16 = ml_dtypes.bfloat16


def bf(x):
    return np.asarray(x, np.float32).astype(BF16)


def f64(x):
    return np.asarray(x).astype(np.float64)


B, SIDE, HE, Z, HD, XO = 1024, 32, 1024, 512, 2048, 1024


def setup_inputs():
    n = np.random.standard_normal
    s, t = mx_kscale(HE), mx_kscale(Z)
    return {"h": bf(np.tanh(n((B, HE))) * s),
            "W_mu_e": bf(n((Z, HE)) * 1.5 / np.sqrt(HE) / s[None, :] * t[:, None]),
            "b_mu_e": bf(n(Z) * 0.3 * t),
            "W_ls_e": bf(n((Z, HE)) * 1.5 / np.sqrt(HE) / s[None, :]),
            "b_ls_e": bf(n(Z) * 0.3),
            "eps_z": bf(n((B, Z)) * t),
            "W_in_d": bf(n((HD, Z)) * 0.6 / np.sqrt(Z) / t[None, :]),
            "b_in_d": bf(n(HD) * 0.3)}


def reference(h, W_mu_e, b_mu_e, W_ls_e, b_ls_e, eps_z, W_in_d, b_in_d):
    hq = mxq(f64(h), 1, "e4m3")
    mu_e = (hq @ mxq(f64(W_mu_e), 1, "e4m3").T) + f64(b_mu_e)
    ls_e = (hq @ mxq(f64(W_ls_e), 1, "e4m3").T) + f64(b_ls_e)
    z = mu_e + np.exp(0.5 * ls_e) * f64(eps_z)
    return np.tanh((mxq(z, 1, "e4m3") @ mxq(f64(W_in_d), 1, "e4m3").T) + f64(b_in_d))

@@ -1,0 +1,215 @@
+from contextlib import ExitStack
+
+import concourse.mybir as mybir
+from concourse.masks import make_identity
+
+FLOPS = 2 * 1024 * 1024 * 1024 + 2 * 1024 * 512 * 2048
+
+F32 = mybir.dt.float32
+BF16 = mybir.dt.bfloat16
+U32 = mybir.dt.uint32
+U8 = mybir.dt.uint8
+FP8X4 = mybir.dt.float8_e4m3fn_x4
+ACT = mybir.ActivationFunctionType
+ALU = mybir.AluOpType
+
+P = 128
+
+
+def tile_vae_pa_kernel(tc, h, W_mu_e, b_mu_e, W_ls_e, b_ls_e, eps_z, W_in_d, b_in_d, out):
+    nc = tc.nc
+    with ExitStack() as ctx:
+        keep = ctx.enter_context(tc.tile_pool(name="keep", bufs=1))
+        work = ctx.enter_context(tc.tile_pool(name="work", bufs=2))
+        psum = ctx.enter_context(tc.psum_pool(name="psum", bufs=2))
+
+        h_sb = keep.tile([P, 8, 1024], BF16)
+        wmu_sb = keep.tile([P, 2, 2, 1024], BF16)
+        wls_sb = keep.tile([P, 2, 2, 1024], BF16)
+        eps_sb = keep.tile([P, 8, 512], BF16)
+        wd_sb = keep.tile([P, 16, 512], BF16)
+        bd_sb = keep.tile([P, 2048], BF16)
+        braw = keep.tile([P, P], F32)
+        ident = keep.tile([P, P], F32)
+        bmu = keep.tile([P, 4], F32)
+        hbls = keep.tile([P, 4], F32)
+
+        h_codes = keep.tile([P, 2, 1024], U32, align_bytes=64)
+        h_scales = keep.tile([P, 2, 1024], U8, align_bytes=64)
+        wmu_codes = keep.tile([P, 4, 256], U32, align_bytes=64)
+        wmu_scales = keep.tile([P, 4, 256], U8, align_bytes=64)
+        wls_codes = keep.tile([P, 4, 256], U32, align_bytes=64)
+        wls_scales = keep.tile([P, 4, 256], U8, align_bytes=64)
+        d_codes = keep.tile([P, 2048], U32, align_bytes=64)
+        d_scales = keep.tile([P, 2048], U8, align_bytes=64)
+        z_codes = keep.tile([P, 1024], U32, align_bytes=64)
+        z_scales = keep.tile([P, 1024], U8, align_bytes=64)
+
+        w_sb = {"mu": wmu_sb, "ls": wls_sb}
+        w_codes = {"mu": wmu_codes, "ls": wls_codes}
+        w_scales = {"mu": wmu_scales, "ls": wls_scales}
+
+        nc.vector.memset(braw[:], 0.0)
+        make_identity(nc, ident[:])
+
+        h_v = h.rearrange("(p j) k -> p j k", j=8)
+        eps_v = eps_z.rearrange("(p j) z -> p j z", j=8)
+        wmu_v = W_mu_e.rearrange("(u p e) k -> p u e k", u=2, e=2)
+        wls_v = W_ls_e.rearrange("(u p e) k -> p u e k", u=2, e=2)
+        wd_v = W_in_d.rearrange("(i p) k -> p i k", p=P)
+        out_v = out.rearrange("(p j) n -> p j n", j=8)
+
+        nc.sync.dma_start(out=h_sb[:, 0:4, :], in_=h_v[:, 0:4, :])
+        nc.sync.dma_start(out=wls_sb[:, 0], in_=wls_v[:, 0])
+        nc.sync.dma_start(out=wmu_sb[:, 0], in_=wmu_v[:, 0])
+        nc.sync.dma_start(out=braw[0:2, :].bitcast(BF16), in_=b_mu_e.rearrange("(u w) -> u w", u=2))
+        nc.sync.dma_start(out=braw[2:4, :].bitcast(BF16), in_=b_ls_e.rearrange("(u w) -> u w", u=2))
+        nc.sync.dma_start(out=eps_sb[:, 0:4, :], in_=eps_v[:, 0:4, :])
+        nc.sync.dma_start(out=wls_sb[:, 1], in_=wls_v[:, 1])
+        nc.sync.dma_start(out=wmu_sb[:, 1], in_=wmu_v[:, 1])
+        for q in range(4):
+            nc.sync.dma_start(out=wd_sb[:, 4 * q:4 * q + 4, :], in_=wd_v[:, 4 * q:4 * q + 4, :])
+        nc.sync.dma_start(out=bd_sb[:], in_=b_in_d.partition_broadcast(P))
+        nc.sync.dma_start(out=h_sb[:, 4:8, :], in_=h_v[:, 4:8, :])
+        nc.sync.dma_start(out=eps_sb[:, 4:8, :], in_=eps_v[:, 4:8, :])
+
+        def exit_bank(bank_view):
+            grouped = work.tile([P, 1024], BF16, align_bytes=64, bufs=4)
+            gv = grouped[:].bitcast(F32).rearrange("p (a r u) -> p a r u", a=2, u=2)
+            nc.scalar.copy(out=gv, in_=bank_view)
+            return grouped
+
+        def prep_bias():
+            bt = psum.tile([P, 4, P], F32, tag="tr", bufs=2)
+            nc.tensor.transpose(bt[:, 0, :], braw[:], ident[:])
+            bview = bt[:, 0, :].bitcast(BF16)
+            nc.vector.tensor_copy(out=bmu[:], in_=bview[:, 0:4])
+            nc.vector.tensor_scalar(out=hbls[:], in0=bview[:, 4:8], scalar1=0.5, scalar2=0.0,
+                                    op0=ALU.mult, op1=ALU.add)
+
+        def prep_h(j):
+            bank = psum.tile([P, 4, P], F32, tag="tr", bufs=2)
+            words = h_sb[:, j, :].bitcast(F32)
+            for a in range(4):
+                nc.tensor.transpose(bank[:, a, :], words[:, P * a:P * a + P], ident[:])
+            grouped = exit_bank(bank[:].rearrange("p (g u) r -> p g r u", u=2))
+            for g in range(2):
+                cols = slice(P * j, P * j + P)
+                nc.vector.quantize_mx(out=h_codes[:, g, cols].bitcast(FP8X4), scales=h_scales[:, g, cols],
+                                      in_=grouped[:, 512 * g:512 * g + 512])
+
+        def prep_w(m, t):
+            bank = psum.tile([P, 4, P], F32, tag="tr", bufs=2)
+            words = w_sb[m][:, t // 2, t % 2, :].bitcast(F32)
+            for a in range(4):
+                nc.tensor.transpose(bank[:, a, :], words[:, P * a:P * a + P], ident[:])
+            grouped = exit_bank(bank[:].rearrange("p (g u) r -> p g r u", u=2))
+            nc.vector.quantize_mx(out=w_codes[m][:, t, :].bitcast(FP8X4), scales=w_scales[m][:, t, :],
+                                  in_=grouped[:])
+
+        def prep_d(ip):
+            bank = psum.tile([P, 4, P], F32, tag="tr", bufs=2)
+            for i2 in range(2):
+                words = wd_sb[:, 2 * ip + i2, :].bitcast(F32)
+                for u in range(2):
+                    nc.tensor.transpose(bank[:, 2 * i2 + u, :], words[:, P * u:P * u + P], ident[:])
+            grouped = exit_bank(bank[:].rearrange("p (i u) r -> p i r u", u=2))
+            cols = slice(256 * ip, 256 * ip + 256)
+            nc.vector.quantize_mx(out=d_codes[:, cols].bitcast(FP8X4), scales=d_scales[:, cols], in_=grouped[:])
+
+        zplanes = {}
+
+        def stage1(hh, u):
+            if u == 0:
+                zp_new = work.tile([P, 4, 512], BF16, name="zp", bufs=2)
+                zplanes[hh] = zp_new
+            zp = zplanes[hh]
+            epsT = psum.tile([P, 512], F32, tag="eps", bufs=2)
+            for jl in range(4):
+                nc.tensor.transpose(epsT[:, P * jl:P * jl + P],
+                                    eps_sb[:, 4 * hh + jl, :].bitcast(F32)[:, P * u:P * u + P], ident[:])
+            cols = slice(512 * hh, 512 * hh + 512)
+            acc = {}
+            for m in ("ls", "mu"):
+                for e in range(2):
+                    t = 2 * u + e
+                    bank = psum.tile([P, 512], F32, tag="acc", bufs=4, name="acc_" + m)
+                    acc[(m, e)] = bank
+                    for g in range(2):
+                        nc.tensor.matmul_mx(
+                            out=bank[:],
+                            lhsT=w_codes[m][:, t, P * g:P * g + P].bitcast(FP8X4),
+                            lhsT_scale=w_scales[m][:, t, P * g:P * g + P],
+                            rhs=h_codes[:, g, cols].bitcast(FP8X4),
+                            rhs_scale=h_scales[:, g, cols],
+                            start=(g == 0), stop=(g == 1))
+            sd = work.tile([P, 2, 512], F32, bufs=2)
+            for e in range(2):
+                t = 2 * u + e
+                nc.scalar.activation(out=sd[:, e, :], in_=acc[("ls", e)][:], func=ACT.Exp,
+                                     bias=hbls[:, t:t + 1], scale=0.5)
+            noise = work.tile([P, 2, 512], F32, bufs=2)
+            nc.vector.tensor_tensor(out=noise[:], in0=sd[:],
+                                    in1=epsT[:].bitcast(BF16).rearrange("p (b e) -> p e b", e=2), op=ALU.mult)
+            for e in range(2):
+                t = 2 * u + e
+                nc.vector.scalar_tensor_tensor(out=zp[:, t, :], in0=acc[("mu", e)][:], scalar=bmu[:, t:t + 1],
+                                               in1=noise[:, e, :], op0=ALU.add, op1=ALU.add)
+
+        def quant_z(hh):
+            zp = zplanes[hh]
+            zg = work.tile([P, 512, 4], BF16, align_bytes=64, bufs=2)
+            nc.vector.tensor_copy(out=zg[:].rearrange("p (c i) t -> p c t i", i=4),
+                                  in_=zp[:].rearrange("p t (c i) -> p c t i", i=4))
+            cols = slice(512 * hh, 512 * hh + 512)
+            nc.vector.quantize_mx(out=z_codes[:, cols].bitcast(FP8X4), scales=z_scales[:, cols],
+                                  in_=zg[:].rearrange("p b t -> p (b t)"))
+
+        def stage2(j):
+            res = work.tile([P, 2048], F32, bufs=3)
+            for c in range(4):
+                cols = slice(512 * c, 512 * c + 512)
+                bank = psum.tile([P, 512], F32, tag="acc", bufs=4, name="acc_o")
+                nc.tensor.matmul_mx(
+                    out=bank[:],
+                    lhsT=z_codes[:, P * j:P * j + P].bitcast(FP8X4),
+                    lhsT_scale=z_scales[:, P * j:P * j + P],
+                    rhs=d_codes[:, cols].bitcast(FP8X4),
+                    rhs_scale=d_scales[:, cols],
+                    start=True, stop=True)
+                pre = work.tile([P, 512], F32, bufs=4)
+                nc.vector.tensor_tensor(out=pre[:], in0=bank[:], in1=bd_sb[:, cols], op=ALU.add)
+                nc.scalar.activation(out=res[:, cols], in_=pre[:], func=ACT.Tanh)
+                if c % 2 == 1:
+                    half = slice(512 * (c - 1), 512 * (c + 1))
+                    nc.sync.dma_start(out=out_v[:, j, half], in_=res[:, half])
+
+        for j in range(4):
+            prep_h(j)
+        for t in range(2):
+            prep_w("ls", t)
+        for t in range(2):
+            prep_w("mu", t)
+        prep_bias()
+        stage1(0, 0)
+        for t in range(2, 4):
+            prep_w("ls", t)
+        for t in range(2, 4):
+            prep_w("mu", t)
+        stage1(0, 1)
+        quant_z(0)
+        for ip in range(8):
+            prep_d(ip)
+        stage2(0)
+        prep_h(4)
+        prep_h(5)
+        stage2(1)
+        prep_h(6)
+        prep_h(7)
+        stage1(1, 0)
+        stage2(2)
+        stage1(1, 1)
+        stage2(3)
+        quant_z(1)
+        for j in range(4, 8):
+            stage2(j)

@@ -15,6 +15,239 @@ ALU = mybir.AluOpType
 
 P = 128
 
+PROGRAM = [
+    ("ident",),
+    ("load", "h_sb", 0, 524288),
+    ("T", "h", 0),
+    ("load", "braw", "", 1024),
+    ("bias",),
+    ("load", "h_sb", 1, 524288),
+    ("T", "h", 1),
+    ("load", "w_sbls", 0, 524288),
+    ("T", "h", 2),
+    ("T", "h", 3),
+    ("load", "w_sbmu", 0, 524288),
+    ("T", "ls", 0),
+    ("load", "w_sbls", 1, 524288),
+    ("X", "h", 2, "V"),
+    ("Q", "h", 2),
+    ("T", "ls", 1),
+    ("X", "h", 1, "V"),
+    ("T", "mu", 0),
+    ("load", "eps_sb", 0, 524288),
+    ("T", "mu", 1),
+    ("X", "h", 0, "S"),
+    ("X", "h", 3, "S"),
+    ("X", "ls", 0, "S"),
+    ("load", "w_sbmu", 1, 524288),
+    ("Q", "h", 3),
+    ("Q", "h", 0),
+    ("load", "h_sb", 3, 524288),
+    ("Q", "ls", 0),
+    ("T", "ls", 2),
+    ("X", "ls", 1, "S"),
+    ("load", "wd_sb", 1, 524288),
+    ("load", "wd_sb", 0, 524288),
+    ("load", "h_sb", 2, 524288),
+    ("Q", "h", 1),
+    ("T", "ls", 3),
+    ("Q", "ls", 1),
+    ("mm1", "ls", 0, 0),
+    ("X", "mu", 0, "V"),
+    ("X", "ls", 3, "V"),
+    ("te", 0, 1),
+    ("te", 0, 0),
+    ("T", "mu", 3),
+    ("X", "mu", 1, "S"),
+    ("T", "mu", 2),
+    ("Q", "ls", 3),
+    ("X", "ls", 2, "S"),
+    ("Q", "mu", 1),
+    ("Q", "ls", 2),
+    ("exp", 0, 0),
+    ("Q", "mu", 0),
+    ("mm1", "ls", 0, 1),
+    ("X", "mu", 3, "S"),
+    ("mm1", "mu", 0, 0),
+    ("T", "d", 3),
+    ("mul", 0, 0, "V", 1),
+    ("X", "mu", 2, "S"),
+    ("exp", 0, 1),
+    ("Q", "mu", 2),
+    ("Q", "mu", 3),
+    ("mm1", "mu", 0, 1),
+    ("zadd", 0, 0),
+    ("T", "h", 6),
+    ("T", "d", 2),
+    ("mul", 0, 1, "V", 1),
+    ("load", "wd_sb", 2, 524288),
+    ("T", "d", 4),
+    ("T", "d", 1),
+    ("zadd", 0, 1),
+    ("X", "d", 3, "S"),
+    ("Q", "d", 3),
+    ("T", "h", 7),
+    ("X", "d", 2, "S"),
+    ("T", "d", 0),
+    ("X", "h", 6, "S"),
+    ("rg", 0, "V"),
+    ("Q", "h", 6),
+    ("T", "h", 4),
+    ("Q", "d", 2),
+    ("load", "wd_sb", 3, 524288),
+    ("qz", 0),
+    ("X", "d", 1, "S"),
+    ("T", "d", 5),
+    ("T", "d", 6),
+    ("T", "h", 5),
+    ("X", "d", 0, "S"),
+    ("Q", "d", 1),
+    ("mm2", 0, 1),
+    ("X", "h", 7, "S"),
+    ("X", "h", 4, "S"),
+    ("Q", "h", 7),
+    ("Q", "d", 0),
+    ("X", "d", 5, "S"),
+    ("mm2", 1, 1),
+    ("mm2", 2, 1),
+    ("load", "bd", "", 524288),
+    ("mm2", 2, 0),
+    ("mm2", 3, 0),
+    ("Q", "h", 4),
+    ("add", 0, 1),
+    ("add", 2, 1),
+    ("mm2", 0, 0),
+    ("T", "d", 7),
+    ("load", "eps_sb", 1, 524288),
+    ("Q", "d", 5),
+    ("X", "d", 4, "S"),
+    ("X", "h", 5, "S"),
+    ("add", 0, 0),
+    ("Q", "h", 5),
+    ("Q", "d", 4),
+    ("X", "d", 6, "S"),
+    ("add", 3, 0),
+    ("X", "d", 7, "S"),
+    ("te", 1, 0),
+    ("mm1", "ls", 1, 0),
+    ("exp", 1, 0),
+    ("mm1", "ls", 1, 1),
+    ("Q", "d", 6),
+    ("mm1", "mu", 1, 0),
+    ("Q", "d", 7),
+    ("add", 2, 0),
+    ("mm2", 1, 0),
+    ("tanh", 0, 0),
+    ("add", 1, 1),
+    ("tanh", 0, 1),
+    ("mm2", 2, 2),
+    ("mm2", 1, 2),
+    ("mul", 1, 0, "V", 1),
+    ("zadd", 1, 0),
+    ("add", 1, 0),
+    ("mm2", 0, 2),
+    ("add", 1, 2),
+    ("mm2", 1, 3),
+    ("exp", 1, 1),
+    ("add", 1, 3),
+    ("add", 2, 2),
+    ("mm2", 0, 3),
+    ("add", 0, 2),
+    ("tanh", 2, 0),
+    ("tanh", 3, 0),
+    ("tanh", 1, 0),
+    ("te", 1, 1),
+    ("tanh", 2, 1),
+    ("mm2", 3, 1),
+    ("tanh", 1, 1),
+    ("mm2", 2, 3),
+    ("mm2", 3, 2),
+    ("add", 0, 3),
+    ("add", 3, 1),
+    ("tanh", 0, 2),
+    ("tanh", 0, 3),
+    ("st", 0, 1),
+    ("mm2", 3, 3),
+    ("mul", 1, 1, "V", 1),
+    ("mm1", "mu", 1, 1),
+    ("zadd", 1, 1),
+    ("st", 1, 1),
+    ("rg", 1, "V"),
+    ("qz", 1),
+    ("mm2", 7, 0),
+    ("tanh", 2, 2),
+    ("mm2", 4, 1),
+    ("tanh", 1, 2),
+    ("mm2", 4, 0),
+    ("mm2", 5, 1),
+    ("add", 2, 3),
+    ("add", 3, 2),
+    ("mm2", 5, 0),
+    ("mm2", 6, 3),
+    ("mm2", 4, 2),
+    ("st", 0, 3),
+    ("add", 3, 3),
+    ("tanh", 3, 1),
+    ("tanh", 1, 3),
+    ("mm2", 5, 2),
+    ("mm2", 4, 3),
+    ("st", 2, 1),
+    ("add", 4, 0),
+    ("st", 1, 3),
+    ("tanh", 2, 3),
+    ("add", 4, 1),
+    ("mm2", 5, 3),
+    ("add", 4, 2),
+    ("tanh", 3, 2),
+    ("add", 4, 3),
+    ("add", 5, 0),
+    ("mm2", 6, 0),
+    ("st", 3, 1),
+    ("tanh", 3, 3),
+    ("tanh", 4, 0),
+    ("tanh", 4, 1),
+    ("add", 5, 1),
+    ("add", 5, 2),
+    ("tanh", 4, 2),
+    ("mm2", 7, 1),
+    ("add", 5, 3),
+    ("tanh", 4, 3),
+    ("st", 2, 3),
+    ("mm2", 7, 2),
+    ("add", 6, 0),
+    ("mm2", 6, 2),
+    ("st", 3, 3),
+    ("st", 4, 1),
+    ("tanh", 5, 0),
+    ("mm2", 6, 1),
+    ("st", 4, 3),
+    ("tanh", 5, 1),
+    ("tanh", 5, 2),
+    ("add", 6, 1),
+    ("mm2", 7, 3),
+    ("add", 6, 2),
+    ("tanh", 5, 3),
+    ("tanh", 6, 0),
+    ("tanh", 6, 1),
+    ("add", 6, 3),
+    ("tanh", 6, 2),
+    ("add", 7, 0),
+    ("tanh", 6, 3),
+    ("st", 5, 1),
+    ("st", 5, 3),
+    ("tanh", 7, 0),
+    ("add", 7, 1),
+    ("tanh", 7, 1),
+    ("st", 6, 1),
+    ("add", 7, 2),
+    ("tanh", 7, 2),
+    ("add", 7, 3),
+    ("tanh", 7, 3),
+    ("st", 6, 3),
+    ("st", 7, 1),
+    ("st", 7, 3),
+]
+
 
 def tile_vae_pa_kernel(tc, h, W_mu_e, b_mu_e, W_ls_e, b_ls_e, eps_z, W_in_d, b_in_d, out):
     nc = tc.nc
@@ -22,6 +255,7 @@ def tile_vae_pa_kernel(tc, h, W_mu_e, b_mu_e, W_ls_e, b_ls_e, eps_z, W_in_d, b_i
         keep = ctx.enter_context(tc.tile_pool(name="keep", bufs=1))
         work = ctx.enter_context(tc.tile_pool(name="work", bufs=2))
         psum = ctx.enter_context(tc.psum_pool(name="psum", bufs=2))
+        ctx.enter_context(tc.manual_schedule())
 
         h_sb = keep.tile([P, 8, 1024], BF16)
         wmu_sb = keep.tile([P, 2, 2, 1024], BF16)
@@ -49,167 +283,183 @@ def tile_vae_pa_kernel(tc, h, W_mu_e, b_mu_e, W_ls_e, b_ls_e, eps_z, W_in_d, b_i
         w_codes = {"mu": wmu_codes, "ls": wls_codes}
         w_scales = {"mu": wmu_scales, "ls": wls_scales}
 
-        nc.vector.memset(braw[:], 0.0)
-        make_identity(nc, ident[:])
-
         h_v = h.rearrange("(p j) k -> p j k", j=8)
         eps_v = eps_z.rearrange("(p j) z -> p j z", j=8)
-        wmu_v = W_mu_e.rearrange("(u p e) k -> p u e k", u=2, e=2)
-        wls_v = W_ls_e.rearrange("(u p e) k -> p u e k", u=2, e=2)
+        w_v = {"mu": W_mu_e.rearrange("(u p e) k -> p u e k", u=2, e=2),
+               "ls": W_ls_e.rearrange("(u p e) k -> p u e k", u=2, e=2)}
         wd_v = W_in_d.rearrange("(i p) k -> p i k", p=P)
         out_v = out.rearrange("(p j) n -> p j n", j=8)
 
-        nc.sync.dma_start(out=h_sb[:, 0:4, :], in_=h_v[:, 0:4, :])
-        nc.sync.dma_start(out=wls_sb[:, 0], in_=wls_v[:, 0])
-        nc.sync.dma_start(out=wmu_sb[:, 0], in_=wmu_v[:, 0])
-        nc.sync.dma_start(out=braw[0:2, :].bitcast(BF16), in_=b_mu_e.rearrange("(u w) -> u w", u=2))
-        nc.sync.dma_start(out=braw[2:4, :].bitcast(BF16), in_=b_ls_e.rearrange("(u w) -> u w", u=2))
-        nc.sync.dma_start(out=eps_sb[:, 0:4, :], in_=eps_v[:, 0:4, :])
-        nc.sync.dma_start(out=wls_sb[:, 1], in_=wls_v[:, 1])
-        nc.sync.dma_start(out=wmu_sb[:, 1], in_=wmu_v[:, 1])
-        for q in range(4):
-            nc.sync.dma_start(out=wd_sb[:, 4 * q:4 * q + 4, :], in_=wd_v[:, 4 * q:4 * q + 4, :])
-        nc.sync.dma_start(out=bd_sb[:], in_=b_in_d.partition_broadcast(P))
-        nc.sync.dma_start(out=h_sb[:, 4:8, :], in_=h_v[:, 4:8, :])
-        nc.sync.dma_start(out=eps_sb[:, 4:8, :], in_=eps_v[:, 4:8, :])
+        st = {}
 
-        def exit_bank(bank_view):
-            grouped = work.tile([P, 1024], BF16, align_bytes=64, bufs=4)
-            gv = grouped[:].bitcast(F32).rearrange("p (a r u) -> p a r u", a=2, u=2)
-            nc.scalar.copy(out=gv, in_=bank_view)
-            return grouped
+        def op_ident():
+            nc.vector.memset(braw[:], 0.0)
+            make_identity(nc, ident[:])
 
-        def prep_bias():
-            bt = psum.tile([P, 4, P], F32, tag="tr", bufs=2)
+        def op_load(name, part, nbytes):
+            if name == "h_sb":
+                nc.sync.dma_start(out=h_sb[:, 2 * part:2 * part + 2, :], in_=h_v[:, 2 * part:2 * part + 2, :])
+            elif name == "w_sbls":
+                nc.sync.dma_start(out=wls_sb[:, part], in_=w_v["ls"][:, part])
+            elif name == "w_sbmu":
+                nc.sync.dma_start(out=wmu_sb[:, part], in_=w_v["mu"][:, part])
+            elif name == "braw":
+                nc.sync.dma_start(out=braw[0:2, :].bitcast(BF16), in_=b_mu_e.rearrange("(u w) -> u w", u=2))
+                nc.sync.dma_start(out=braw[2:4, :].bitcast(BF16), in_=b_ls_e.rearrange("(u w) -> u w", u=2))
+            elif name == "eps_sb":
+                nc.sync.dma_start(out=eps_sb[:, 4 * part:4 * part + 4, :], in_=eps_v[:, 4 * part:4 * part + 4, :])
+            elif name == "wd_sb":
+                nc.sync.dma_start(out=wd_sb[:, 4 * part:4 * part + 4, :], in_=wd_v[:, 4 * part:4 * part + 4, :])
+            else:
+                nc.sync.dma_start(out=bd_sb[:], in_=b_in_d.partition_broadcast(P))
+
+        def op_bias():
+            bt = psum.tile([P, 4, P], F32, tag="acc", bufs=6)
             nc.tensor.transpose(bt[:, 0, :], braw[:], ident[:])
             bview = bt[:, 0, :].bitcast(BF16)
             nc.vector.tensor_copy(out=bmu[:], in_=bview[:, 0:4])
             nc.vector.tensor_scalar(out=hbls[:], in0=bview[:, 4:8], scalar1=0.5, scalar2=0.0,
                                     op0=ALU.mult, op1=ALU.add)
 
-        def prep_h(j):
-            bank = psum.tile([P, 4, P], F32, tag="tr", bufs=2)
-            words = h_sb[:, j, :].bitcast(F32)
+        def op_T(k, i):
+            bank = psum.tile([P, 4, P], F32, tag="acc", bufs=6)
+            st[("b", k, i)] = bank
             for a in range(4):
-                nc.tensor.transpose(bank[:, a, :], words[:, P * a:P * a + P], ident[:])
-            grouped = exit_bank(bank[:].rearrange("p (g u) r -> p g r u", u=2))
-            for g in range(2):
-                cols = slice(P * j, P * j + P)
-                nc.vector.quantize_mx(out=h_codes[:, g, cols].bitcast(FP8X4), scales=h_scales[:, g, cols],
-                                      in_=grouped[:, 512 * g:512 * g + 512])
+                if k == "h":
+                    words = h_sb[:, i, :].bitcast(F32)[:, P * a:P * a + P]
+                elif k == "d":
+                    words = wd_sb[:, 2 * i + a // 2, :].bitcast(F32)[:, P * (a % 2):P * (a % 2) + P]
+                else:
+                    words = w_sb[k][:, i // 2, i % 2, :].bitcast(F32)[:, P * a:P * a + P]
+                nc.tensor.transpose(bank[:, a, :], words, ident[:])
 
-        def prep_w(m, t):
-            bank = psum.tile([P, 4, P], F32, tag="tr", bufs=2)
-            words = w_sb[m][:, t // 2, t % 2, :].bitcast(F32)
-            for a in range(4):
-                nc.tensor.transpose(bank[:, a, :], words[:, P * a:P * a + P], ident[:])
-            grouped = exit_bank(bank[:].rearrange("p (g u) r -> p g r u", u=2))
-            nc.vector.quantize_mx(out=w_codes[m][:, t, :].bitcast(FP8X4), scales=w_scales[m][:, t, :],
-                                  in_=grouped[:])
+        def op_X(k, i, eng):
+            grouped = work.tile([P, 1024], BF16, align_bytes=64, bufs=6)
+            st[("g", k, i)] = grouped
+            gv = grouped[:].bitcast(F32).rearrange("p (a r u) -> p a r u", a=2, u=2)
+            src = st[("b", k, i)][:].rearrange("p (a u) r -> p a r u", u=2)
+            if eng == "S":
+                nc.scalar.copy(out=gv, in_=src)
+            else:
+                nc.vector.tensor_copy(out=gv, in_=src)
 
-        def prep_d(ip):
-            bank = psum.tile([P, 4, P], F32, tag="tr", bufs=2)
-            for i2 in range(2):
-                words = wd_sb[:, 2 * ip + i2, :].bitcast(F32)
-                for u in range(2):
-                    nc.tensor.transpose(bank[:, 2 * i2 + u, :], words[:, P * u:P * u + P], ident[:])
-            grouped = exit_bank(bank[:].rearrange("p (i u) r -> p i r u", u=2))
-            cols = slice(256 * ip, 256 * ip + 256)
-            nc.vector.quantize_mx(out=d_codes[:, cols].bitcast(FP8X4), scales=d_scales[:, cols], in_=grouped[:])
+        def op_Q(k, i):
+            grouped = st[("g", k, i)]
+            if k == "h":
+                cols = slice(P * i, P * i + P)
+                for g in range(2):
+                    nc.vector.quantize_mx(out=h_codes[:, g, cols].bitcast(FP8X4), scales=h_scales[:, g, cols],
+                                          in_=grouped[:, 512 * g:512 * g + 512])
+            elif k == "d":
+                cols = slice(256 * i, 256 * i + 256)
+                nc.vector.quantize_mx(out=d_codes[:, cols].bitcast(FP8X4), scales=d_scales[:, cols], in_=grouped[:])
+            else:
+                nc.vector.quantize_mx(out=w_codes[k][:, i, :].bitcast(FP8X4), scales=w_scales[k][:, i, :],
+                                      in_=grouped[:])
 
-        zplanes = {}
-
-        def stage1(hh, u):
-            if u == 0:
-                zp_new = work.tile([P, 4, 512], BF16, name="zp", bufs=2)
-                zplanes[hh] = zp_new
-            zp = zplanes[hh]
+        def op_te(hh, u):
             epsT = psum.tile([P, 512], F32, tag="eps", bufs=2)
+            st[("eps", hh, u)] = epsT
             for jl in range(4):
                 nc.tensor.transpose(epsT[:, P * jl:P * jl + P],
                                     eps_sb[:, 4 * hh + jl, :].bitcast(F32)[:, P * u:P * u + P], ident[:])
-            cols = slice(512 * hh, 512 * hh + 512)
-            acc = {}
-            for m in ("ls", "mu"):
-                for e in range(2):
-                    t = 2 * u + e
-                    bank = psum.tile([P, 512], F32, tag="acc", bufs=4, name="acc_" + m)
-                    acc[(m, e)] = bank
-                    for g in range(2):
-                        nc.tensor.matmul_mx(
-                            out=bank[:],
-                            lhsT=w_codes[m][:, t, P * g:P * g + P].bitcast(FP8X4),
-                            lhsT_scale=w_scales[m][:, t, P * g:P * g + P],
-                            rhs=h_codes[:, g, cols].bitcast(FP8X4),
-                            rhs_scale=h_scales[:, g, cols],
-                            start=(g == 0), stop=(g == 1))
-            sd = work.tile([P, 2, 512], F32, bufs=2)
-            for e in range(2):
-                t = 2 * u + e
-                nc.scalar.activation(out=sd[:, e, :], in_=acc[("ls", e)][:], func=ACT.Exp,
-                                     bias=hbls[:, t:t + 1], scale=0.5)
-            noise = work.tile([P, 2, 512], F32, bufs=2)
-            nc.vector.tensor_tensor(out=noise[:], in0=sd[:],
-                                    in1=epsT[:].bitcast(BF16).rearrange("p (b e) -> p e b", e=2), op=ALU.mult)
-            for e in range(2):
-                t = 2 * u + e
-                nc.vector.scalar_tensor_tensor(out=zp[:, t, :], in0=acc[("mu", e)][:], scalar=bmu[:, t:t + 1],
-                                               in1=noise[:, e, :], op0=ALU.add, op1=ALU.add)
 
-        def quant_z(hh):
-            zp = zplanes[hh]
+        def op_teX(hh, u):
+            epsS = work.tile([P, 512], F32, bufs=2)
+            nc.scalar.copy(out=epsS[:], in_=st[("eps", hh, u)][:])
+            st[("eps", hh, u)] = epsS
+
+        def op_mm1(m, hh, u):
+            cols = slice(512 * hh, 512 * hh + 512)
+            for e in range(2):
+                t = 2 * u + e
+                bank = psum.tile([P, 512], F32, tag="acc", bufs=6, name="acc_" + m)
+                st[(m, hh, t)] = bank
+                for g in range(2):
+                    nc.tensor.matmul_mx(
+                        out=bank[:],
+                        lhsT=w_codes[m][:, t, P * g:P * g + P].bitcast(FP8X4),
+                        lhsT_scale=w_scales[m][:, t, P * g:P * g + P],
+                        rhs=h_codes[:, g, cols].bitcast(FP8X4),
+                        rhs_scale=h_scales[:, g, cols],
+                        start=(g == 0), stop=(g == 1))
+
+        def op_exp(hh, u):
+            sd = work.tile([P, 2, 512], F32, bufs=2)
+            st[("sd", hh, u)] = sd
+            for e in range(2):
+                t = 2 * u + e
+                nc.scalar.activation(out=sd[:, e, :], in_=st[("ls", hh, t)][:], func=ACT.Exp,
+                                     bias=hbls[:, t:t + 1], scale=0.5)
+
+        def op_mul(hh, u, eng, pieces):
+            noise = work.tile([P, 2, 512], F32, bufs=2)
+            st[("n", hh, u)] = noise
+            sd = st[("sd", hh, u)]
+            ev = st[("eps", hh, u)][:].bitcast(BF16).rearrange("p (b e) -> p e b", e=2)
+            if eng == "G":
+                for e in range(2):
+                    nc.gpsimd.tensor_tensor(out=noise[:, e, :], in0=sd[:, e, :], in1=ev[:, e, :], op=ALU.mult)
+            else:
+                nc.vector.tensor_tensor(out=noise[:], in0=sd[:], in1=ev, op=ALU.mult)
+
+        def op_zadd(hh, u):
+            if u == 0:
+                zp_new = work.tile([P, 4, 512], BF16, name="zp", bufs=2)
+                st[("zp", hh)] = zp_new
+            zp = st[("zp", hh)]
+            for e in range(2):
+                t = 2 * u + e
+                nc.vector.scalar_tensor_tensor(out=zp[:, t, :], in0=st[("mu", hh, t)][:], scalar=bmu[:, t:t + 1],
+                                               in1=st[("n", hh, u)][:, e, :], op0=ALU.add, op1=ALU.add)
+
+        def op_rg(hh, eng):
+            zp = st[("zp", hh)]
             zg = work.tile([P, 512, 4], BF16, align_bytes=64, bufs=2)
-            nc.vector.tensor_copy(out=zg[:].rearrange("p (c i) t -> p c t i", i=4),
-                                  in_=zp[:].rearrange("p t (c i) -> p c t i", i=4))
+            st[("zg", hh)] = zg
+            dst = zg[:].rearrange("p (c i) t -> p c t i", i=4)
+            src = zp[:].rearrange("p t (c i) -> p c t i", i=4)
+            if eng == "G":
+                nc.gpsimd.tensor_scalar(out=dst, in0=src, scalar1=1.0, scalar2=0.0, op0=ALU.mult, op1=ALU.add)
+            elif eng == "S":
+                nc.scalar.copy(out=dst, in_=src)
+            else:
+                nc.vector.tensor_copy(out=dst, in_=src)
+
+        def op_qz(hh):
             cols = slice(512 * hh, 512 * hh + 512)
             nc.vector.quantize_mx(out=z_codes[:, cols].bitcast(FP8X4), scales=z_scales[:, cols],
-                                  in_=zg[:].rearrange("p b t -> p (b t)"))
+                                  in_=st[("zg", hh)][:].rearrange("p b t -> p (b t)"))
 
-        def stage2(j):
-            res = work.tile([P, 2048], F32, bufs=3)
-            for c in range(4):
-                cols = slice(512 * c, 512 * c + 512)
-                bank = psum.tile([P, 512], F32, tag="acc", bufs=4, name="acc_o")
-                nc.tensor.matmul_mx(
-                    out=bank[:],
-                    lhsT=z_codes[:, P * j:P * j + P].bitcast(FP8X4),
-                    lhsT_scale=z_scales[:, P * j:P * j + P],
-                    rhs=d_codes[:, cols].bitcast(FP8X4),
-                    rhs_scale=d_scales[:, cols],
-                    start=True, stop=True)
-                pre = work.tile([P, 512], F32, bufs=4)
-                nc.vector.tensor_tensor(out=pre[:], in0=bank[:], in1=bd_sb[:, cols], op=ALU.add)
-                nc.scalar.activation(out=res[:, cols], in_=pre[:], func=ACT.Tanh)
-                if c % 2 == 1:
-                    half = slice(512 * (c - 1), 512 * (c + 1))
-                    nc.sync.dma_start(out=out_v[:, j, half], in_=res[:, half])
+        def op_mm2(j, c):
+            cols = slice(512 * c, 512 * c + 512)
+            bank = psum.tile([P, 512], F32, tag="acc", bufs=6, name="acc_o")
+            st[("o", j, c)] = bank
+            nc.tensor.matmul_mx(
+                out=bank[:],
+                lhsT=z_codes[:, P * j:P * j + P].bitcast(FP8X4),
+                lhsT_scale=z_scales[:, P * j:P * j + P],
+                rhs=d_codes[:, cols].bitcast(FP8X4),
+                rhs_scale=d_scales[:, cols],
+                start=True, stop=True)
 
-        for j in range(4):
-            prep_h(j)
-        for t in range(2):
-            prep_w("ls", t)
-        for t in range(2):
-            prep_w("mu", t)
-        prep_bias()
-        stage1(0, 0)
-        for t in range(2, 4):
-            prep_w("ls", t)
-        for t in range(2, 4):
-            prep_w("mu", t)
-        stage1(0, 1)
-        quant_z(0)
-        for ip in range(8):
-            prep_d(ip)
-        stage2(0)
-        prep_h(4)
-        prep_h(5)
-        stage2(1)
-        prep_h(6)
-        prep_h(7)
-        stage1(1, 0)
-        stage2(2)
-        stage1(1, 1)
-        stage2(3)
-        quant_z(1)
-        for j in range(4, 8):
-            stage2(j)
+        def op_add(j, c):
+            pre = work.tile([P, 512], F32, bufs=4)
+            st[("p", j, c)] = pre
+            nc.vector.tensor_tensor(out=pre[:], in0=st[("o", j, c)][:], in1=bd_sb[:, 512 * c:512 * c + 512], op=ALU.add)
+
+        def op_tanh(j, c):
+            if c % 2 == 0:
+                res_new = work.tile([P, 1024], F32, name="res", bufs=4)
+                st[("r", j, c // 2)] = res_new
+            res = st[("r", j, c // 2)]
+            nc.scalar.activation(out=res[:, 512 * (c % 2):512 * (c % 2) + 512], in_=st[("p", j, c)][:], func=ACT.Tanh)
+
+        def op_st(j, c):
+            nc.sync.dma_start(out=out_v[:, j, 512 * (c - 1):512 * (c + 1)], in_=st[("r", j, c // 2)][:])
+
+        ops = {"ident": op_ident, "load": op_load, "bias": op_bias, "T": op_T, "X": op_X, "Q": op_Q, "te": op_te,
+               "teX": op_teX, "mm1": op_mm1, "exp": op_exp, "mul": op_mul, "zadd": op_zadd, "rg": op_rg, "qz": op_qz,
+               "mm2": op_mm2, "add": op_add, "tanh": op_tanh, "st": op_st}
+        for op in PROGRAM:
+            ops[op[0]](*op[1:])

@@ -18,233 +18,233 @@ P = 128
 PROGRAM = [
     ("ident",),
     ("load", "h_sb", 0, 524288),
-    ("T", "h", 0),
-    ("load", "braw", "", 1024),
-    ("bias",),
     ("load", "h_sb", 1, 524288),
+    ("T", "h", 0),
     ("T", "h", 1),
-    ("load", "w_sbls", 0, 524288),
     ("T", "h", 2),
     ("T", "h", 3),
-    ("load", "w_sbmu", 0, 524288),
+    ("load", "braw", "", 1024),
+    ("load", "w_sbls", 0, 524288),
     ("T", "ls", 0),
-    ("load", "w_sbls", 1, 524288),
-    ("X", "h", 2, "V"),
-    ("Q", "h", 2),
+    ("load", "w_sbmu", 0, 524288),
     ("T", "ls", 1),
-    ("X", "h", 1, "V"),
-    ("T", "mu", 0),
-    ("load", "eps_sb", 0, 524288),
-    ("T", "mu", 1),
+    ("load", "w_sbls", 1, 524288),
     ("X", "h", 0, "S"),
-    ("X", "h", 3, "S"),
-    ("X", "ls", 0, "S"),
-    ("load", "w_sbmu", 1, 524288),
-    ("Q", "h", 3),
+    ("T", "mu", 0),
+    ("X", "h", 1, "S"),
     ("Q", "h", 0),
-    ("load", "h_sb", 3, 524288),
-    ("Q", "ls", 0),
-    ("T", "ls", 2),
-    ("X", "ls", 1, "S"),
-    ("load", "wd_sb", 1, 524288),
-    ("load", "wd_sb", 0, 524288),
-    ("load", "h_sb", 2, 524288),
     ("Q", "h", 1),
+    ("T", "mu", 1),
+    ("X", "h", 3, "S"),
     ("T", "ls", 3),
-    ("Q", "ls", 1),
-    ("mm1", "ls", 0, 0),
-    ("X", "mu", 0, "V"),
-    ("X", "ls", 3, "V"),
-    ("te", 0, 1),
-    ("te", 0, 0),
+    ("load", "w_sbmu", 1, 524288),
+    ("load", "wd_sb", 1, 524288),
+    ("T", "ls", 2),
+    ("X", "h", 2, "V"),
+    ("X", "ls", 0, "V"),
+    ("X", "ls", 1, "S"),
+    ("Q", "h", 2),
+    ("load", "eps_sb", 0, 524288),
+    ("load", "wd_sb", 3, 524288),
     ("T", "mu", 3),
-    ("X", "mu", 1, "S"),
+    ("Q", "ls", 1),
     ("T", "mu", 2),
-    ("Q", "ls", 3),
+    ("Q", "h", 3),
+    ("Q", "ls", 0),
+    ("load", "eps_sb", 1, 524288),
+    ("bias",),
+    ("X", "mu", 1, "S"),
+    ("T", "d", 2),
+    ("X", "mu", 0, "S"),
     ("X", "ls", 2, "S"),
-    ("Q", "mu", 1),
+    ("X", "ls", 3, "S"),
     ("Q", "ls", 2),
-    ("exp", 0, 0),
+    ("mm1", "ls", 0, 0),
+    ("Q", "ls", 3),
+    ("Q", "mu", 1),
+    ("load", "wd_sb", 0, 524288),
+    ("te", 0, 0),
     ("Q", "mu", 0),
-    ("mm1", "ls", 0, 1),
     ("X", "mu", 3, "S"),
+    ("X", "mu", 2, "S"),
+    ("mm1", "ls", 0, 1),
     ("mm1", "mu", 0, 0),
+    ("Q", "mu", 2),
+    ("te", 0, 1),
+    ("Q", "mu", 3),
+    ("X", "d", 2, "V"),
+    ("exp", 0, 0),
+    ("Q", "d", 2),
+    ("load", "h_sb", 3, 524288),
     ("T", "d", 3),
     ("mul", 0, 0, "V", 1),
-    ("X", "mu", 2, "S"),
-    ("exp", 0, 1),
-    ("Q", "mu", 2),
-    ("Q", "mu", 3),
     ("mm1", "mu", 0, 1),
-    ("zadd", 0, 0),
+    ("T", "d", 0),
     ("T", "h", 6),
-    ("T", "d", 2),
+    ("T", "d", 1),
+    ("zadd", 0, 0),
+    ("T", "d", 7),
+    ("T", "h", 7),
+    ("load", "h_sb", 2, 524288),
+    ("exp", 0, 1),
+    ("X", "d", 3, "S"),
     ("mul", 0, 1, "V", 1),
     ("load", "wd_sb", 2, 524288),
-    ("T", "d", 4),
-    ("T", "d", 1),
     ("zadd", 0, 1),
-    ("X", "d", 3, "S"),
     ("Q", "d", 3),
-    ("T", "h", 7),
-    ("X", "d", 2, "S"),
-    ("T", "d", 0),
-    ("X", "h", 6, "S"),
-    ("rg", 0, "V"),
-    ("Q", "h", 6),
     ("T", "h", 4),
-    ("Q", "d", 2),
-    ("load", "wd_sb", 3, 524288),
+    ("rg", 0, "V"),
+    ("T", "d", 4),
+    ("X", "d", 0, "S"),
     ("qz", 0),
+    ("X", "h", 6, "S"),
+    ("T", "h", 5),
+    ("mm2", 1, 1),
     ("X", "d", 1, "S"),
+    ("Q", "d", 0),
+    ("X", "d", 7, "S"),
+    ("Q", "d", 1),
+    ("X", "h", 7, "S"),
+    ("Q", "h", 6),
+    ("mm2", 3, 1),
+    ("mm2", 2, 0),
+    ("mm2", 1, 0),
+    ("Q", "d", 7),
+    ("Q", "h", 7),
+    ("load", "bd", "", 524288),
+    ("X", "h", 4, "S"),
+    ("mm2", 3, 0),
     ("T", "d", 5),
     ("T", "d", 6),
-    ("T", "h", 5),
-    ("X", "d", 0, "S"),
-    ("Q", "d", 1),
-    ("mm2", 0, 1),
-    ("X", "h", 7, "S"),
-    ("X", "h", 4, "S"),
-    ("Q", "h", 7),
-    ("Q", "d", 0),
-    ("X", "d", 5, "S"),
-    ("mm2", 1, 1),
-    ("mm2", 2, 1),
-    ("load", "bd", "", 524288),
-    ("mm2", 2, 0),
-    ("mm2", 3, 0),
     ("Q", "h", 4),
-    ("add", 0, 1),
-    ("add", 2, 1),
-    ("mm2", 0, 0),
-    ("T", "d", 7),
-    ("load", "eps_sb", 1, 524288),
-    ("Q", "d", 5),
-    ("X", "d", 4, "S"),
-    ("X", "h", 5, "S"),
-    ("add", 0, 0),
-    ("Q", "h", 5),
-    ("Q", "d", 4),
-    ("X", "d", 6, "S"),
-    ("add", 3, 0),
-    ("X", "d", 7, "S"),
-    ("te", 1, 0),
-    ("mm1", "ls", 1, 0),
-    ("exp", 1, 0),
-    ("mm1", "ls", 1, 1),
-    ("Q", "d", 6),
-    ("mm1", "mu", 1, 0),
-    ("Q", "d", 7),
-    ("add", 2, 0),
-    ("mm2", 1, 0),
-    ("tanh", 0, 0),
     ("add", 1, 1),
-    ("tanh", 0, 1),
-    ("mm2", 2, 2),
-    ("mm2", 1, 2),
-    ("mul", 1, 0, "V", 1),
-    ("zadd", 1, 0),
-    ("add", 1, 0),
-    ("mm2", 0, 2),
-    ("add", 1, 2),
-    ("mm2", 1, 3),
-    ("exp", 1, 1),
-    ("add", 1, 3),
-    ("add", 2, 2),
-    ("mm2", 0, 3),
-    ("add", 0, 2),
-    ("tanh", 2, 0),
-    ("tanh", 3, 0),
-    ("tanh", 1, 0),
-    ("te", 1, 1),
-    ("tanh", 2, 1),
-    ("mm2", 3, 1),
-    ("tanh", 1, 1),
-    ("mm2", 2, 3),
-    ("mm2", 3, 2),
-    ("add", 0, 3),
+    ("mm2", 0, 0),
+    ("add", 2, 0),
+    ("mm2", 0, 1),
+    ("X", "h", 5, "S"),
+    ("X", "d", 5, "S"),
+    ("Q", "h", 5),
     ("add", 3, 1),
-    ("tanh", 0, 2),
-    ("tanh", 0, 3),
-    ("st", 0, 1),
-    ("mm2", 3, 3),
-    ("mul", 1, 1, "V", 1),
+    ("mm2", 2, 1),
+    ("mm1", "ls", 1, 0),
+    ("te", 1, 0),
+    ("X", "d", 6, "S"),
+    ("mm1", "ls", 1, 1),
+    ("add", 3, 0),
+    ("add", 0, 0),
+    ("add", 0, 1),
+    ("mm1", "mu", 1, 0),
+    ("te", 1, 1),
+    ("X", "d", 4, "S"),
+    ("add", 2, 1),
+    ("tanh", 3, 0),
+    ("exp", 1, 0),
+    ("Q", "d", 5),
+    ("Q", "d", 4),
     ("mm1", "mu", 1, 1),
+    ("tanh", 0, 0),
+    ("Q", "d", 6),
+    ("exp", 1, 1),
+    ("add", 1, 0),
+    ("mm2", 0, 3),
+    ("mul", 1, 0, "V", 1),
+    ("tanh", 0, 1),
+    ("zadd", 1, 0),
+    ("mul", 1, 1, "V", 1),
+    ("mm2", 1, 2),
     ("zadd", 1, 1),
-    ("st", 1, 1),
+    ("mm2", 2, 3),
+    ("mm2", 2, 2),
+    ("mm2", 0, 2),
+    ("mm2", 1, 3),
+    ("st", 0, 1),
     ("rg", 1, "V"),
+    ("tanh", 2, 0),
     ("qz", 1),
-    ("mm2", 7, 0),
-    ("tanh", 2, 2),
-    ("mm2", 4, 1),
-    ("tanh", 1, 2),
-    ("mm2", 4, 0),
-    ("mm2", 5, 1),
-    ("add", 2, 3),
-    ("add", 3, 2),
-    ("mm2", 5, 0),
-    ("mm2", 6, 3),
-    ("mm2", 4, 2),
-    ("st", 0, 3),
-    ("add", 3, 3),
-    ("tanh", 3, 1),
-    ("tanh", 1, 3),
-    ("mm2", 5, 2),
-    ("mm2", 4, 3),
-    ("st", 2, 1),
-    ("add", 4, 0),
-    ("st", 1, 3),
-    ("tanh", 2, 3),
-    ("add", 4, 1),
+    ("tanh", 1, 0),
+    ("add", 0, 2),
+    ("mm2", 3, 3),
     ("mm2", 5, 3),
+    ("tanh", 1, 1),
+    ("mm2", 5, 2),
+    ("mm2", 3, 2),
+    ("tanh", 3, 1),
+    ("add", 2, 2),
+    ("mm2", 4, 2),
+    ("add", 1, 2),
+    ("tanh", 2, 1),
+    ("tanh", 0, 2),
+    ("mm2", 5, 1),
+    ("add", 0, 3),
+    ("mm2", 4, 0),
+    ("tanh", 2, 2),
+    ("tanh", 1, 2),
+    ("add", 2, 3),
+    ("st", 1, 1),
     ("add", 4, 2),
-    ("tanh", 3, 2),
-    ("add", 4, 3),
-    ("add", 5, 0),
-    ("mm2", 6, 0),
-    ("st", 3, 1),
-    ("tanh", 3, 3),
-    ("tanh", 4, 0),
-    ("tanh", 4, 1),
-    ("add", 5, 1),
-    ("add", 5, 2),
+    ("tanh", 0, 3),
+    ("add", 1, 3),
+    ("mm2", 4, 3),
+    ("mm2", 4, 1),
+    ("tanh", 2, 3),
+    ("add", 3, 2),
     ("tanh", 4, 2),
-    ("mm2", 7, 1),
-    ("add", 5, 3),
-    ("tanh", 4, 3),
-    ("st", 2, 3),
-    ("mm2", 7, 2),
-    ("add", 6, 0),
-    ("mm2", 6, 2),
-    ("st", 3, 3),
-    ("st", 4, 1),
-    ("tanh", 5, 0),
+    ("tanh", 1, 3),
+    ("tanh", 3, 2),
+    ("add", 4, 0),
+    ("st", 3, 1),
+    ("tanh", 4, 0),
+    ("st", 2, 1),
+    ("add", 4, 1),
+    ("add", 3, 3),
+    ("add", 4, 3),
+    ("tanh", 4, 1),
+    ("st", 0, 3),
+    ("mm2", 7, 0),
+    ("mm2", 5, 0),
     ("mm2", 6, 1),
-    ("st", 4, 3),
-    ("tanh", 5, 1),
+    ("st", 2, 3),
+    ("add", 5, 2),
+    ("tanh", 3, 3),
+    ("mm2", 6, 0),
+    ("mm2", 6, 2),
+    ("tanh", 4, 3),
+    ("mm2", 6, 3),
+    ("st", 1, 3),
+    ("add", 5, 3),
     ("tanh", 5, 2),
-    ("add", 6, 1),
-    ("mm2", 7, 3),
-    ("add", 6, 2),
     ("tanh", 5, 3),
+    ("add", 5, 0),
+    ("mm2", 7, 1),
+    ("add", 5, 1),
+    ("add", 6, 0),
+    ("st", 4, 1),
+    ("st", 3, 3),
+    ("tanh", 5, 0),
+    ("tanh", 5, 1),
+    ("mm2", 7, 3),
+    ("add", 6, 1),
     ("tanh", 6, 0),
     ("tanh", 6, 1),
-    ("add", 6, 3),
+    ("add", 6, 2),
     ("tanh", 6, 2),
-    ("add", 7, 0),
+    ("mm2", 7, 2),
+    ("add", 6, 3),
     ("tanh", 6, 3),
-    ("st", 5, 1),
+    ("st", 4, 3),
     ("st", 5, 3),
-    ("tanh", 7, 0),
-    ("add", 7, 1),
-    ("tanh", 7, 1),
+    ("st", 5, 1),
+    ("add", 7, 0),
     ("st", 6, 1),
+    ("add", 7, 1),
+    ("tanh", 7, 0),
     ("add", 7, 2),
-    ("tanh", 7, 2),
-    ("add", 7, 3),
-    ("tanh", 7, 3),
+    ("tanh", 7, 1),
     ("st", 6, 3),
+    ("add", 7, 3),
     ("st", 7, 1),
+    ("tanh", 7, 2),
+    ("tanh", 7, 3),
     ("st", 7, 3),
 ]
 
@@ -255,7 +255,6 @@ def tile_vae_pa_kernel(tc, h, W_mu_e, b_mu_e, W_ls_e, b_ls_e, eps_z, W_in_d, b_i
         keep = ctx.enter_context(tc.tile_pool(name="keep", bufs=1))
         work = ctx.enter_context(tc.tile_pool(name="work", bufs=2))
         psum = ctx.enter_context(tc.psum_pool(name="psum", bufs=2))
-        ctx.enter_context(tc.manual_schedule())
 
         h_sb = keep.tile([P, 8, 1024], BF16)
         wmu_sb = keep.tile([P, 2, 2, 1024], BF16)
@@ -385,7 +384,7 @@ def tile_vae_pa_kernel(tc, h, W_mu_e, b_mu_e, W_ls_e, b_ls_e, eps_z, W_in_d, b_i
                         start=(g == 0), stop=(g == 1))
 
         def op_exp(hh, u):
-            sd = work.tile([P, 2, 512], F32, bufs=2)
+            sd = work.tile([P, 2, 512], F32, bufs=3)
             st[("sd", hh, u)] = sd
             for e in range(2):
                 t = 2 * u + e
@@ -393,7 +392,7 @@ def tile_vae_pa_kernel(tc, h, W_mu_e, b_mu_e, W_ls_e, b_ls_e, eps_z, W_in_d, b_i
                                      bias=hbls[:, t:t + 1], scale=0.5)
 
         def op_mul(hh, u, eng, pieces):
-            noise = work.tile([P, 2, 512], F32, bufs=2)
+            noise = work.tile([P, 2, 512], F32, bufs=3)
             st[("n", hh, u)] = noise
             sd = st[("sd", hh, u)]
             ev = st[("eps", hh, u)][:].bitcast(BF16).rearrange("p (b e) -> p e b", e=2)
@@ -444,13 +443,13 @@ def tile_vae_pa_kernel(tc, h, W_mu_e, b_mu_e, W_ls_e, b_ls_e, eps_z, W_in_d, b_i
                 start=True, stop=True)
 
         def op_add(j, c):
-            pre = work.tile([P, 512], F32, bufs=4)
+            pre = work.tile([P, 512], F32, bufs=6)
             st[("p", j, c)] = pre
             nc.vector.tensor_tensor(out=pre[:], in0=st[("o", j, c)][:], in1=bd_sb[:, 512 * c:512 * c + 512], op=ALU.add)
 
         def op_tanh(j, c):
             if c % 2 == 0:
-                res_new = work.tile([P, 1024], F32, name="res", bufs=4)
+                res_new = work.tile([P, 1024], F32, name="res", bufs=6)
                 st[("r", j, c // 2)] = res_new
             res = st[("r", j, c // 2)]
             nc.scalar.activation(out=res[:, 512 * (c % 2):512 * (c % 2) + 512], in_=st[("p", j, c)][:], func=ACT.Tanh)

@@ -14,239 +14,12 @@ ACT = mybir.ActivationFunctionType
 ALU = mybir.AluOpType
 
 P = 128
-
-PROGRAM = [
-    ("ident",),
-    ("load", "h_sb", 0, 524288),
-    ("load", "h_sb", 1, 524288),
-    ("T", "h", 0),
-    ("T", "h", 1),
-    ("T", "h", 2),
-    ("T", "h", 3),
-    ("load", "braw", "", 1024),
-    ("load", "w_sbls", 0, 524288),
-    ("T", "ls", 0),
-    ("load", "w_sbmu", 0, 524288),
-    ("T", "ls", 1),
-    ("load", "w_sbls", 1, 524288),
-    ("X", "h", 0, "S"),
-    ("T", "mu", 0),
-    ("X", "h", 1, "S"),
-    ("Q", "h", 0),
-    ("Q", "h", 1),
-    ("T", "mu", 1),
-    ("X", "h", 3, "S"),
-    ("T", "ls", 3),
-    ("load", "w_sbmu", 1, 524288),
-    ("load", "wd_sb", 1, 524288),
-    ("T", "ls", 2),
-    ("X", "h", 2, "V"),
-    ("X", "ls", 0, "V"),
-    ("X", "ls", 1, "S"),
-    ("Q", "h", 2),
-    ("load", "eps_sb", 0, 524288),
-    ("load", "wd_sb", 3, 524288),
-    ("T", "mu", 3),
-    ("Q", "ls", 1),
-    ("T", "mu", 2),
-    ("Q", "h", 3),
-    ("Q", "ls", 0),
-    ("load", "eps_sb", 1, 524288),
-    ("bias",),
-    ("X", "mu", 1, "S"),
-    ("T", "d", 2),
-    ("X", "mu", 0, "S"),
-    ("X", "ls", 2, "S"),
-    ("X", "ls", 3, "S"),
-    ("Q", "ls", 2),
-    ("mm1", "ls", 0, 0),
-    ("Q", "ls", 3),
-    ("Q", "mu", 1),
-    ("load", "wd_sb", 0, 524288),
-    ("te", 0, 0),
-    ("Q", "mu", 0),
-    ("X", "mu", 3, "S"),
-    ("X", "mu", 2, "S"),
-    ("mm1", "ls", 0, 1),
-    ("mm1", "mu", 0, 0),
-    ("Q", "mu", 2),
-    ("te", 0, 1),
-    ("Q", "mu", 3),
-    ("X", "d", 2, "V"),
-    ("exp", 0, 0),
-    ("Q", "d", 2),
-    ("load", "h_sb", 3, 524288),
-    ("T", "d", 3),
-    ("mul", 0, 0, "V", 1),
-    ("mm1", "mu", 0, 1),
-    ("T", "d", 0),
-    ("T", "h", 6),
-    ("T", "d", 1),
-    ("zadd", 0, 0),
-    ("T", "d", 7),
-    ("T", "h", 7),
-    ("load", "h_sb", 2, 524288),
-    ("exp", 0, 1),
-    ("X", "d", 3, "S"),
-    ("mul", 0, 1, "V", 1),
-    ("load", "wd_sb", 2, 524288),
-    ("zadd", 0, 1),
-    ("Q", "d", 3),
-    ("T", "h", 4),
-    ("rg", 0, "V"),
-    ("T", "d", 4),
-    ("X", "d", 0, "S"),
-    ("qz", 0),
-    ("X", "h", 6, "S"),
-    ("T", "h", 5),
-    ("mm2", 1, 1),
-    ("X", "d", 1, "S"),
-    ("Q", "d", 0),
-    ("X", "d", 7, "S"),
-    ("Q", "d", 1),
-    ("X", "h", 7, "S"),
-    ("Q", "h", 6),
-    ("mm2", 3, 1),
-    ("mm2", 2, 0),
-    ("mm2", 1, 0),
-    ("Q", "d", 7),
-    ("Q", "h", 7),
-    ("load", "bd", "", 524288),
-    ("X", "h", 4, "S"),
-    ("mm2", 3, 0),
-    ("T", "d", 5),
-    ("T", "d", 6),
-    ("Q", "h", 4),
-    ("add", 1, 1),
-    ("mm2", 0, 0),
-    ("add", 2, 0),
-    ("mm2", 0, 1),
-    ("X", "h", 5, "S"),
-    ("X", "d", 5, "S"),
-    ("Q", "h", 5),
-    ("add", 3, 1),
-    ("mm2", 2, 1),
-    ("mm1", "ls", 1, 0),
-    ("te", 1, 0),
-    ("X", "d", 6, "S"),
-    ("mm1", "ls", 1, 1),
-    ("add", 3, 0),
-    ("add", 0, 0),
-    ("add", 0, 1),
-    ("mm1", "mu", 1, 0),
-    ("te", 1, 1),
-    ("X", "d", 4, "S"),
-    ("add", 2, 1),
-    ("tanh", 3, 0),
-    ("exp", 1, 0),
-    ("Q", "d", 5),
-    ("Q", "d", 4),
-    ("mm1", "mu", 1, 1),
-    ("tanh", 0, 0),
-    ("Q", "d", 6),
-    ("exp", 1, 1),
-    ("add", 1, 0),
-    ("mm2", 0, 3),
-    ("mul", 1, 0, "V", 1),
-    ("tanh", 0, 1),
-    ("zadd", 1, 0),
-    ("mul", 1, 1, "V", 1),
-    ("mm2", 1, 2),
-    ("zadd", 1, 1),
-    ("mm2", 2, 3),
-    ("mm2", 2, 2),
-    ("mm2", 0, 2),
-    ("mm2", 1, 3),
-    ("st", 0, 1),
-    ("rg", 1, "V"),
-    ("tanh", 2, 0),
-    ("qz", 1),
-    ("tanh", 1, 0),
-    ("add", 0, 2),
-    ("mm2", 3, 3),
-    ("mm2", 5, 3),
-    ("tanh", 1, 1),
-    ("mm2", 5, 2),
-    ("mm2", 3, 2),
-    ("tanh", 3, 1),
-    ("add", 2, 2),
-    ("mm2", 4, 2),
-    ("add", 1, 2),
-    ("tanh", 2, 1),
-    ("tanh", 0, 2),
-    ("mm2", 5, 1),
-    ("add", 0, 3),
-    ("mm2", 4, 0),
-    ("tanh", 2, 2),
-    ("tanh", 1, 2),
-    ("add", 2, 3),
-    ("st", 1, 1),
-    ("add", 4, 2),
-    ("tanh", 0, 3),
-    ("add", 1, 3),
-    ("mm2", 4, 3),
-    ("mm2", 4, 1),
-    ("tanh", 2, 3),
-    ("add", 3, 2),
-    ("tanh", 4, 2),
-    ("tanh", 1, 3),
-    ("tanh", 3, 2),
-    ("add", 4, 0),
-    ("st", 3, 1),
-    ("tanh", 4, 0),
-    ("st", 2, 1),
-    ("add", 4, 1),
-    ("add", 3, 3),
-    ("add", 4, 3),
-    ("tanh", 4, 1),
-    ("st", 0, 3),
-    ("mm2", 7, 0),
-    ("mm2", 5, 0),
-    ("mm2", 6, 1),
-    ("st", 2, 3),
-    ("add", 5, 2),
-    ("tanh", 3, 3),
-    ("mm2", 6, 0),
-    ("mm2", 6, 2),
-    ("tanh", 4, 3),
-    ("mm2", 6, 3),
-    ("st", 1, 3),
-    ("add", 5, 3),
-    ("tanh", 5, 2),
-    ("tanh", 5, 3),
-    ("add", 5, 0),
-    ("mm2", 7, 1),
-    ("add", 5, 1),
-    ("add", 6, 0),
-    ("st", 4, 1),
-    ("st", 3, 3),
-    ("tanh", 5, 0),
-    ("tanh", 5, 1),
-    ("mm2", 7, 3),
-    ("add", 6, 1),
-    ("tanh", 6, 0),
-    ("tanh", 6, 1),
-    ("add", 6, 2),
-    ("tanh", 6, 2),
-    ("mm2", 7, 2),
-    ("add", 6, 3),
-    ("tanh", 6, 3),
-    ("st", 4, 3),
-    ("st", 5, 3),
-    ("st", 5, 1),
-    ("add", 7, 0),
-    ("st", 6, 1),
-    ("add", 7, 1),
-    ("tanh", 7, 0),
-    ("add", 7, 2),
-    ("tanh", 7, 1),
-    ("st", 6, 3),
-    ("add", 7, 3),
-    ("st", 7, 1),
-    ("tanh", 7, 2),
-    ("tanh", 7, 3),
-    ("st", 7, 3),
-]
+BANK = 512
+BATCH_TILES = 8
+HALF_TILES = 4
+Z_TILES = 4
+PASSES_1 = 2
+OUT_CHUNKS = 4
 
 
 def tile_vae_pa_kernel(tc, h, W_mu_e, b_mu_e, W_ls_e, b_ls_e, eps_z, W_in_d, b_in_d, out):
@@ -256,209 +29,189 @@ def tile_vae_pa_kernel(tc, h, W_mu_e, b_mu_e, W_ls_e, b_ls_e, eps_z, W_in_d, b_i
         work = ctx.enter_context(tc.tile_pool(name="work", bufs=2))
         psum = ctx.enter_context(tc.psum_pool(name="psum", bufs=2))
 
-        h_sb = keep.tile([P, 8, 1024], BF16)
-        wmu_sb = keep.tile([P, 2, 2, 1024], BF16)
-        wls_sb = keep.tile([P, 2, 2, 1024], BF16)
-        eps_sb = keep.tile([P, 8, 512], BF16)
+        h_sb = keep.tile([P, BATCH_TILES, 1024], BF16)
+        eps_sb = keep.tile([P, BATCH_TILES, 512], BF16)
+        w_sb = {"mu": keep.tile([P, 2, 2, 1024], BF16, name="wmu_sb"),
+                "ls": keep.tile([P, 2, 2, 1024], BF16, name="wls_sb")}
         wd_sb = keep.tile([P, 16, 512], BF16)
         bd_sb = keep.tile([P, 2048], BF16)
-        braw = keep.tile([P, P], F32)
+        bias_rows = keep.tile([P, P], F32)
         ident = keep.tile([P, P], F32)
-        bmu = keep.tile([P, 4], F32)
-        hbls = keep.tile([P, 4], F32)
+        b_mu = keep.tile([P, Z_TILES], F32)
+        half_b_ls = keep.tile([P, Z_TILES], F32)
 
-        h_codes = keep.tile([P, 2, 1024], U32, align_bytes=64)
-        h_scales = keep.tile([P, 2, 1024], U8, align_bytes=64)
-        wmu_codes = keep.tile([P, 4, 256], U32, align_bytes=64)
-        wmu_scales = keep.tile([P, 4, 256], U8, align_bytes=64)
-        wls_codes = keep.tile([P, 4, 256], U32, align_bytes=64)
-        wls_scales = keep.tile([P, 4, 256], U8, align_bytes=64)
+        h_codes = keep.tile([P, PASSES_1, 1024], U32, align_bytes=64)
+        h_scales = keep.tile([P, PASSES_1, 1024], U8, align_bytes=64)
+        w_codes = {"mu": keep.tile([P, Z_TILES, PASSES_1 * P], U32, align_bytes=64, name="wmu_codes"),
+                   "ls": keep.tile([P, Z_TILES, PASSES_1 * P], U32, align_bytes=64, name="wls_codes")}
+        w_scales = {"mu": keep.tile([P, Z_TILES, PASSES_1 * P], U8, align_bytes=64, name="wmu_scales"),
+                    "ls": keep.tile([P, Z_TILES, PASSES_1 * P], U8, align_bytes=64, name="wls_scales")}
         d_codes = keep.tile([P, 2048], U32, align_bytes=64)
         d_scales = keep.tile([P, 2048], U8, align_bytes=64)
         z_codes = keep.tile([P, 1024], U32, align_bytes=64)
         z_scales = keep.tile([P, 1024], U8, align_bytes=64)
 
-        w_sb = {"mu": wmu_sb, "ls": wls_sb}
-        w_codes = {"mu": wmu_codes, "ls": wls_codes}
-        w_scales = {"mu": wmu_scales, "ls": wls_scales}
+        nc.vector.memset(bias_rows[:], 0.0)
+        make_identity(nc, ident[:])
 
-        h_v = h.rearrange("(p j) k -> p j k", j=8)
-        eps_v = eps_z.rearrange("(p j) z -> p j z", j=8)
+        h_v = h.rearrange("(r j) k -> r j k", j=BATCH_TILES)
+        eps_v = eps_z.rearrange("(r j) z -> r j z", j=BATCH_TILES)
         w_v = {"mu": W_mu_e.rearrange("(u p e) k -> p u e k", u=2, e=2),
                "ls": W_ls_e.rearrange("(u p e) k -> p u e k", u=2, e=2)}
         wd_v = W_in_d.rearrange("(i p) k -> p i k", p=P)
-        out_v = out.rearrange("(p j) n -> p j n", j=8)
+        out_v = out.rearrange("(r j) n -> r j n", j=BATCH_TILES)
 
-        st = {}
+        def load_h(pair):
+            nc.sync.dma_start(out=h_sb[:, 2 * pair:2 * pair + 2, :], in_=h_v[:, 2 * pair:2 * pair + 2, :])
 
-        def op_ident():
-            nc.vector.memset(braw[:], 0.0)
-            make_identity(nc, ident[:])
+        def load_eps(half):
+            tiles = slice(HALF_TILES * half, HALF_TILES * (half + 1))
+            nc.sync.dma_start(out=eps_sb[:, tiles, :], in_=eps_v[:, tiles, :])
 
-        def op_load(name, part, nbytes):
-            if name == "h_sb":
-                nc.sync.dma_start(out=h_sb[:, 2 * part:2 * part + 2, :], in_=h_v[:, 2 * part:2 * part + 2, :])
-            elif name == "w_sbls":
-                nc.sync.dma_start(out=wls_sb[:, part], in_=w_v["ls"][:, part])
-            elif name == "w_sbmu":
-                nc.sync.dma_start(out=wmu_sb[:, part], in_=w_v["mu"][:, part])
-            elif name == "braw":
-                nc.sync.dma_start(out=braw[0:2, :].bitcast(BF16), in_=b_mu_e.rearrange("(u w) -> u w", u=2))
-                nc.sync.dma_start(out=braw[2:4, :].bitcast(BF16), in_=b_ls_e.rearrange("(u w) -> u w", u=2))
-            elif name == "eps_sb":
-                nc.sync.dma_start(out=eps_sb[:, 4 * part:4 * part + 4, :], in_=eps_v[:, 4 * part:4 * part + 4, :])
-            elif name == "wd_sb":
-                nc.sync.dma_start(out=wd_sb[:, 4 * part:4 * part + 4, :], in_=wd_v[:, 4 * part:4 * part + 4, :])
-            else:
-                nc.sync.dma_start(out=bd_sb[:], in_=b_in_d.partition_broadcast(P))
+        def load_w(m, u):
+            nc.sync.dma_start(out=w_sb[m][:, u], in_=w_v[m][:, u])
 
-        def op_bias():
-            bt = psum.tile([P, 4, P], F32, tag="acc", bufs=6)
-            nc.tensor.transpose(bt[:, 0, :], braw[:], ident[:])
-            bview = bt[:, 0, :].bitcast(BF16)
-            nc.vector.tensor_copy(out=bmu[:], in_=bview[:, 0:4])
-            nc.vector.tensor_scalar(out=hbls[:], in0=bview[:, 4:8], scalar1=0.5, scalar2=0.0,
+        def load_wd(quarter):
+            nc.sync.dma_start(out=wd_sb[:, 4 * quarter:4 * quarter + 4, :], in_=wd_v[:, 4 * quarter:4 * quarter + 4, :])
+
+        load_h(0)
+        load_h(1)
+        nc.sync.dma_start(out=bias_rows[0:2, :].bitcast(BF16), in_=b_mu_e.rearrange("(u w) -> u w", u=2))
+        nc.sync.dma_start(out=bias_rows[2:4, :].bitcast(BF16), in_=b_ls_e.rearrange("(u w) -> u w", u=2))
+        load_w("ls", 0)
+        load_w("mu", 0)
+        load_w("ls", 1)
+        load_w("mu", 1)
+        load_eps(0)
+        load_wd(0)
+        load_wd(1)
+        load_h(2)
+        load_h(3)
+        load_eps(1)
+        nc.sync.dma_start(out=bd_sb[:], in_=b_in_d.partition_broadcast(P))
+        load_wd(2)
+        load_wd(3)
+
+        def new_bank(shape):
+            bank = psum.tile(shape, F32, tag="bank", bufs=6)
+            return bank
+
+        def transpose_and_regroup(word_blocks):
+            bank = new_bank([P, 4, P])
+            for n, words in enumerate(word_blocks):
+                nc.tensor.transpose(bank[:, n, :], words, ident[:])
+            grouped = work.tile([P, 2 * BANK], BF16, align_bytes=64, bufs=6)
+            nc.scalar.copy(out=grouped[:].bitcast(F32).rearrange("p (a r u) -> p a r u", a=2, u=2),
+                           in_=bank[:].rearrange("p (a u) r -> p a r u", u=2))
+            return grouped
+
+        def prepare_h(j):
+            words = h_sb[:, j, :].bitcast(F32)
+            grouped = transpose_and_regroup([words[:, P * n:P * (n + 1)] for n in range(4)])
+            rows = slice(P * j, P * (j + 1))
+            for g in range(PASSES_1):
+                nc.vector.quantize_mx(out=h_codes[:, g, rows].bitcast(FP8X4), scales=h_scales[:, g, rows],
+                                      in_=grouped[:, BANK * g:BANK * (g + 1)])
+
+        def prepare_w(m, t):
+            words = w_sb[m][:, t // 2, t % 2, :].bitcast(F32)
+            grouped = transpose_and_regroup([words[:, P * n:P * (n + 1)] for n in range(4)])
+            nc.vector.quantize_mx(out=w_codes[m][:, t, :].bitcast(FP8X4), scales=w_scales[m][:, t, :], in_=grouped[:])
+
+        def prepare_wd(pair):
+            blocks = [wd_sb[:, 2 * pair + n // 2, :].bitcast(F32)[:, P * (n % 2):P * (n % 2 + 1)] for n in range(4)]
+            grouped = transpose_and_regroup(blocks)
+            cols = slice(2 * P * pair, 2 * P * (pair + 1))
+            nc.vector.quantize_mx(out=d_codes[:, cols].bitcast(FP8X4), scales=d_scales[:, cols], in_=grouped[:])
+
+        def prepare_biases():
+            bank = new_bank([P, 4, P])
+            nc.tensor.transpose(bank[:, 0, :], bias_rows[:], ident[:])
+            pairs = bank[:, 0, :].bitcast(BF16)
+            nc.vector.tensor_copy(out=b_mu[:], in_=pairs[:, 0:Z_TILES])
+            nc.vector.tensor_scalar(out=half_b_ls[:], in0=pairs[:, Z_TILES:2 * Z_TILES], scalar1=0.5, scalar2=0.0,
                                     op0=ALU.mult, op1=ALU.add)
 
-        def op_T(k, i):
-            bank = psum.tile([P, 4, P], F32, tag="acc", bufs=6)
-            st[("b", k, i)] = bank
-            for a in range(4):
-                if k == "h":
-                    words = h_sb[:, i, :].bitcast(F32)[:, P * a:P * a + P]
-                elif k == "d":
-                    words = wd_sb[:, 2 * i + a // 2, :].bitcast(F32)[:, P * (a % 2):P * (a % 2) + P]
-                else:
-                    words = w_sb[k][:, i // 2, i % 2, :].bitcast(F32)[:, P * a:P * a + P]
-                nc.tensor.transpose(bank[:, a, :], words, ident[:])
+        def stage1_passes(m, half, t):
+            cols = slice(BANK * half, BANK * (half + 1))
+            acc = new_bank([P, BANK])
+            for g in range(PASSES_1):
+                nc.tensor.matmul_mx(out=acc[:],
+                                    lhsT=w_codes[m][:, t, P * g:P * (g + 1)].bitcast(FP8X4),
+                                    lhsT_scale=w_scales[m][:, t, P * g:P * (g + 1)],
+                                    rhs=h_codes[:, g, cols].bitcast(FP8X4),
+                                    rhs_scale=h_scales[:, g, cols],
+                                    start=(g == 0), stop=(g == PASSES_1 - 1))
+            return acc
 
-        def op_X(k, i, eng):
-            grouped = work.tile([P, 1024], BF16, align_bytes=64, bufs=6)
-            st[("g", k, i)] = grouped
-            gv = grouped[:].bitcast(F32).rearrange("p (a r u) -> p a r u", a=2, u=2)
-            src = st[("b", k, i)][:].rearrange("p (a u) r -> p a r u", u=2)
-            if eng == "S":
-                nc.scalar.copy(out=gv, in_=src)
-            else:
-                nc.vector.tensor_copy(out=gv, in_=src)
-
-        def op_Q(k, i):
-            grouped = st[("g", k, i)]
-            if k == "h":
-                cols = slice(P * i, P * i + P)
-                for g in range(2):
-                    nc.vector.quantize_mx(out=h_codes[:, g, cols].bitcast(FP8X4), scales=h_scales[:, g, cols],
-                                          in_=grouped[:, 512 * g:512 * g + 512])
-            elif k == "d":
-                cols = slice(256 * i, 256 * i + 256)
-                nc.vector.quantize_mx(out=d_codes[:, cols].bitcast(FP8X4), scales=d_scales[:, cols], in_=grouped[:])
-            else:
-                nc.vector.quantize_mx(out=w_codes[k][:, i, :].bitcast(FP8X4), scales=w_scales[k][:, i, :],
-                                      in_=grouped[:])
-
-        def op_te(hh, u):
-            epsT = psum.tile([P, 512], F32, tag="eps", bufs=2)
-            st[("eps", hh, u)] = epsT
-            for jl in range(4):
-                nc.tensor.transpose(epsT[:, P * jl:P * jl + P],
-                                    eps_sb[:, 4 * hh + jl, :].bitcast(F32)[:, P * u:P * u + P], ident[:])
-
-        def op_teX(hh, u):
-            epsS = work.tile([P, 512], F32, bufs=2)
-            nc.scalar.copy(out=epsS[:], in_=st[("eps", hh, u)][:])
-            st[("eps", hh, u)] = epsS
-
-        def op_mm1(m, hh, u):
-            cols = slice(512 * hh, 512 * hh + 512)
-            for e in range(2):
-                t = 2 * u + e
-                bank = psum.tile([P, 512], F32, tag="acc", bufs=6, name="acc_" + m)
-                st[(m, hh, t)] = bank
-                for g in range(2):
-                    nc.tensor.matmul_mx(
-                        out=bank[:],
-                        lhsT=w_codes[m][:, t, P * g:P * g + P].bitcast(FP8X4),
-                        lhsT_scale=w_scales[m][:, t, P * g:P * g + P],
-                        rhs=h_codes[:, g, cols].bitcast(FP8X4),
-                        rhs_scale=h_scales[:, g, cols],
-                        start=(g == 0), stop=(g == 1))
-
-        def op_exp(hh, u):
-            sd = work.tile([P, 2, 512], F32, bufs=3)
-            st[("sd", hh, u)] = sd
-            for e in range(2):
-                t = 2 * u + e
-                nc.scalar.activation(out=sd[:, e, :], in_=st[("ls", hh, t)][:], func=ACT.Exp,
-                                     bias=hbls[:, t:t + 1], scale=0.5)
-
-        def op_mul(hh, u, eng, pieces):
-            noise = work.tile([P, 2, 512], F32, bufs=3)
-            st[("n", hh, u)] = noise
-            sd = st[("sd", hh, u)]
-            ev = st[("eps", hh, u)][:].bitcast(BF16).rearrange("p (b e) -> p e b", e=2)
-            if eng == "G":
+        def stage1(half):
+            eps_t = []
+            for u in range(2):
+                bank = psum.tile([P, BANK], F32, tag="eps", bufs=2)
+                for n in range(HALF_TILES):
+                    nc.tensor.transpose(bank[:, P * n:P * (n + 1)],
+                                        eps_sb[:, HALF_TILES * half + n, :].bitcast(F32)[:, P * u:P * (u + 1)], ident[:])
+                eps_t.append(bank)
+            ls = [stage1_passes("ls", half, t) for t in range(Z_TILES)]
+            sd = []
+            for u in range(2):
+                sd_u = work.tile([P, 2, BANK], F32, name="sd", bufs=3)
                 for e in range(2):
-                    nc.gpsimd.tensor_tensor(out=noise[:, e, :], in0=sd[:, e, :], in1=ev[:, e, :], op=ALU.mult)
-            else:
-                nc.vector.tensor_tensor(out=noise[:], in0=sd[:], in1=ev, op=ALU.mult)
-
-        def op_zadd(hh, u):
-            if u == 0:
-                zp_new = work.tile([P, 4, 512], BF16, name="zp", bufs=2)
-                st[("zp", hh)] = zp_new
-            zp = st[("zp", hh)]
-            for e in range(2):
-                t = 2 * u + e
-                nc.vector.scalar_tensor_tensor(out=zp[:, t, :], in0=st[("mu", hh, t)][:], scalar=bmu[:, t:t + 1],
-                                               in1=st[("n", hh, u)][:, e, :], op0=ALU.add, op1=ALU.add)
-
-        def op_rg(hh, eng):
-            zp = st[("zp", hh)]
-            zg = work.tile([P, 512, 4], BF16, align_bytes=64, bufs=2)
-            st[("zg", hh)] = zg
-            dst = zg[:].rearrange("p (c i) t -> p c t i", i=4)
-            src = zp[:].rearrange("p t (c i) -> p c t i", i=4)
-            if eng == "G":
-                nc.gpsimd.tensor_scalar(out=dst, in0=src, scalar1=1.0, scalar2=0.0, op0=ALU.mult, op1=ALU.add)
-            elif eng == "S":
-                nc.scalar.copy(out=dst, in_=src)
-            else:
-                nc.vector.tensor_copy(out=dst, in_=src)
-
-        def op_qz(hh):
-            cols = slice(512 * hh, 512 * hh + 512)
+                    t = 2 * u + e
+                    nc.scalar.activation(out=sd_u[:, e, :], in_=ls[t][:], func=ACT.Exp,
+                                         bias=half_b_ls[:, t:t + 1], scale=0.5)
+                sd.append(sd_u)
+            mu = [stage1_passes("mu", half, t) for t in range(Z_TILES)]
+            z_planes = work.tile([P, Z_TILES, BANK], BF16, bufs=2)
+            for u in range(2):
+                noise = work.tile([P, 2, BANK], F32, bufs=3)
+                nc.vector.tensor_tensor(out=noise[:], in0=sd[u][:],
+                                        in1=eps_t[u][:].bitcast(BF16).rearrange("p (b e) -> p e b", e=2), op=ALU.mult)
+                for e in range(2):
+                    t = 2 * u + e
+                    nc.vector.scalar_tensor_tensor(out=z_planes[:, t, :], in0=mu[t][:], scalar=b_mu[:, t:t + 1],
+                                                   in1=noise[:, e, :], op0=ALU.add, op1=ALU.add)
+            z_grouped = work.tile([P, BANK, Z_TILES], BF16, align_bytes=64, bufs=2)
+            nc.vector.tensor_copy(out=z_grouped[:].rearrange("p (c i) t -> p c t i", i=4),
+                                  in_=z_planes[:].rearrange("p t (c i) -> p c t i", i=4))
+            cols = slice(BANK * half, BANK * (half + 1))
             nc.vector.quantize_mx(out=z_codes[:, cols].bitcast(FP8X4), scales=z_scales[:, cols],
-                                  in_=st[("zg", hh)][:].rearrange("p b t -> p (b t)"))
+                                  in_=z_grouped[:].rearrange("p b t -> p (b t)"))
 
-        def op_mm2(j, c):
-            cols = slice(512 * c, 512 * c + 512)
-            bank = psum.tile([P, 512], F32, tag="acc", bufs=6, name="acc_o")
-            st[("o", j, c)] = bank
-            nc.tensor.matmul_mx(
-                out=bank[:],
-                lhsT=z_codes[:, P * j:P * j + P].bitcast(FP8X4),
-                lhsT_scale=z_scales[:, P * j:P * j + P],
-                rhs=d_codes[:, cols].bitcast(FP8X4),
-                rhs_scale=d_scales[:, cols],
-                start=True, stop=True)
+        def stage2(j, chunk_pair):
+            result = work.tile([P, 2 * BANK], F32, bufs=6)
+            for n in range(2):
+                cols = slice(BANK * (2 * chunk_pair + n), BANK * (2 * chunk_pair + n + 1))
+                acc = new_bank([P, BANK])
+                nc.tensor.matmul_mx(out=acc[:],
+                                    lhsT=z_codes[:, P * j:P * (j + 1)].bitcast(FP8X4),
+                                    lhsT_scale=z_scales[:, P * j:P * (j + 1)],
+                                    rhs=d_codes[:, cols].bitcast(FP8X4),
+                                    rhs_scale=d_scales[:, cols],
+                                    start=True, stop=True)
+                biased = work.tile([P, BANK], F32, bufs=6)
+                nc.vector.tensor_tensor(out=biased[:], in0=acc[:], in1=bd_sb[:, cols], op=ALU.add)
+                nc.scalar.activation(out=result[:, BANK * n:BANK * (n + 1)], in_=biased[:], func=ACT.Tanh)
+            nc.sync.dma_start(out=out_v[:, j, 2 * BANK * chunk_pair:2 * BANK * (chunk_pair + 1)], in_=result[:])
 
-        def op_add(j, c):
-            pre = work.tile([P, 512], F32, bufs=6)
-            st[("p", j, c)] = pre
-            nc.vector.tensor_tensor(out=pre[:], in0=st[("o", j, c)][:], in1=bd_sb[:, 512 * c:512 * c + 512], op=ALU.add)
-
-        def op_tanh(j, c):
-            if c % 2 == 0:
-                res_new = work.tile([P, 1024], F32, name="res", bufs=6)
-                st[("r", j, c // 2)] = res_new
-            res = st[("r", j, c // 2)]
-            nc.scalar.activation(out=res[:, 512 * (c % 2):512 * (c % 2) + 512], in_=st[("p", j, c)][:], func=ACT.Tanh)
-
-        def op_st(j, c):
-            nc.sync.dma_start(out=out_v[:, j, 512 * (c - 1):512 * (c + 1)], in_=st[("r", j, c // 2)][:])
-
-        ops = {"ident": op_ident, "load": op_load, "bias": op_bias, "T": op_T, "X": op_X, "Q": op_Q, "te": op_te,
-               "teX": op_teX, "mm1": op_mm1, "exp": op_exp, "mul": op_mul, "zadd": op_zadd, "rg": op_rg, "qz": op_qz,
-               "mm2": op_mm2, "add": op_add, "tanh": op_tanh, "st": op_st}
-        for op in PROGRAM:
-            ops[op[0]](*op[1:])
+        for j in range(HALF_TILES):
+            prepare_h(j)
+        for u in range(2):
+            for m in ("ls", "mu"):
+                for e in range(2):
+                    prepare_w(m, 2 * u + e)
+        prepare_biases()
+        stage1(0)
+        for pair in range(4):
+            prepare_wd(pair)
+        for j in range(HALF_TILES, BATCH_TILES):
+            prepare_h(j)
+        for pair in range(4, 8):
+            prepare_wd(pair)
+        stage1(1)
+        for chunk_pair in range(OUT_CHUNKS // 2):
+            for j in range(HALF_TILES):
+                stage2(j, chunk_pair)
+        for j in range(HALF_TILES, BATCH_TILES):
+            for chunk_pair in range(OUT_CHUNKS // 2):
+                stage2(j, chunk_pair)

@@ -28,6 +28,7 @@ def tile_vae_pa_kernel(tc, h, W_mu_e, b_mu_e, W_ls_e, b_ls_e, eps_z, W_in_d, b_i
         keep = ctx.enter_context(tc.tile_pool(name="keep", bufs=1))
         work = ctx.enter_context(tc.tile_pool(name="work", bufs=2))
         psum = ctx.enter_context(tc.psum_pool(name="psum", bufs=2))
+        ctx.enter_context(tc.manual_schedule())
 
         h_sb = keep.tile([P, BATCH_TILES, 1024], BF16)
         eps_sb = keep.tile([P, BATCH_TILES, 512], BF16)

@@ -14,12 +14,240 @@ ACT = mybir.ActivationFunctionType
 ALU = mybir.AluOpType
 
 P = 128
-BANK = 512
-BATCH_TILES = 8
-HALF_TILES = 4
-Z_TILES = 4
-PASSES_1 = 2
-OUT_CHUNKS = 4
+TAPER = ()
+
+PROGRAM = [
+    ("ident",),
+    ("load", "h_sb", 0, 524288),
+    ("load", "h_sb", 1, 524288),
+    ("load", "braw", "", 1024),
+    ("load", "w_sbls", 0, 524288),
+    ("load", "w_sbmu", 0, 524288),
+    ("load", "w_sbls", 1, 524288),
+    ("load", "w_sbmu", 1, 524288),
+    ("load", "eps_sb", 0, 524288),
+    ("load", "wd_sb", 0, 524288),
+    ("load", "wd_sb", 1, 524288),
+    ("load", "h_sb", 2, 524288),
+    ("load", "h_sb", 3, 524288),
+    ("load", "eps_sb", 1, 524288),
+    ("load", "bd", "", 524288),
+    ("load", "wd_sb", 2, 524288),
+    ("load", "wd_sb", 3, 524288),
+    ("T", "h", 0),
+    ("X", "h", 0, "S"),
+    ("Q", "h", 0),
+    ("T", "h", 1),
+    ("X", "h", 1, "S"),
+    ("Q", "h", 1),
+    ("T", "h", 2),
+    ("X", "h", 2, "S"),
+    ("Q", "h", 2),
+    ("T", "h", 3),
+    ("X", "h", 3, "S"),
+    ("Q", "h", 3),
+    ("T", "ls", 0),
+    ("X", "ls", 0, "S"),
+    ("Q", "ls", 0),
+    ("T", "ls", 1),
+    ("X", "ls", 1, "S"),
+    ("Q", "ls", 1),
+    ("T", "mu", 0),
+    ("X", "mu", 0, "S"),
+    ("Q", "mu", 0),
+    ("T", "mu", 1),
+    ("X", "mu", 1, "S"),
+    ("Q", "mu", 1),
+    ("T", "ls", 2),
+    ("X", "ls", 2, "S"),
+    ("Q", "ls", 2),
+    ("T", "ls", 3),
+    ("X", "ls", 3, "S"),
+    ("Q", "ls", 3),
+    ("T", "mu", 2),
+    ("X", "mu", 2, "S"),
+    ("Q", "mu", 2),
+    ("T", "mu", 3),
+    ("X", "mu", 3, "S"),
+    ("Q", "mu", 3),
+    ("bias",),
+    ("te", 0, 0),
+    ("te", 0, 1),
+    ("mm1", "ls", 0, 0),
+    ("mm1", "ls", 0, 1),
+    ("exp", 0, 0),
+    ("exp", 0, 1),
+    ("mm1", "mu", 0, 0),
+    ("mm1", "mu", 0, 1),
+    ("mul", 0, 0, "V", 1),
+    ("zadd", 0, 0),
+    ("mul", 0, 1, "V", 1),
+    ("zadd", 0, 1),
+    ("rg", 0, "V"),
+    ("qz", 0),
+    ("T", "d", 0),
+    ("X", "d", 0, "S"),
+    ("Q", "d", 0),
+    ("T", "d", 1),
+    ("X", "d", 1, "S"),
+    ("Q", "d", 1),
+    ("T", "d", 2),
+    ("X", "d", 2, "S"),
+    ("Q", "d", 2),
+    ("T", "d", 3),
+    ("X", "d", 3, "S"),
+    ("Q", "d", 3),
+    ("T", "h", 4),
+    ("X", "h", 4, "S"),
+    ("Q", "h", 4),
+    ("T", "h", 5),
+    ("X", "h", 5, "S"),
+    ("Q", "h", 5),
+    ("mm2", 0, 0),
+    ("add", 0, 0),
+    ("tanh", 0, 0),
+    ("mm2", 0, 1),
+    ("add", 0, 1),
+    ("tanh", 0, 1),
+    ("st", 0, 1),
+    ("T", "h", 6),
+    ("X", "h", 6, "S"),
+    ("Q", "h", 6),
+    ("T", "h", 7),
+    ("X", "h", 7, "S"),
+    ("Q", "h", 7),
+    ("mm2", 1, 0),
+    ("add", 1, 0),
+    ("tanh", 1, 0),
+    ("mm2", 1, 1),
+    ("add", 1, 1),
+    ("tanh", 1, 1),
+    ("st", 1, 1),
+    ("te", 1, 0),
+    ("te", 1, 1),
+    ("mm1", "ls", 1, 0),
+    ("mm1", "ls", 1, 1),
+    ("mm2", 2, 0),
+    ("add", 2, 0),
+    ("tanh", 2, 0),
+    ("mm2", 2, 1),
+    ("add", 2, 1),
+    ("tanh", 2, 1),
+    ("st", 2, 1),
+    ("exp", 1, 0),
+    ("exp", 1, 1),
+    ("mm1", "mu", 1, 0),
+    ("mm1", "mu", 1, 1),
+    ("mm2", 3, 0),
+    ("add", 3, 0),
+    ("tanh", 3, 0),
+    ("mm2", 3, 1),
+    ("add", 3, 1),
+    ("tanh", 3, 1),
+    ("st", 3, 1),
+    ("T", "d", 4),
+    ("X", "d", 4, "S"),
+    ("Q", "d", 4),
+    ("T", "d", 5),
+    ("X", "d", 5, "S"),
+    ("Q", "d", 5),
+    ("mul", 1, 0, "V", 1),
+    ("zadd", 1, 0),
+    ("T", "d", 6),
+    ("X", "d", 6, "S"),
+    ("Q", "d", 6),
+    ("T", "d", 7),
+    ("X", "d", 7, "S"),
+    ("Q", "d", 7),
+    ("mul", 1, 1, "V", 1),
+    ("zadd", 1, 1),
+    ("mm2", 0, 2),
+    ("add", 0, 2),
+    ("tanh", 0, 2),
+    ("mm2", 0, 3),
+    ("add", 0, 3),
+    ("tanh", 0, 3),
+    ("st", 0, 3),
+    ("rg", 1, "V"),
+    ("qz", 1),
+    ("mm2", 1, 2),
+    ("add", 1, 2),
+    ("tanh", 1, 2),
+    ("mm2", 1, 3),
+    ("add", 1, 3),
+    ("tanh", 1, 3),
+    ("st", 1, 3),
+    ("mm2", 2, 2),
+    ("add", 2, 2),
+    ("tanh", 2, 2),
+    ("mm2", 2, 3),
+    ("add", 2, 3),
+    ("tanh", 2, 3),
+    ("st", 2, 3),
+    ("mm2", 3, 2),
+    ("add", 3, 2),
+    ("tanh", 3, 2),
+    ("mm2", 3, 3),
+    ("add", 3, 3),
+    ("tanh", 3, 3),
+    ("st", 3, 3),
+    ("mm2", 4, 0),
+    ("add", 4, 0),
+    ("tanh", 4, 0),
+    ("mm2", 4, 1),
+    ("add", 4, 1),
+    ("tanh", 4, 1),
+    ("st", 4, 1),
+    ("mm2", 4, 2),
+    ("add", 4, 2),
+    ("tanh", 4, 2),
+    ("mm2", 4, 3),
+    ("add", 4, 3),
+    ("tanh", 4, 3),
+    ("st", 4, 3),
+    ("mm2", 5, 0),
+    ("add", 5, 0),
+    ("tanh", 5, 0),
+    ("mm2", 5, 1),
+    ("add", 5, 1),
+    ("tanh", 5, 1),
+    ("st", 5, 1),
+    ("mm2", 5, 2),
+    ("add", 5, 2),
+    ("tanh", 5, 2),
+    ("mm2", 5, 3),
+    ("add", 5, 3),
+    ("tanh", 5, 3),
+    ("st", 5, 3),
+    ("mm2", 6, 0),
+    ("add", 6, 0),
+    ("tanh", 6, 0),
+    ("mm2", 6, 1),
+    ("add", 6, 1),
+    ("tanh", 6, 1),
+    ("st", 6, 1),
+    ("mm2", 6, 2),
+    ("add", 6, 2),
+    ("tanh", 6, 2),
+    ("mm2", 6, 3),
+    ("add", 6, 3),
+    ("tanh", 6, 3),
+    ("st", 6, 3),
+    ("mm2", 7, 0),
+    ("add", 7, 0),
+    ("tanh", 7, 0),
+    ("mm2", 7, 1),
+    ("add", 7, 1),
+    ("tanh", 7, 1),
+    ("st", 7, 1),
+    ("mm2", 7, 2),
+    ("add", 7, 2),
+    ("tanh", 7, 2),
+    ("mm2", 7, 3),
+    ("add", 7, 3),
+    ("tanh", 7, 3),
+    ("st", 7, 3),
+]
 
 
 def tile_vae_pa_kernel(tc, h, W_mu_e, b_mu_e, W_ls_e, b_ls_e, eps_z, W_in_d, b_in_d, out):
@@ -28,191 +256,218 @@ def tile_vae_pa_kernel(tc, h, W_mu_e, b_mu_e, W_ls_e, b_ls_e, eps_z, W_in_d, b_i
         keep = ctx.enter_context(tc.tile_pool(name="keep", bufs=1))
         work = ctx.enter_context(tc.tile_pool(name="work", bufs=2))
         psum = ctx.enter_context(tc.psum_pool(name="psum", bufs=2))
-        ctx.enter_context(tc.manual_schedule())
 
-        h_sb = keep.tile([P, BATCH_TILES, 1024], BF16)
-        eps_sb = keep.tile([P, BATCH_TILES, 512], BF16)
-        w_sb = {"mu": keep.tile([P, 2, 2, 1024], BF16, name="wmu_sb"),
-                "ls": keep.tile([P, 2, 2, 1024], BF16, name="wls_sb")}
+        h_sb = keep.tile([P, 8, 1024], BF16)
+        wmu_sb = keep.tile([P, 2, 2, 1024], BF16)
+        wls_sb = keep.tile([P, 2, 2, 1024], BF16)
+        eps_sb = keep.tile([P, 8, 512], BF16)
         wd_sb = keep.tile([P, 16, 512], BF16)
         bd_sb = keep.tile([P, 2048], BF16)
-        bias_rows = keep.tile([P, P], F32)
+        braw = keep.tile([P, P], F32)
         ident = keep.tile([P, P], F32)
-        b_mu = keep.tile([P, Z_TILES], F32)
-        half_b_ls = keep.tile([P, Z_TILES], F32)
+        bmu = keep.tile([P, 4], F32)
+        hbls = keep.tile([P, 4], F32)
 
-        h_codes = keep.tile([P, PASSES_1, 1024], U32, align_bytes=64)
-        h_scales = keep.tile([P, PASSES_1, 1024], U8, align_bytes=64)
-        w_codes = {"mu": keep.tile([P, Z_TILES, PASSES_1 * P], U32, align_bytes=64, name="wmu_codes"),
-                   "ls": keep.tile([P, Z_TILES, PASSES_1 * P], U32, align_bytes=64, name="wls_codes")}
-        w_scales = {"mu": keep.tile([P, Z_TILES, PASSES_1 * P], U8, align_bytes=64, name="wmu_scales"),
-                    "ls": keep.tile([P, Z_TILES, PASSES_1 * P], U8, align_bytes=64, name="wls_scales")}
+        h_codes = keep.tile([P, 2, 1024], U32, align_bytes=64)
+        h_scales = keep.tile([P, 2, 1024], U8, align_bytes=64)
+        wmu_codes = keep.tile([P, 4, 256], U32, align_bytes=64)
+        wmu_scales = keep.tile([P, 4, 256], U8, align_bytes=64)
+        wls_codes = keep.tile([P, 4, 256], U32, align_bytes=64)
+        wls_scales = keep.tile([P, 4, 256], U8, align_bytes=64)
         d_codes = keep.tile([P, 2048], U32, align_bytes=64)
         d_scales = keep.tile([P, 2048], U8, align_bytes=64)
         z_codes = keep.tile([P, 1024], U32, align_bytes=64)
         z_scales = keep.tile([P, 1024], U8, align_bytes=64)
 
-        nc.vector.memset(bias_rows[:], 0.0)
-        make_identity(nc, ident[:])
+        w_sb = {"mu": wmu_sb, "ls": wls_sb}
+        w_codes = {"mu": wmu_codes, "ls": wls_codes}
+        w_scales = {"mu": wmu_scales, "ls": wls_scales}
 
-        h_v = h.rearrange("(r j) k -> r j k", j=BATCH_TILES)
-        eps_v = eps_z.rearrange("(r j) z -> r j z", j=BATCH_TILES)
+        h_v = h.rearrange("(p j) k -> p j k", j=8)
+        eps_v = eps_z.rearrange("(p j) z -> p j z", j=8)
         w_v = {"mu": W_mu_e.rearrange("(u p e) k -> p u e k", u=2, e=2),
                "ls": W_ls_e.rearrange("(u p e) k -> p u e k", u=2, e=2)}
         wd_v = W_in_d.rearrange("(i p) k -> p i k", p=P)
-        out_v = out.rearrange("(r j) n -> r j n", j=BATCH_TILES)
+        out_v = out.rearrange("(p j) n -> p j n", j=8)
 
-        def load_h(pair):
-            nc.sync.dma_start(out=h_sb[:, 2 * pair:2 * pair + 2, :], in_=h_v[:, 2 * pair:2 * pair + 2, :])
+        st = {}
 
-        def load_eps(half):
-            tiles = slice(HALF_TILES * half, HALF_TILES * (half + 1))
-            nc.sync.dma_start(out=eps_sb[:, tiles, :], in_=eps_v[:, tiles, :])
+        def op_ident():
+            nc.vector.memset(braw[:], 0.0)
+            make_identity(nc, ident[:])
 
-        def load_w(m, u):
-            nc.sync.dma_start(out=w_sb[m][:, u], in_=w_v[m][:, u])
+        def op_load(name, part, nbytes):
+            if name == "h_sb":
+                nc.sync.dma_start(out=h_sb[:, 2 * part:2 * part + 2, :], in_=h_v[:, 2 * part:2 * part + 2, :])
+            elif name == "w_sbls":
+                nc.sync.dma_start(out=wls_sb[:, part], in_=w_v["ls"][:, part])
+            elif name == "w_sbmu":
+                nc.sync.dma_start(out=wmu_sb[:, part], in_=w_v["mu"][:, part])
+            elif name == "braw":
+                nc.sync.dma_start(out=braw[0:2, :].bitcast(BF16), in_=b_mu_e.rearrange("(u w) -> u w", u=2))
+                nc.sync.dma_start(out=braw[2:4, :].bitcast(BF16), in_=b_ls_e.rearrange("(u w) -> u w", u=2))
+            elif name == "eps_sb":
+                nc.sync.dma_start(out=eps_sb[:, 4 * part:4 * part + 4, :], in_=eps_v[:, 4 * part:4 * part + 4, :])
+            elif name == "wd_sb":
+                nc.sync.dma_start(out=wd_sb[:, 4 * part:4 * part + 4, :], in_=wd_v[:, 4 * part:4 * part + 4, :])
+            else:
+                nc.sync.dma_start(out=bd_sb[:], in_=b_in_d.partition_broadcast(P))
 
-        def load_wd(quarter):
-            nc.sync.dma_start(out=wd_sb[:, 4 * quarter:4 * quarter + 4, :], in_=wd_v[:, 4 * quarter:4 * quarter + 4, :])
-
-        load_h(0)
-        load_h(1)
-        nc.sync.dma_start(out=bias_rows[0:2, :].bitcast(BF16), in_=b_mu_e.rearrange("(u w) -> u w", u=2))
-        nc.sync.dma_start(out=bias_rows[2:4, :].bitcast(BF16), in_=b_ls_e.rearrange("(u w) -> u w", u=2))
-        load_w("ls", 0)
-        load_w("mu", 0)
-        load_w("ls", 1)
-        load_w("mu", 1)
-        load_eps(0)
-        load_wd(0)
-        load_wd(1)
-        load_h(2)
-        load_h(3)
-        load_eps(1)
-        nc.sync.dma_start(out=bd_sb[:], in_=b_in_d.partition_broadcast(P))
-        load_wd(2)
-        load_wd(3)
-
-        def new_bank(shape):
-            bank = psum.tile(shape, F32, tag="bank", bufs=6)
-            return bank
-
-        def transpose_and_regroup(word_blocks):
-            bank = new_bank([P, 4, P])
-            for n, words in enumerate(word_blocks):
-                nc.tensor.transpose(bank[:, n, :], words, ident[:])
-            grouped = work.tile([P, 2 * BANK], BF16, align_bytes=64, bufs=6)
-            nc.scalar.copy(out=grouped[:].bitcast(F32).rearrange("p (a r u) -> p a r u", a=2, u=2),
-                           in_=bank[:].rearrange("p (a u) r -> p a r u", u=2))
-            return grouped
-
-        def prepare_h(j):
-            words = h_sb[:, j, :].bitcast(F32)
-            grouped = transpose_and_regroup([words[:, P * n:P * (n + 1)] for n in range(4)])
-            rows = slice(P * j, P * (j + 1))
-            for g in range(PASSES_1):
-                nc.vector.quantize_mx(out=h_codes[:, g, rows].bitcast(FP8X4), scales=h_scales[:, g, rows],
-                                      in_=grouped[:, BANK * g:BANK * (g + 1)])
-
-        def prepare_w(m, t):
-            words = w_sb[m][:, t // 2, t % 2, :].bitcast(F32)
-            grouped = transpose_and_regroup([words[:, P * n:P * (n + 1)] for n in range(4)])
-            nc.vector.quantize_mx(out=w_codes[m][:, t, :].bitcast(FP8X4), scales=w_scales[m][:, t, :], in_=grouped[:])
-
-        def prepare_wd(pair):
-            blocks = [wd_sb[:, 2 * pair + n // 2, :].bitcast(F32)[:, P * (n % 2):P * (n % 2 + 1)] for n in range(4)]
-            grouped = transpose_and_regroup(blocks)
-            cols = slice(2 * P * pair, 2 * P * (pair + 1))
-            nc.vector.quantize_mx(out=d_codes[:, cols].bitcast(FP8X4), scales=d_scales[:, cols], in_=grouped[:])
-
-        def prepare_biases():
-            bank = new_bank([P, 4, P])
-            nc.tensor.transpose(bank[:, 0, :], bias_rows[:], ident[:])
-            pairs = bank[:, 0, :].bitcast(BF16)
-            nc.vector.tensor_copy(out=b_mu[:], in_=pairs[:, 0:Z_TILES])
-            nc.vector.tensor_scalar(out=half_b_ls[:], in0=pairs[:, Z_TILES:2 * Z_TILES], scalar1=0.5, scalar2=0.0,
+        def op_bias():
+            bt = psum.tile([P, 4, P], F32, tag="acc", bufs=6)
+            nc.tensor.transpose(bt[:, 0, :], braw[:], ident[:])
+            bview = bt[:, 0, :].bitcast(BF16)
+            nc.vector.tensor_copy(out=bmu[:], in_=bview[:, 0:4])
+            nc.vector.tensor_scalar(out=hbls[:], in0=bview[:, 4:8], scalar1=0.5, scalar2=0.0,
                                     op0=ALU.mult, op1=ALU.add)
 
-        def stage1_passes(m, half, t):
-            cols = slice(BANK * half, BANK * (half + 1))
-            acc = new_bank([P, BANK])
-            for g in range(PASSES_1):
-                nc.tensor.matmul_mx(out=acc[:],
-                                    lhsT=w_codes[m][:, t, P * g:P * (g + 1)].bitcast(FP8X4),
-                                    lhsT_scale=w_scales[m][:, t, P * g:P * (g + 1)],
-                                    rhs=h_codes[:, g, cols].bitcast(FP8X4),
-                                    rhs_scale=h_scales[:, g, cols],
-                                    start=(g == 0), stop=(g == PASSES_1 - 1))
-            return acc
+        def op_T(k, i):
+            bank = psum.tile([P, 4, P], F32, tag="acc", bufs=6)
+            st[("b", k, i)] = bank
+            for a in range(4):
+                if k == "h":
+                    words = h_sb[:, i, :].bitcast(F32)[:, P * a:P * a + P]
+                elif k == "d":
+                    words = wd_sb[:, 2 * i + a // 2, :].bitcast(F32)[:, P * (a % 2):P * (a % 2) + P]
+                else:
+                    words = w_sb[k][:, i // 2, i % 2, :].bitcast(F32)[:, P * a:P * a + P]
+                nc.tensor.transpose(bank[:, a, :], words, ident[:])
 
-        def stage1(half):
-            eps_t = []
-            for u in range(2):
-                bank = psum.tile([P, BANK], F32, tag="eps", bufs=2)
-                for n in range(HALF_TILES):
-                    nc.tensor.transpose(bank[:, P * n:P * (n + 1)],
-                                        eps_sb[:, HALF_TILES * half + n, :].bitcast(F32)[:, P * u:P * (u + 1)], ident[:])
-                eps_t.append(bank)
-            ls = [stage1_passes("ls", half, t) for t in range(Z_TILES)]
-            sd = []
-            for u in range(2):
-                sd_u = work.tile([P, 2, BANK], F32, name="sd", bufs=3)
+        def op_X(k, i, eng):
+            grouped = work.tile([P, 1024], BF16, align_bytes=64, bufs=6)
+            st[("g", k, i)] = grouped
+            gv = grouped[:].bitcast(F32).rearrange("p (a r u) -> p a r u", a=2, u=2)
+            src = st[("b", k, i)][:].rearrange("p (a u) r -> p a r u", u=2)
+            if eng == "S":
+                nc.scalar.copy(out=gv, in_=src)
+            else:
+                nc.vector.tensor_copy(out=gv, in_=src)
+
+        def op_Q(k, i):
+            grouped = st[("g", k, i)]
+            if k == "h":
+                cols = slice(P * i, P * i + P)
+                for g in range(2):
+                    nc.vector.quantize_mx(out=h_codes[:, g, cols].bitcast(FP8X4), scales=h_scales[:, g, cols],
+                                          in_=grouped[:, 512 * g:512 * g + 512])
+            elif k == "d":
+                cols = slice(256 * i, 256 * i + 256)
+                nc.vector.quantize_mx(out=d_codes[:, cols].bitcast(FP8X4), scales=d_scales[:, cols], in_=grouped[:])
+            else:
+                nc.vector.quantize_mx(out=w_codes[k][:, i, :].bitcast(FP8X4), scales=w_scales[k][:, i, :],
+                                      in_=grouped[:])
+
+        def op_te(hh, u):
+            epsT = psum.tile([P, 512], F32, tag="eps", bufs=2)
+            st[("eps", hh, u)] = epsT
+            for jl in range(4):
+                nc.tensor.transpose(epsT[:, P * jl:P * jl + P],
+                                    eps_sb[:, 4 * hh + jl, :].bitcast(F32)[:, P * u:P * u + P], ident[:])
+
+        def op_teX(hh, u):
+            epsS = work.tile([P, 512], F32, bufs=2)
+            nc.scalar.copy(out=epsS[:], in_=st[("eps", hh, u)][:])
+            st[("eps", hh, u)] = epsS
+
+        def op_mm1(m, hh, u):
+            cols = slice(512 * hh, 512 * hh + 512)
+            for e in range(2):
+                t = 2 * u + e
+                bank = psum.tile([P, 512], F32, tag="acc", bufs=6, name="acc_" + m)
+                st[(m, hh, t)] = bank
+                for g in range(2):
+                    nc.tensor.matmul_mx(
+                        out=bank[:],
+                        lhsT=w_codes[m][:, t, P * g:P * g + P].bitcast(FP8X4),
+                        lhsT_scale=w_scales[m][:, t, P * g:P * g + P],
+                        rhs=h_codes[:, g, cols].bitcast(FP8X4),
+                        rhs_scale=h_scales[:, g, cols],
+                        start=(g == 0), stop=(g == 1))
+
+        def op_exp(hh, u):
+            sd = work.tile([P, 2, 512], F32, bufs=3)
+            st[("sd", hh, u)] = sd
+            for e in range(2):
+                t = 2 * u + e
+                nc.scalar.activation(out=sd[:, e, :], in_=st[("ls", hh, t)][:], func=ACT.Exp,
+                                     bias=hbls[:, t:t + 1], scale=0.5)
+
+        def op_mul(hh, u, eng, pieces):
+            noise = work.tile([P, 2, 512], F32, bufs=3)
+            st[("n", hh, u)] = noise
+            sd = st[("sd", hh, u)]
+            ev = st[("eps", hh, u)][:].bitcast(BF16).rearrange("p (b e) -> p e b", e=2)
+            if eng == "G":
                 for e in range(2):
-                    t = 2 * u + e
-                    nc.scalar.activation(out=sd_u[:, e, :], in_=ls[t][:], func=ACT.Exp,
-                                         bias=half_b_ls[:, t:t + 1], scale=0.5)
-                sd.append(sd_u)
-            mu = [stage1_passes("mu", half, t) for t in range(Z_TILES)]
-            z_planes = work.tile([P, Z_TILES, BANK], BF16, bufs=2)
-            for u in range(2):
-                noise = work.tile([P, 2, BANK], F32, bufs=3)
-                nc.vector.tensor_tensor(out=noise[:], in0=sd[u][:],
-                                        in1=eps_t[u][:].bitcast(BF16).rearrange("p (b e) -> p e b", e=2), op=ALU.mult)
-                for e in range(2):
-                    t = 2 * u + e
-                    nc.vector.scalar_tensor_tensor(out=z_planes[:, t, :], in0=mu[t][:], scalar=b_mu[:, t:t + 1],
-                                                   in1=noise[:, e, :], op0=ALU.add, op1=ALU.add)
-            z_grouped = work.tile([P, BANK, Z_TILES], BF16, align_bytes=64, bufs=2)
-            nc.vector.tensor_copy(out=z_grouped[:].rearrange("p (c i) t -> p c t i", i=4),
-                                  in_=z_planes[:].rearrange("p t (c i) -> p c t i", i=4))
-            cols = slice(BANK * half, BANK * (half + 1))
+                    nc.gpsimd.tensor_tensor(out=noise[:, e, :], in0=sd[:, e, :], in1=ev[:, e, :], op=ALU.mult)
+            else:
+                nc.vector.tensor_tensor(out=noise[:], in0=sd[:], in1=ev, op=ALU.mult)
+
+        def op_zadd(hh, u):
+            if u == 0:
+                zp_new = work.tile([P, 4, 512], BF16, name="zp", bufs=2)
+                st[("zp", hh)] = zp_new
+            zp = st[("zp", hh)]
+            for e in range(2):
+                t = 2 * u + e
+                nc.vector.scalar_tensor_tensor(out=zp[:, t, :], in0=st[("mu", hh, t)][:], scalar=bmu[:, t:t + 1],
+                                               in1=st[("n", hh, u)][:, e, :], op0=ALU.add, op1=ALU.add)
+
+        def op_rg(hh, eng):
+            zp = st[("zp", hh)]
+            zg = work.tile([P, 512, 4], BF16, align_bytes=64, bufs=2)
+            st[("zg", hh)] = zg
+            dst = zg[:].rearrange("p (c i) t -> p c t i", i=4)
+            src = zp[:].rearrange("p t (c i) -> p c t i", i=4)
+            if eng == "G":
+                nc.gpsimd.tensor_scalar(out=dst, in0=src, scalar1=1.0, scalar2=0.0, op0=ALU.mult, op1=ALU.add)
+            elif eng == "S":
+                nc.scalar.copy(out=dst, in_=src)
+            else:
+                nc.vector.tensor_copy(out=dst, in_=src)
+
+        def op_qz(hh):
+            cols = slice(512 * hh, 512 * hh + 512)
             nc.vector.quantize_mx(out=z_codes[:, cols].bitcast(FP8X4), scales=z_scales[:, cols],
-                                  in_=z_grouped[:].rearrange("p b t -> p (b t)"))
+                                  in_=st[("zg", hh)][:].rearrange("p b t -> p (b t)"))
 
-        def stage2(j, chunk_pair):
-            result = work.tile([P, 2 * BANK], F32, bufs=6)
-            for n in range(2):
-                cols = slice(BANK * (2 * chunk_pair + n), BANK * (2 * chunk_pair + n + 1))
-                acc = new_bank([P, BANK])
-                nc.tensor.matmul_mx(out=acc[:],
-                                    lhsT=z_codes[:, P * j:P * (j + 1)].bitcast(FP8X4),
-                                    lhsT_scale=z_scales[:, P * j:P * (j + 1)],
-                                    rhs=d_codes[:, cols].bitcast(FP8X4),
-                                    rhs_scale=d_scales[:, cols],
-                                    start=True, stop=True)
-                biased = work.tile([P, BANK], F32, bufs=6)
-                nc.vector.tensor_tensor(out=biased[:], in0=acc[:], in1=bd_sb[:, cols], op=ALU.add)
-                nc.scalar.activation(out=result[:, BANK * n:BANK * (n + 1)], in_=biased[:], func=ACT.Tanh)
-            nc.sync.dma_start(out=out_v[:, j, 2 * BANK * chunk_pair:2 * BANK * (chunk_pair + 1)], in_=result[:])
+        def op_mm2(j, c):
+            cols = slice(512 * c, 512 * c + 512)
+            bank = psum.tile([P, 512], F32, tag="acc", bufs=6, name="acc_o")
+            st[("o", j, c)] = bank
+            nc.tensor.matmul_mx(
+                out=bank[:],
+                lhsT=z_codes[:, P * j:P * j + P].bitcast(FP8X4),
+                lhsT_scale=z_scales[:, P * j:P * j + P],
+                rhs=d_codes[:, cols].bitcast(FP8X4),
+                rhs_scale=d_scales[:, cols],
+                start=True, stop=True)
 
-        for j in range(HALF_TILES):
-            prepare_h(j)
-        for u in range(2):
-            for m in ("ls", "mu"):
-                for e in range(2):
-                    prepare_w(m, 2 * u + e)
-        prepare_biases()
-        stage1(0)
-        for pair in range(4):
-            prepare_wd(pair)
-        for j in range(HALF_TILES, BATCH_TILES):
-            prepare_h(j)
-        for pair in range(4, 8):
-            prepare_wd(pair)
-        stage1(1)
-        for chunk_pair in range(OUT_CHUNKS // 2):
-            for j in range(HALF_TILES):
-                stage2(j, chunk_pair)
-        for j in range(HALF_TILES, BATCH_TILES):
-            for chunk_pair in range(OUT_CHUNKS // 2):
-                stage2(j, chunk_pair)
+        def op_add(j, c):
+            pre = work.tile([P, 512], F32, bufs=6)
+            st[("p", j, c)] = pre
+            nc.vector.tensor_tensor(out=pre[:], in0=st[("o", j, c)][:], in1=bd_sb[:, 512 * c:512 * c + 512], op=ALU.add)
+
+        def op_tanh(j, c):
+            if j in TAPER:
+                res_one = work.tile([P, 1024], F32, name="res", bufs=6)
+                st[("r", j, c)] = res_one
+                nc.scalar.activation(out=res_one[:, 0:512], in_=st[("p", j, c)][:], func=ACT.Tanh)
+                return
+            if c % 2 == 0:
+                res_new = work.tile([P, 1024], F32, name="res", bufs=6)
+                st[("r", j, c // 2)] = res_new
+            res = st[("r", j, c // 2)]
+            nc.scalar.activation(out=res[:, 512 * (c % 2):512 * (c % 2) + 512], in_=st[("p", j, c)][:], func=ACT.Tanh)
+
+        def op_st(j, c):
+            if j in TAPER:
+                nc.sync.dma_start(out=out_v[:, j, 512 * c:512 * (c + 1)], in_=st[("r", j, c)][:, 0:512])
+                return
+            nc.sync.dma_start(out=out_v[:, j, 512 * (c - 1):512 * (c + 1)], in_=st[("r", j, c // 2)][:])
+
+        ops = {"ident": op_ident, "load": op_load, "bias": op_bias, "T": op_T, "X": op_X, "Q": op_Q, "te": op_te,
+               "teX": op_teX, "mm1": op_mm1, "exp": op_exp, "mul": op_mul, "zadd": op_zadd, "rg": op_rg, "qz": op_qz,
+               "mm2": op_mm2, "add": op_add, "tanh": op_tanh, "st": op_st}
+        for op in PROGRAM:
+            ops[op[0]](*op[1:])

@@ -14,240 +14,12 @@ ACT = mybir.ActivationFunctionType
 ALU = mybir.AluOpType
 
 P = 128
-TAPER = ()
-
-PROGRAM = [
-    ("ident",),
-    ("load", "h_sb", 0, 524288),
-    ("load", "h_sb", 1, 524288),
-    ("load", "braw", "", 1024),
-    ("load", "w_sbls", 0, 524288),
-    ("load", "w_sbmu", 0, 524288),
-    ("load", "w_sbls", 1, 524288),
-    ("load", "w_sbmu", 1, 524288),
-    ("load", "eps_sb", 0, 524288),
-    ("load", "wd_sb", 0, 524288),
-    ("load", "wd_sb", 1, 524288),
-    ("load", "h_sb", 2, 524288),
-    ("load", "h_sb", 3, 524288),
-    ("load", "eps_sb", 1, 524288),
-    ("load", "bd", "", 524288),
-    ("load", "wd_sb", 2, 524288),
-    ("load", "wd_sb", 3, 524288),
-    ("T", "h", 0),
-    ("X", "h", 0, "S"),
-    ("Q", "h", 0),
-    ("T", "h", 1),
-    ("X", "h", 1, "S"),
-    ("Q", "h", 1),
-    ("T", "h", 2),
-    ("X", "h", 2, "S"),
-    ("Q", "h", 2),
-    ("T", "h", 3),
-    ("X", "h", 3, "S"),
-    ("Q", "h", 3),
-    ("T", "ls", 0),
-    ("X", "ls", 0, "S"),
-    ("Q", "ls", 0),
-    ("T", "ls", 1),
-    ("X", "ls", 1, "S"),
-    ("Q", "ls", 1),
-    ("T", "mu", 0),
-    ("X", "mu", 0, "S"),
-    ("Q", "mu", 0),
-    ("T", "mu", 1),
-    ("X", "mu", 1, "S"),
-    ("Q", "mu", 1),
-    ("T", "ls", 2),
-    ("X", "ls", 2, "S"),
-    ("Q", "ls", 2),
-    ("T", "ls", 3),
-    ("X", "ls", 3, "S"),
-    ("Q", "ls", 3),
-    ("T", "mu", 2),
-    ("X", "mu", 2, "S"),
-    ("Q", "mu", 2),
-    ("T", "mu", 3),
-    ("X", "mu", 3, "S"),
-    ("Q", "mu", 3),
-    ("bias",),
-    ("te", 0, 0),
-    ("te", 0, 1),
-    ("mm1", "ls", 0, 0),
-    ("mm1", "ls", 0, 1),
-    ("exp", 0, 0),
-    ("exp", 0, 1),
-    ("mm1", "mu", 0, 0),
-    ("mm1", "mu", 0, 1),
-    ("mul", 0, 0, "V", 1),
-    ("zadd", 0, 0),
-    ("mul", 0, 1, "V", 1),
-    ("zadd", 0, 1),
-    ("rg", 0, "V"),
-    ("qz", 0),
-    ("T", "d", 0),
-    ("X", "d", 0, "S"),
-    ("Q", "d", 0),
-    ("T", "d", 1),
-    ("X", "d", 1, "S"),
-    ("Q", "d", 1),
-    ("T", "d", 2),
-    ("X", "d", 2, "S"),
-    ("Q", "d", 2),
-    ("T", "d", 3),
-    ("X", "d", 3, "S"),
-    ("Q", "d", 3),
-    ("T", "h", 4),
-    ("X", "h", 4, "S"),
-    ("Q", "h", 4),
-    ("T", "h", 5),
-    ("X", "h", 5, "S"),
-    ("Q", "h", 5),
-    ("mm2", 0, 0),
-    ("add", 0, 0),
-    ("tanh", 0, 0),
-    ("mm2", 0, 1),
-    ("add", 0, 1),
-    ("tanh", 0, 1),
-    ("st", 0, 1),
-    ("T", "h", 6),
-    ("X", "h", 6, "S"),
-    ("Q", "h", 6),
-    ("T", "h", 7),
-    ("X", "h", 7, "S"),
-    ("Q", "h", 7),
-    ("mm2", 1, 0),
-    ("add", 1, 0),
-    ("tanh", 1, 0),
-    ("mm2", 1, 1),
-    ("add", 1, 1),
-    ("tanh", 1, 1),
-    ("st", 1, 1),
-    ("te", 1, 0),
-    ("te", 1, 1),
-    ("mm1", "ls", 1, 0),
-    ("mm1", "ls", 1, 1),
-    ("mm2", 2, 0),
-    ("add", 2, 0),
-    ("tanh", 2, 0),
-    ("mm2", 2, 1),
-    ("add", 2, 1),
-    ("tanh", 2, 1),
-    ("st", 2, 1),
-    ("exp", 1, 0),
-    ("exp", 1, 1),
-    ("mm1", "mu", 1, 0),
-    ("mm1", "mu", 1, 1),
-    ("mm2", 3, 0),
-    ("add", 3, 0),
-    ("tanh", 3, 0),
-    ("mm2", 3, 1),
-    ("add", 3, 1),
-    ("tanh", 3, 1),
-    ("st", 3, 1),
-    ("T", "d", 4),
-    ("X", "d", 4, "S"),
-    ("Q", "d", 4),
-    ("T", "d", 5),
-    ("X", "d", 5, "S"),
-    ("Q", "d", 5),
-    ("mul", 1, 0, "V", 1),
-    ("zadd", 1, 0),
-    ("T", "d", 6),
-    ("X", "d", 6, "S"),
-    ("Q", "d", 6),
-    ("T", "d", 7),
-    ("X", "d", 7, "S"),
-    ("Q", "d", 7),
-    ("mul", 1, 1, "V", 1),
-    ("zadd", 1, 1),
-    ("mm2", 0, 2),
-    ("add", 0, 2),
-    ("tanh", 0, 2),
-    ("mm2", 0, 3),
-    ("add", 0, 3),
-    ("tanh", 0, 3),
-    ("st", 0, 3),
-    ("rg", 1, "V"),
-    ("qz", 1),
-    ("mm2", 1, 2),
-    ("add", 1, 2),
-    ("tanh", 1, 2),
-    ("mm2", 1, 3),
-    ("add", 1, 3),
-    ("tanh", 1, 3),
-    ("st", 1, 3),
-    ("mm2", 2, 2),
-    ("add", 2, 2),
-    ("tanh", 2, 2),
-    ("mm2", 2, 3),
-    ("add", 2, 3),
-    ("tanh", 2, 3),
-    ("st", 2, 3),
-    ("mm2", 3, 2),
-    ("add", 3, 2),
-    ("tanh", 3, 2),
-    ("mm2", 3, 3),
-    ("add", 3, 3),
-    ("tanh", 3, 3),
-    ("st", 3, 3),
-    ("mm2", 4, 0),
-    ("add", 4, 0),
-    ("tanh", 4, 0),
-    ("mm2", 4, 1),
-    ("add", 4, 1),
-    ("tanh", 4, 1),
-    ("st", 4, 1),
-    ("mm2", 4, 2),
-    ("add", 4, 2),
-    ("tanh", 4, 2),
-    ("mm2", 4, 3),
-    ("add", 4, 3),
-    ("tanh", 4, 3),
-    ("st", 4, 3),
-    ("mm2", 5, 0),
-    ("add", 5, 0),
-    ("tanh", 5, 0),
-    ("mm2", 5, 1),
-    ("add", 5, 1),
-    ("tanh", 5, 1),
-    ("st", 5, 1),
-    ("mm2", 5, 2),
-    ("add", 5, 2),
-    ("tanh", 5, 2),
-    ("mm2", 5, 3),
-    ("add", 5, 3),
-    ("tanh", 5, 3),
-    ("st", 5, 3),
-    ("mm2", 6, 0),
-    ("add", 6, 0),
-    ("tanh", 6, 0),
-    ("mm2", 6, 1),
-    ("add", 6, 1),
-    ("tanh", 6, 1),
-    ("st", 6, 1),
-    ("mm2", 6, 2),
-    ("add", 6, 2),
-    ("tanh", 6, 2),
-    ("mm2", 6, 3),
-    ("add", 6, 3),
-    ("tanh", 6, 3),
-    ("st", 6, 3),
-    ("mm2", 7, 0),
-    ("add", 7, 0),
-    ("tanh", 7, 0),
-    ("mm2", 7, 1),
-    ("add", 7, 1),
-    ("tanh", 7, 1),
-    ("st", 7, 1),
-    ("mm2", 7, 2),
-    ("add", 7, 2),
-    ("tanh", 7, 2),
-    ("mm2", 7, 3),
-    ("add", 7, 3),
-    ("tanh", 7, 3),
-    ("st", 7, 3),
-]
+BANK = 512
+BATCH_TILES = 8
+HALF_TILES = 4
+Z_TILES = 4
+PASSES_1 = 2
+OUT_CHUNKS = 4
 
 
 def tile_vae_pa_kernel(tc, h, W_mu_e, b_mu_e, W_ls_e, b_ls_e, eps_z, W_in_d, b_in_d, out):
@@ -257,217 +29,190 @@ def tile_vae_pa_kernel(tc, h, W_mu_e, b_mu_e, W_ls_e, b_ls_e, eps_z, W_in_d, b_i
         work = ctx.enter_context(tc.tile_pool(name="work", bufs=2))
         psum = ctx.enter_context(tc.psum_pool(name="psum", bufs=2))
 
-        h_sb = keep.tile([P, 8, 1024], BF16)
-        wmu_sb = keep.tile([P, 2, 2, 1024], BF16)
-        wls_sb = keep.tile([P, 2, 2, 1024], BF16)
-        eps_sb = keep.tile([P, 8, 512], BF16)
+        h_sb = keep.tile([P, BATCH_TILES, 1024], BF16)
+        eps_sb = keep.tile([P, BATCH_TILES, 512], BF16)
+        w_sb = {"mu": keep.tile([P, 2, 2, 1024], BF16, name="wmu_sb"),
+                "ls": keep.tile([P, 2, 2, 1024], BF16, name="wls_sb")}
         wd_sb = keep.tile([P, 16, 512], BF16)
         bd_sb = keep.tile([P, 2048], BF16)
-        braw = keep.tile([P, P], F32)
+        bias_rows = keep.tile([P, P], F32)
         ident = keep.tile([P, P], F32)
-        bmu = keep.tile([P, 4], F32)
-        hbls = keep.tile([P, 4], F32)
+        b_mu = keep.tile([P, Z_TILES], F32)
+        half_b_ls = keep.tile([P, Z_TILES], F32)
 
-        h_codes = keep.tile([P, 2, 1024], U32, align_bytes=64)
-        h_scales = keep.tile([P, 2, 1024], U8, align_bytes=64)
-        wmu_codes = keep.tile([P, 4, 256], U32, align_bytes=64)
-        wmu_scales = keep.tile([P, 4, 256], U8, align_bytes=64)
-        wls_codes = keep.tile([P, 4, 256], U32, align_bytes=64)
-        wls_scales = keep.tile([P, 4, 256], U8, align_bytes=64)
+        h_codes = keep.tile([P, PASSES_1, 1024], U32, align_bytes=64)
+        h_scales = keep.tile([P, PASSES_1, 1024], U8, align_bytes=64)
+        w_codes = {"mu": keep.tile([P, Z_TILES, PASSES_1 * P], U32, align_bytes=64, name="wmu_codes"),
+                   "ls": keep.tile([P, Z_TILES, PASSES_1 * P], U32, align_bytes=64, name="wls_codes")}
+        w_scales = {"mu": keep.tile([P, Z_TILES, PASSES_1 * P], U8, align_bytes=64, name="wmu_scales"),
+                    "ls": keep.tile([P, Z_TILES, PASSES_1 * P], U8, align_bytes=64, name="wls_scales")}
         d_codes = keep.tile([P, 2048], U32, align_bytes=64)
         d_scales = keep.tile([P, 2048], U8, align_bytes=64)
         z_codes = keep.tile([P, 1024], U32, align_bytes=64)
         z_scales = keep.tile([P, 1024], U8, align_bytes=64)
 
-        w_sb = {"mu": wmu_sb, "ls": wls_sb}
-        w_codes = {"mu": wmu_codes, "ls": wls_codes}
-        w_scales = {"mu": wmu_scales, "ls": wls_scales}
+        nc.vector.memset(bias_rows[:], 0.0)
+        make_identity(nc, ident[:])
 
-        h_v = h.rearrange("(p j) k -> p j k", j=8)
-        eps_v = eps_z.rearrange("(p j) z -> p j z", j=8)
+        h_v = h.rearrange("(r j) k -> r j k", j=BATCH_TILES)
+        eps_v = eps_z.rearrange("(r j) z -> r j z", j=BATCH_TILES)
         w_v = {"mu": W_mu_e.rearrange("(u p e) k -> p u e k", u=2, e=2),
                "ls": W_ls_e.rearrange("(u p e) k -> p u e k", u=2, e=2)}
         wd_v = W_in_d.rearrange("(i p) k -> p i k", p=P)
-        out_v = out.rearrange("(p j) n -> p j n", j=8)
+        out_v = out.rearrange("(r j) n -> r j n", j=BATCH_TILES)
 
-        st = {}
+        def load_h(first, tiles):
+            nc.sync.dma_start(out=h_sb[:, first:first + tiles, :], in_=h_v[:, first:first + tiles, :])
 
-        def op_ident():
-            nc.vector.memset(braw[:], 0.0)
-            make_identity(nc, ident[:])
+        def load_eps(half):
+            tiles = slice(HALF_TILES * half, HALF_TILES * (half + 1))
+            nc.sync.dma_start(out=eps_sb[:, tiles, :], in_=eps_v[:, tiles, :])
 
-        def op_load(name, part, nbytes):
-            if name == "h_sb":
-                nc.sync.dma_start(out=h_sb[:, 2 * part:2 * part + 2, :], in_=h_v[:, 2 * part:2 * part + 2, :])
-            elif name == "w_sbls":
-                nc.sync.dma_start(out=wls_sb[:, part], in_=w_v["ls"][:, part])
-            elif name == "w_sbmu":
-                nc.sync.dma_start(out=wmu_sb[:, part], in_=w_v["mu"][:, part])
-            elif name == "braw":
-                nc.sync.dma_start(out=braw[0:2, :].bitcast(BF16), in_=b_mu_e.rearrange("(u w) -> u w", u=2))
-                nc.sync.dma_start(out=braw[2:4, :].bitcast(BF16), in_=b_ls_e.rearrange("(u w) -> u w", u=2))
-            elif name == "eps_sb":
-                nc.sync.dma_start(out=eps_sb[:, 4 * part:4 * part + 4, :], in_=eps_v[:, 4 * part:4 * part + 4, :])
-            elif name == "wd_sb":
-                nc.sync.dma_start(out=wd_sb[:, 4 * part:4 * part + 4, :], in_=wd_v[:, 4 * part:4 * part + 4, :])
-            else:
-                nc.sync.dma_start(out=bd_sb[:], in_=b_in_d.partition_broadcast(P))
+        def load_w(m, u):
+            nc.sync.dma_start(out=w_sb[m][:, u], in_=w_v[m][:, u])
 
-        def op_bias():
-            bt = psum.tile([P, 4, P], F32, tag="acc", bufs=6)
-            nc.tensor.transpose(bt[:, 0, :], braw[:], ident[:])
-            bview = bt[:, 0, :].bitcast(BF16)
-            nc.vector.tensor_copy(out=bmu[:], in_=bview[:, 0:4])
-            nc.vector.tensor_scalar(out=hbls[:], in0=bview[:, 4:8], scalar1=0.5, scalar2=0.0,
+        def load_wd(quarter):
+            nc.sync.dma_start(out=wd_sb[:, 4 * quarter:4 * quarter + 4, :], in_=wd_v[:, 4 * quarter:4 * quarter + 4, :])
+
+        load_h(0, 1)
+        load_h(1, 1)
+        load_h(2, 2)
+        load_w("ls", 0)
+        load_w("mu", 0)
+        load_w("ls", 1)
+        load_w("mu", 1)
+        nc.sync.dma_start(out=bias_rows[0:2, :].bitcast(BF16), in_=b_mu_e.rearrange("(u w) -> u w", u=2))
+        nc.sync.dma_start(out=bias_rows[2:4, :].bitcast(BF16), in_=b_ls_e.rearrange("(u w) -> u w", u=2))
+        load_eps(0)
+        load_wd(0)
+        load_wd(1)
+        load_h(4, 2)
+        load_h(6, 2)
+        load_wd(2)
+        load_wd(3)
+        load_eps(1)
+        nc.sync.dma_start(out=bd_sb[:], in_=b_in_d.partition_broadcast(P))
+
+        def new_bank(shape):
+            bank = psum.tile(shape, F32, tag="bank", bufs=6)
+            return bank
+
+        def transpose_and_regroup(word_blocks):
+            bank = new_bank([P, 4, P])
+            for n, words in enumerate(word_blocks):
+                nc.tensor.transpose(bank[:, n, :], words, ident[:])
+            grouped = work.tile([P, 2 * BANK], BF16, align_bytes=64, bufs=6)
+            nc.scalar.copy(out=grouped[:].bitcast(F32).rearrange("p (a r u) -> p a r u", a=2, u=2),
+                           in_=bank[:].rearrange("p (a u) r -> p a r u", u=2))
+            return grouped
+
+        def prepare_h(j):
+            words = h_sb[:, j, :].bitcast(F32)
+            grouped = transpose_and_regroup([words[:, P * n:P * (n + 1)] for n in range(4)])
+            rows = slice(P * j, P * (j + 1))
+            for g in range(PASSES_1):
+                nc.vector.quantize_mx(out=h_codes[:, g, rows].bitcast(FP8X4), scales=h_scales[:, g, rows],
+                                      in_=grouped[:, BANK * g:BANK * (g + 1)])
+
+        def prepare_w(m, t):
+            words = w_sb[m][:, t // 2, t % 2, :].bitcast(F32)
+            grouped = transpose_and_regroup([words[:, P * n:P * (n + 1)] for n in range(4)])
+            nc.vector.quantize_mx(out=w_codes[m][:, t, :].bitcast(FP8X4), scales=w_scales[m][:, t, :], in_=grouped[:])
+
+        def prepare_wd(pair):
+            blocks = [wd_sb[:, 2 * pair + n // 2, :].bitcast(F32)[:, P * (n % 2):P * (n % 2 + 1)] for n in range(4)]
+            grouped = transpose_and_regroup(blocks)
+            cols = slice(2 * P * pair, 2 * P * (pair + 1))
+            nc.vector.quantize_mx(out=d_codes[:, cols].bitcast(FP8X4), scales=d_scales[:, cols], in_=grouped[:])
+
+        def prepare_biases():
+            bank = new_bank([P, 4, P])
+            nc.tensor.transpose(bank[:, 0, :], bias_rows[:], ident[:])
+            pairs = bank[:, 0, :].bitcast(BF16)
+            nc.vector.tensor_copy(out=b_mu[:], in_=pairs[:, 0:Z_TILES])
+            nc.vector.tensor_scalar(out=half_b_ls[:], in0=pairs[:, Z_TILES:2 * Z_TILES], scalar1=0.5, scalar2=0.0,
                                     op0=ALU.mult, op1=ALU.add)
 
-        def op_T(k, i):
-            bank = psum.tile([P, 4, P], F32, tag="acc", bufs=6)
-            st[("b", k, i)] = bank
-            for a in range(4):
-                if k == "h":
-                    words = h_sb[:, i, :].bitcast(F32)[:, P * a:P * a + P]
-                elif k == "d":
-                    words = wd_sb[:, 2 * i + a // 2, :].bitcast(F32)[:, P * (a % 2):P * (a % 2) + P]
-                else:
-                    words = w_sb[k][:, i // 2, i % 2, :].bitcast(F32)[:, P * a:P * a + P]
-                nc.tensor.transpose(bank[:, a, :], words, ident[:])
+        def stage1_passes(m, half, t):
+            cols = slice(BANK * half, BANK * (half + 1))
+            acc = new_bank([P, BANK])
+            for g in range(PASSES_1):
+                nc.tensor.matmul_mx(out=acc[:],
+                                    lhsT=w_codes[m][:, t, P * g:P * (g + 1)].bitcast(FP8X4),
+                                    lhsT_scale=w_scales[m][:, t, P * g:P * (g + 1)],
+                                    rhs=h_codes[:, g, cols].bitcast(FP8X4),
+                                    rhs_scale=h_scales[:, g, cols],
+                                    start=(g == 0), stop=(g == PASSES_1 - 1))
+            return acc
 
-        def op_X(k, i, eng):
-            grouped = work.tile([P, 1024], BF16, align_bytes=64, bufs=6)
-            st[("g", k, i)] = grouped
-            gv = grouped[:].bitcast(F32).rearrange("p (a r u) -> p a r u", a=2, u=2)
-            src = st[("b", k, i)][:].rearrange("p (a u) r -> p a r u", u=2)
-            if eng == "S":
-                nc.scalar.copy(out=gv, in_=src)
-            else:
-                nc.vector.tensor_copy(out=gv, in_=src)
-
-        def op_Q(k, i):
-            grouped = st[("g", k, i)]
-            if k == "h":
-                cols = slice(P * i, P * i + P)
-                for g in range(2):
-                    nc.vector.quantize_mx(out=h_codes[:, g, cols].bitcast(FP8X4), scales=h_scales[:, g, cols],
-                                          in_=grouped[:, 512 * g:512 * g + 512])
-            elif k == "d":
-                cols = slice(256 * i, 256 * i + 256)
-                nc.vector.quantize_mx(out=d_codes[:, cols].bitcast(FP8X4), scales=d_scales[:, cols], in_=grouped[:])
-            else:
-                nc.vector.quantize_mx(out=w_codes[k][:, i, :].bitcast(FP8X4), scales=w_scales[k][:, i, :],
-                                      in_=grouped[:])
-
-        def op_te(hh, u):
-            epsT = psum.tile([P, 512], F32, tag="eps", bufs=2)
-            st[("eps", hh, u)] = epsT
-            for jl in range(4):
-                nc.tensor.transpose(epsT[:, P * jl:P * jl + P],
-                                    eps_sb[:, 4 * hh + jl, :].bitcast(F32)[:, P * u:P * u + P], ident[:])
-
-        def op_teX(hh, u):
-            epsS = work.tile([P, 512], F32, bufs=2)
-            nc.scalar.copy(out=epsS[:], in_=st[("eps", hh, u)][:])
-            st[("eps", hh, u)] = epsS
-
-        def op_mm1(m, hh, u):
-            cols = slice(512 * hh, 512 * hh + 512)
-            for e in range(2):
-                t = 2 * u + e
-                bank = psum.tile([P, 512], F32, tag="acc", bufs=6, name="acc_" + m)
-                st[(m, hh, t)] = bank
-                for g in range(2):
-                    nc.tensor.matmul_mx(
-                        out=bank[:],
-                        lhsT=w_codes[m][:, t, P * g:P * g + P].bitcast(FP8X4),
-                        lhsT_scale=w_scales[m][:, t, P * g:P * g + P],
-                        rhs=h_codes[:, g, cols].bitcast(FP8X4),
-                        rhs_scale=h_scales[:, g, cols],
-                        start=(g == 0), stop=(g == 1))
-
-        def op_exp(hh, u):
-            sd = work.tile([P, 2, 512], F32, bufs=3)
-            st[("sd", hh, u)] = sd
-            for e in range(2):
-                t = 2 * u + e
-                nc.scalar.activation(out=sd[:, e, :], in_=st[("ls", hh, t)][:], func=ACT.Exp,
-                                     bias=hbls[:, t:t + 1], scale=0.5)
-
-        def op_mul(hh, u, eng, pieces):
-            noise = work.tile([P, 2, 512], F32, bufs=3)
-            st[("n", hh, u)] = noise
-            sd = st[("sd", hh, u)]
-            ev = st[("eps", hh, u)][:].bitcast(BF16).rearrange("p (b e) -> p e b", e=2)
-            if eng == "G":
+        def stage1(half):
+            eps_t = []
+            for u in range(2):
+                bank = psum.tile([P, BANK], F32, tag="eps", bufs=2)
+                for n in range(HALF_TILES):
+                    nc.tensor.transpose(bank[:, P * n:P * (n + 1)],
+                                        eps_sb[:, HALF_TILES * half + n, :].bitcast(F32)[:, P * u:P * (u + 1)], ident[:])
+                eps_t.append(bank)
+            ls = [stage1_passes("ls", half, t) for t in range(Z_TILES)]
+            sd = []
+            for u in range(2):
+                sd_u = work.tile([P, 2, BANK], F32, name="sd", bufs=3)
                 for e in range(2):
-                    nc.gpsimd.tensor_tensor(out=noise[:, e, :], in0=sd[:, e, :], in1=ev[:, e, :], op=ALU.mult)
-            else:
-                nc.vector.tensor_tensor(out=noise[:], in0=sd[:], in1=ev, op=ALU.mult)
-
-        def op_zadd(hh, u):
-            if u == 0:
-                zp_new = work.tile([P, 4, 512], BF16, name="zp", bufs=2)
-                st[("zp", hh)] = zp_new
-            zp = st[("zp", hh)]
-            for e in range(2):
-                t = 2 * u + e
-                nc.vector.scalar_tensor_tensor(out=zp[:, t, :], in0=st[("mu", hh, t)][:], scalar=bmu[:, t:t + 1],
-                                               in1=st[("n", hh, u)][:, e, :], op0=ALU.add, op1=ALU.add)
-
-        def op_rg(hh, eng):
-            zp = st[("zp", hh)]
-            zg = work.tile([P, 512, 4], BF16, align_bytes=64, bufs=2)
-            st[("zg", hh)] = zg
-            dst = zg[:].rearrange("p (c i) t -> p c t i", i=4)
-            src = zp[:].rearrange("p t (c i) -> p c t i", i=4)
-            if eng == "G":
-                nc.gpsimd.tensor_scalar(out=dst, in0=src, scalar1=1.0, scalar2=0.0, op0=ALU.mult, op1=ALU.add)
-            elif eng == "S":
-                nc.scalar.copy(out=dst, in_=src)
-            else:
-                nc.vector.tensor_copy(out=dst, in_=src)
-
-        def op_qz(hh):
-            cols = slice(512 * hh, 512 * hh + 512)
+                    t = 2 * u + e
+                    nc.scalar.activation(out=sd_u[:, e, :], in_=ls[t][:], func=ACT.Exp,
+                                         bias=half_b_ls[:, t:t + 1], scale=0.5)
+                sd.append(sd_u)
+            mu = [stage1_passes("mu", half, t) for t in range(Z_TILES)]
+            z_planes = work.tile([P, Z_TILES, BANK], BF16, bufs=2)
+            for u in range(2):
+                noise = work.tile([P, 2, BANK], F32, bufs=3)
+                nc.vector.tensor_tensor(out=noise[:], in0=sd[u][:],
+                                        in1=eps_t[u][:].bitcast(BF16).rearrange("p (b e) -> p e b", e=2), op=ALU.mult)
+                for e in range(2):
+                    t = 2 * u + e
+                    nc.vector.scalar_tensor_tensor(out=z_planes[:, t, :], in0=mu[t][:], scalar=b_mu[:, t:t + 1],
+                                                   in1=noise[:, e, :], op0=ALU.add, op1=ALU.add)
+            z_grouped = work.tile([P, BANK, Z_TILES], BF16, align_bytes=64, bufs=2)
+            nc.vector.tensor_copy(out=z_grouped[:].rearrange("p (c i) t -> p c t i", i=4),
+                                  in_=z_planes[:].rearrange("p t (c i) -> p c t i", i=4))
+            cols = slice(BANK * half, BANK * (half + 1))
             nc.vector.quantize_mx(out=z_codes[:, cols].bitcast(FP8X4), scales=z_scales[:, cols],
-                                  in_=st[("zg", hh)][:].rearrange("p b t -> p (b t)"))
+                                  in_=z_grouped[:].rearrange("p b t -> p (b t)"))
 
-        def op_mm2(j, c):
-            cols = slice(512 * c, 512 * c + 512)
-            bank = psum.tile([P, 512], F32, tag="acc", bufs=6, name="acc_o")
-            st[("o", j, c)] = bank
-            nc.tensor.matmul_mx(
-                out=bank[:],
-                lhsT=z_codes[:, P * j:P * j + P].bitcast(FP8X4),
-                lhsT_scale=z_scales[:, P * j:P * j + P],
-                rhs=d_codes[:, cols].bitcast(FP8X4),
-                rhs_scale=d_scales[:, cols],
-                start=True, stop=True)
+        def stage2(j, chunk_pair):
+            result = work.tile([P, 2 * BANK], F32, bufs=6)
+            for n in range(2):
+                cols = slice(BANK * (2 * chunk_pair + n), BANK * (2 * chunk_pair + n + 1))
+                acc = new_bank([P, BANK])
+                nc.tensor.matmul_mx(out=acc[:],
+                                    lhsT=z_codes[:, P * j:P * (j + 1)].bitcast(FP8X4),
+                                    lhsT_scale=z_scales[:, P * j:P * (j + 1)],
+                                    rhs=d_codes[:, cols].bitcast(FP8X4),
+                                    rhs_scale=d_scales[:, cols],
+                                    start=True, stop=True)
+                biased = work.tile([P, BANK], F32, bufs=6)
+                nc.vector.tensor_tensor(out=biased[:], in0=acc[:], in1=bd_sb[:, cols], op=ALU.add)
+                nc.scalar.activation(out=result[:, BANK * n:BANK * (n + 1)], in_=biased[:], func=ACT.Tanh)
+            nc.sync.dma_start(out=out_v[:, j, 2 * BANK * chunk_pair:2 * BANK * (chunk_pair + 1)], in_=result[:])
 
-        def op_add(j, c):
-            pre = work.tile([P, 512], F32, bufs=6)
-            st[("p", j, c)] = pre
-            nc.vector.tensor_tensor(out=pre[:], in0=st[("o", j, c)][:], in1=bd_sb[:, 512 * c:512 * c + 512], op=ALU.add)
-
-        def op_tanh(j, c):
-            if j in TAPER:
-                res_one = work.tile([P, 1024], F32, name="res", bufs=6)
-                st[("r", j, c)] = res_one
-                nc.scalar.activation(out=res_one[:, 0:512], in_=st[("p", j, c)][:], func=ACT.Tanh)
-                return
-            if c % 2 == 0:
-                res_new = work.tile([P, 1024], F32, name="res", bufs=6)
-                st[("r", j, c // 2)] = res_new
-            res = st[("r", j, c // 2)]
-            nc.scalar.activation(out=res[:, 512 * (c % 2):512 * (c % 2) + 512], in_=st[("p", j, c)][:], func=ACT.Tanh)
-
-        def op_st(j, c):
-            if j in TAPER:
-                nc.sync.dma_start(out=out_v[:, j, 512 * c:512 * (c + 1)], in_=st[("r", j, c)][:, 0:512])
-                return
-            nc.sync.dma_start(out=out_v[:, j, 512 * (c - 1):512 * (c + 1)], in_=st[("r", j, c // 2)][:])
-
-        ops = {"ident": op_ident, "load": op_load, "bias": op_bias, "T": op_T, "X": op_X, "Q": op_Q, "te": op_te,
-               "teX": op_teX, "mm1": op_mm1, "exp": op_exp, "mul": op_mul, "zadd": op_zadd, "rg": op_rg, "qz": op_qz,
-               "mm2": op_mm2, "add": op_add, "tanh": op_tanh, "st": op_st}
-        for op in PROGRAM:
-            ops[op[0]](*op[1:])
+        for j in range(HALF_TILES):
+            prepare_h(j)
+        for u in range(2):
+            for m in ("ls", "mu"):
+                for e in range(2):
+                    prepare_w(m, 2 * u + e)
+        prepare_biases()
+        stage1(0)
+        for pair in range(4):
+            prepare_wd(pair)
+        for j in range(HALF_TILES, BATCH_TILES):
+            prepare_h(j)
+        for pair in range(4, 8):
+            prepare_wd(pair)
+        stage1(1)
+        for chunk_pair in range(OUT_CHUNKS // 2):
+            for j in range(HALF_TILES):
+                stage2(j, chunk_pair)
+        for j in range(HALF_TILES, BATCH_TILES):
+            for chunk_pair in range(OUT_CHUNKS // 2):
+                stage2(j, chunk_pair)

@@ -78,11 +78,11 @@ def tile_vae_pa_kernel(tc, h, W_mu_e, b_mu_e, W_ls_e, b_ls_e, eps_z, W_in_d, b_i
         load_h(1, 1)
         load_h(2, 2)
         load_w("ls", 0)
-        load_w("mu", 0)
         load_w("ls", 1)
-        load_w("mu", 1)
         nc.sync.dma_start(out=bias_rows[0:2, :].bitcast(BF16), in_=b_mu_e.rearrange("(u w) -> u w", u=2))
         nc.sync.dma_start(out=bias_rows[2:4, :].bitcast(BF16), in_=b_ls_e.rearrange("(u w) -> u w", u=2))
+        load_w("mu", 0)
+        load_w("mu", 1)
         load_eps(0)
         load_wd(0)
         load_wd(1)
@@ -101,7 +101,7 @@ def tile_vae_pa_kernel(tc, h, W_mu_e, b_mu_e, W_ls_e, b_ls_e, eps_z, W_in_d, b_i
             bank = new_bank([P, 4, P])
             for n, words in enumerate(word_blocks):
                 nc.tensor.transpose(bank[:, n, :], words, ident[:])
-            grouped = work.tile([P, 2 * BANK], BF16, align_bytes=64, bufs=6)
+            grouped = work.tile([P, 2 * BANK], BF16, align_bytes=64, bufs=8)
             nc.scalar.copy(out=grouped[:].bitcast(F32).rearrange("p (a r u) -> p a r u", a=2, u=2),
                            in_=bank[:].rearrange("p (a u) r -> p a r u", u=2))
             return grouped
@@ -110,20 +110,25 @@ def tile_vae_pa_kernel(tc, h, W_mu_e, b_mu_e, W_ls_e, b_ls_e, eps_z, W_in_d, b_i
             words = h_sb[:, j, :].bitcast(F32)
             grouped = transpose_and_regroup([words[:, P * n:P * (n + 1)] for n in range(4)])
             rows = slice(P * j, P * (j + 1))
-            for g in range(PASSES_1):
-                nc.vector.quantize_mx(out=h_codes[:, g, rows].bitcast(FP8X4), scales=h_scales[:, g, rows],
-                                      in_=grouped[:, BANK * g:BANK * (g + 1)])
+
+            def quantise():
+                for g in range(PASSES_1):
+                    nc.vector.quantize_mx(out=h_codes[:, g, rows].bitcast(FP8X4), scales=h_scales[:, g, rows],
+                                          in_=grouped[:, BANK * g:BANK * (g + 1)])
+            return quantise
 
         def prepare_w(m, t):
             words = w_sb[m][:, t // 2, t % 2, :].bitcast(F32)
             grouped = transpose_and_regroup([words[:, P * n:P * (n + 1)] for n in range(4)])
-            nc.vector.quantize_mx(out=w_codes[m][:, t, :].bitcast(FP8X4), scales=w_scales[m][:, t, :], in_=grouped[:])
+            return lambda: nc.vector.quantize_mx(out=w_codes[m][:, t, :].bitcast(FP8X4), scales=w_scales[m][:, t, :],
+                                                 in_=grouped[:])
 
         def prepare_wd(pair):
             blocks = [wd_sb[:, 2 * pair + n // 2, :].bitcast(F32)[:, P * (n % 2):P * (n % 2 + 1)] for n in range(4)]
             grouped = transpose_and_regroup(blocks)
             cols = slice(2 * P * pair, 2 * P * (pair + 1))
-            nc.vector.quantize_mx(out=d_codes[:, cols].bitcast(FP8X4), scales=d_scales[:, cols], in_=grouped[:])
+            return lambda: nc.vector.quantize_mx(out=d_codes[:, cols].bitcast(FP8X4), scales=d_scales[:, cols],
+                                                 in_=grouped[:])
 
         def prepare_biases():
             bank = new_bank([P, 4, P])
@@ -145,74 +150,112 @@ def tile_vae_pa_kernel(tc, h, W_mu_e, b_mu_e, W_ls_e, b_ls_e, eps_z, W_in_d, b_i
                                     start=(g == 0), stop=(g == PASSES_1 - 1))
             return acc
 
-        def stage1(half):
-            eps_t = []
+        def transposed_eps(half):
+            banks = []
             for u in range(2):
                 bank = psum.tile([P, BANK], F32, tag="eps", bufs=2)
                 for n in range(HALF_TILES):
                     nc.tensor.transpose(bank[:, P * n:P * (n + 1)],
                                         eps_sb[:, HALF_TILES * half + n, :].bitcast(F32)[:, P * u:P * (u + 1)], ident[:])
-                eps_t.append(bank)
-            ls = [stage1_passes("ls", half, t) for t in range(Z_TILES)]
-            sd = []
-            for u in range(2):
-                sd_u = work.tile([P, 2, BANK], F32, name="sd", bufs=3)
-                for e in range(2):
-                    t = 2 * u + e
-                    nc.scalar.activation(out=sd_u[:, e, :], in_=ls[t][:], func=ACT.Exp,
-                                         bias=half_b_ls[:, t:t + 1], scale=0.5)
-                sd.append(sd_u)
-            mu = [stage1_passes("mu", half, t) for t in range(Z_TILES)]
-            z_planes = work.tile([P, Z_TILES, BANK], BF16, bufs=2)
-            for u in range(2):
-                noise = work.tile([P, 2, BANK], F32, bufs=3)
-                nc.vector.tensor_tensor(out=noise[:], in0=sd[u][:],
-                                        in1=eps_t[u][:].bitcast(BF16).rearrange("p (b e) -> p e b", e=2), op=ALU.mult)
-                for e in range(2):
-                    t = 2 * u + e
-                    nc.vector.scalar_tensor_tensor(out=z_planes[:, t, :], in0=mu[t][:], scalar=b_mu[:, t:t + 1],
-                                                   in1=noise[:, e, :], op0=ALU.add, op1=ALU.add)
-            z_grouped = work.tile([P, BANK, Z_TILES], BF16, align_bytes=64, bufs=2)
-            nc.vector.tensor_copy(out=z_grouped[:].rearrange("p (c i) t -> p c t i", i=4),
-                                  in_=z_planes[:].rearrange("p t (c i) -> p c t i", i=4))
-            cols = slice(BANK * half, BANK * (half + 1))
-            nc.vector.quantize_mx(out=z_codes[:, cols].bitcast(FP8X4), scales=z_scales[:, cols],
-                                  in_=z_grouped[:].rearrange("p b t -> p (b t)"))
+                banks.append(bank)
+            return banks
 
-        def stage2(j, chunk_pair):
-            result = work.tile([P, 2 * BANK], F32, bufs=6)
-            for n in range(2):
-                cols = slice(BANK * (2 * chunk_pair + n), BANK * (2 * chunk_pair + n + 1))
-                acc = new_bank([P, BANK])
-                nc.tensor.matmul_mx(out=acc[:],
-                                    lhsT=z_codes[:, P * j:P * (j + 1)].bitcast(FP8X4),
-                                    lhsT_scale=z_scales[:, P * j:P * (j + 1)],
-                                    rhs=d_codes[:, cols].bitcast(FP8X4),
-                                    rhs_scale=d_scales[:, cols],
-                                    start=True, stop=True)
-                biased = work.tile([P, BANK], F32, bufs=6)
-                nc.vector.tensor_tensor(out=biased[:], in0=acc[:], in1=bd_sb[:, cols], op=ALU.add)
-                nc.scalar.activation(out=result[:, BANK * n:BANK * (n + 1)], in_=biased[:], func=ACT.Tanh)
-            nc.sync.dma_start(out=out_v[:, j, 2 * BANK * chunk_pair:2 * BANK * (chunk_pair + 1)], in_=result[:])
+        def deviations(half):
+            sd = work.tile([P, Z_TILES, BANK], F32, bufs=2)
+            for t in range(Z_TILES):
+                ls = stage1_passes("ls", half, t)
+                nc.scalar.activation(out=sd[:, t, :], in_=ls[:], func=ACT.Exp, bias=half_b_ls[:, t:t + 1], scale=0.5)
+            return sd
+
+        def noise_product(sd, eps_t):
+            noise = work.tile([P, Z_TILES, BANK], F32, bufs=2)
+            for u in range(2):
+                nc.vector.tensor_tensor(out=noise[:, 2 * u:2 * u + 2, :], in0=sd[:, 2 * u:2 * u + 2, :],
+                                        in1=eps_t[u][:].bitcast(BF16).rearrange("p (b e) -> p e b", e=2), op=ALU.mult)
+            return noise
+
+        def quantise_z(z_grouped, half, first, tiles):
+            cols = slice(BANK * half + P * first, BANK * half + P * (first + tiles))
+            nc.vector.quantize_mx(out=z_codes[:, cols].bitcast(FP8X4), scales=z_scales[:, cols],
+                                  in_=z_grouped[:, P * first:P * (first + tiles), :].rearrange("p b t -> p (b t)"))
+
+        results = {}
+
+        def stage2(j, chunk):
+            cols = slice(BANK * chunk, BANK * (chunk + 1))
+            acc = new_bank([P, BANK])
+            nc.tensor.matmul_mx(out=acc[:],
+                                lhsT=z_codes[:, P * j:P * (j + 1)].bitcast(FP8X4),
+                                lhsT_scale=z_scales[:, P * j:P * (j + 1)],
+                                rhs=d_codes[:, cols].bitcast(FP8X4),
+                                rhs_scale=d_scales[:, cols],
+                                start=True, stop=True)
+            biased = work.tile([P, BANK], F32, bufs=6)
+            nc.vector.tensor_tensor(out=biased[:], in0=acc[:], in1=bd_sb[:, cols], op=ALU.add)
+            if chunk % 2 == 0:
+                result = work.tile([P, 2 * BANK], F32, bufs=6)
+                results[j] = result
+            n = chunk % 2
+            nc.scalar.activation(out=results[j][:, BANK * n:BANK * (n + 1)], in_=biased[:], func=ACT.Tanh)
+            if n == 1:
+                nc.sync.dma_start(out=out_v[:, j, BANK * (chunk - 1):BANK * (chunk + 1)], in_=results[j][:])
+
+        ctx.enter_context(tc.manual_schedule())
+        for j in range(HALF_TILES):
+            prepare_h(j)()
+        for t in range(Z_TILES):
+            prepare_w("ls", t)()
+        prepare_biases()
+        sd = deviations(0)
+        quantise = [prepare_w("mu", t) for t in range(2)]
+        noise = noise_product(sd, transposed_eps(0))
+        for t in range(2):
+            quantise[t]()
+        for t in range(2, Z_TILES):
+            prepare_w("mu", t)()
+
+        quantise = prepare_wd(0)
+        for prepare, index in ((prepare_wd, 1), (prepare_h, 4), (prepare_h, 5), (prepare_h, 6)):
+            following = prepare(index)
+            quantise()
+            quantise = following
+        z_planes = work.tile([P, Z_TILES, BANK], BF16)
+        for t in range(Z_TILES):
+            mu = stage1_passes("mu", 0, t)
+            nc.vector.scalar_tensor_tensor(out=z_planes[:, t, :], in0=mu[:], scalar=b_mu[:, t:t + 1],
+                                           in1=noise[:, t, :], op0=ALU.add, op1=ALU.add)
+        z_grouped = work.tile([P, BANK, Z_TILES], BF16, align_bytes=64, bufs=2)
+        nc.gpsimd.tensor_scalar(out=z_grouped[:], in0=z_planes[:].rearrange("p t b -> p b t"), scalar1=1.0, scalar2=0.0,
+                                op0=ALU.mult, op1=ALU.add)
+        for prepare, index in ((prepare_h, 7),) + tuple((prepare_wd, pair) for pair in range(2, 8)):
+            following = prepare(index)
+            quantise()
+            quantise = following
+        quantise()
+
+        eps_t = transposed_eps(1)
+        sd = deviations(1)
+        quantise_z(z_grouped, 0, 0, HALF_TILES)
+        noise = noise_product(sd, eps_t)
+        mu_sb = work.tile([P, Z_TILES, BANK], F32)
+        for t in range(Z_TILES):
+            mu = stage1_passes("mu", 1, t)
+            nc.scalar.activation(out=mu_sb[:, t, :], in_=mu[:], func=ACT.Identity, bias=b_mu[:, t:t + 1])
+        z_grouped = work.tile([P, BANK, Z_TILES], BF16, align_bytes=64, bufs=2)
+        for n in range(HALF_TILES):
+            rows = slice(P * n, P * (n + 1))
+            nc.gpsimd.tensor_tensor(out=z_grouped[:, rows, :], in0=mu_sb[:, :, rows].rearrange("p t b -> p b t"),
+                                    in1=noise[:, :, rows].rearrange("p t b -> p b t"), op=ALU.add)
 
         for j in range(HALF_TILES):
-            prepare_h(j)
-        for u in range(2):
-            for m in ("ls", "mu"):
-                for e in range(2):
-                    prepare_w(m, 2 * u + e)
-        prepare_biases()
-        stage1(0)
-        for pair in range(4):
-            prepare_wd(pair)
+            for chunk in range(2):
+                stage2(j, chunk)
+        for j in range(HALF_TILES):
+            if j == 2:
+                quantise_z(z_grouped, 1, 0, 2)
+            for chunk in range(2, OUT_CHUNKS):
+                stage2(j, chunk)
+        quantise_z(z_grouped, 1, 2, 2)
         for j in range(HALF_TILES, BATCH_TILES):
-            prepare_h(j)
-        for pair in range(4, 8):
-            prepare_wd(pair)
-        stage1(1)
-        for chunk_pair in range(OUT_CHUNKS // 2):
-            for j in range(HALF_TILES):
-                stage2(j, chunk_pair)
-        for j in range(HALF_TILES, BATCH_TILES):
-            for chunk_pair in range(OUT_CHUNKS // 2):
-                stage2(j, chunk_pair)
+            for chunk in range(OUT_CHUNKS):
+                stage2(j, chunk)

@@ -167,12 +167,19 @@ def tile_vae_pa_kernel(tc, h, W_mu_e, b_mu_e, W_ls_e, b_ls_e, eps_z, W_in_d, b_i
                 nc.scalar.activation(out=sd[:, t, :], in_=ls[:], func=ACT.Exp, bias=half_b_ls[:, t:t + 1], scale=0.5)
             return sd
 
-        def noise_product(sd, eps_t):
-            noise = work.tile([P, Z_TILES, BANK], F32, bufs=2)
-            for u in range(2):
-                nc.vector.tensor_tensor(out=noise[:, 2 * u:2 * u + 2, :], in0=sd[:, 2 * u:2 * u + 2, :],
-                                        in1=eps_t[u][:].bitcast(BF16).rearrange("p (b e) -> p e b", e=2), op=ALU.mult)
-            return noise
+        def multiply_noise(noise, sd, eps_t, u):
+            nc.vector.tensor_tensor(out=noise[:, 2 * u:2 * u + 2, :], in0=sd[:, 2 * u:2 * u + 2, :],
+                                    in1=eps_t[u][:].bitcast(BF16).rearrange("p (b e) -> p e b", e=2), op=ALU.mult)
+
+        def add_z(z_planes, mu, noise, t):
+            nc.vector.scalar_tensor_tensor(out=z_planes[:, t, :], in0=mu[:], scalar=b_mu[:, t:t + 1],
+                                           in1=noise[:, t, :], op0=ALU.add, op1=ALU.add)
+
+        def regroup_z(z_planes):
+            z_grouped = work.tile([P, BANK, Z_TILES], BF16, align_bytes=64, bufs=2)
+            nc.vector.tensor_copy(out=z_grouped[:].rearrange("p (c i) t -> p c t i", i=4),
+                                  in_=z_planes[:].rearrange("p t (c i) -> p c t i", i=4))
+            return z_grouped
 
         def quantise_z(z_grouped, half, first, tiles):
             cols = slice(BANK * half + P * first, BANK * half + P * (first + tiles))
@@ -208,54 +215,60 @@ def tile_vae_pa_kernel(tc, h, W_mu_e, b_mu_e, W_ls_e, b_ls_e, eps_z, W_in_d, b_i
         prepare_biases()
         sd = deviations(0)
         quantise = [prepare_w("mu", t) for t in range(2)]
-        noise = noise_product(sd, transposed_eps(0))
+        eps_t = transposed_eps(0)
+        noise = work.tile([P, Z_TILES, BANK], F32, bufs=2)
+        for u in range(2):
+            multiply_noise(noise, sd, eps_t, u)
         for t in range(2):
             quantise[t]()
         for t in range(2, Z_TILES):
             prepare_w("mu", t)()
 
         quantise = prepare_wd(0)
-        for prepare, index in ((prepare_wd, 1), (prepare_h, 4), (prepare_h, 5), (prepare_h, 6)):
+        for prepare, index in ((prepare_wd, 1), (prepare_h, 4), (prepare_h, 5), (prepare_h, 6), (prepare_h, 7)):
             following = prepare(index)
             quantise()
             quantise = following
         z_planes = work.tile([P, Z_TILES, BANK], BF16)
         for t in range(Z_TILES):
-            mu = stage1_passes("mu", 0, t)
-            nc.vector.scalar_tensor_tensor(out=z_planes[:, t, :], in0=mu[:], scalar=b_mu[:, t:t + 1],
-                                           in1=noise[:, t, :], op0=ALU.add, op1=ALU.add)
-        z_grouped = work.tile([P, BANK, Z_TILES], BF16, align_bytes=64, bufs=2)
-        nc.gpsimd.tensor_scalar(out=z_grouped[:], in0=z_planes[:].rearrange("p t b -> p b t"), scalar1=1.0, scalar2=0.0,
-                                op0=ALU.mult, op1=ALU.add)
-        for prepare, index in ((prepare_h, 7),) + tuple((prepare_wd, pair) for pair in range(2, 8)):
-            following = prepare(index)
+            add_z(z_planes, stage1_passes("mu", 0, t), noise, t)
+        for pair in range(2, 8):
+            following = prepare_wd(pair)
             quantise()
             quantise = following
+            if pair == 2:
+                z_grouped = regroup_z(z_planes)
+            if pair == 3:
+                quantise_z(z_grouped, 0, 0, HALF_TILES)
         quantise()
 
         eps_t = transposed_eps(1)
         sd = deviations(1)
-        quantise_z(z_grouped, 0, 0, HALF_TILES)
-        noise = noise_product(sd, eps_t)
-        mu_sb = work.tile([P, Z_TILES, BANK], F32)
-        for t in range(Z_TILES):
-            mu = stage1_passes("mu", 1, t)
-            nc.scalar.activation(out=mu_sb[:, t, :], in_=mu[:], func=ACT.Identity, bias=b_mu[:, t:t + 1])
-        z_grouped = work.tile([P, BANK, Z_TILES], BF16, align_bytes=64, bufs=2)
-        for n in range(HALF_TILES):
-            rows = slice(P * n, P * (n + 1))
-            nc.gpsimd.tensor_tensor(out=z_grouped[:, rows, :], in0=mu_sb[:, :, rows].rearrange("p t b -> p b t"),
-                                    in1=noise[:, :, rows].rearrange("p t b -> p b t"), op=ALU.add)
+        first_half = [(j, chunk) for chunks in ((0, 1), (2, 3)) for j in range(HALF_TILES) for chunk in chunks]
 
-        for j in range(HALF_TILES):
-            for chunk in range(2):
-                stage2(j, chunk)
-        for j in range(HALF_TILES):
-            if j == 2:
-                quantise_z(z_grouped, 1, 0, 2)
-            for chunk in range(2, OUT_CHUNKS):
-                stage2(j, chunk)
-        quantise_z(z_grouped, 1, 2, 2)
+        def next_stage2(count):
+            for n in range(count):
+                block = first_half[0]
+                first_half.remove(block)
+                stage2(*block)
+
+        next_stage2(2)
+        noise = work.tile([P, Z_TILES, BANK], F32, bufs=2)
+        mu = [stage1_passes("mu", 1, 0)]
+        for u in range(2):
+            multiply_noise(noise, sd, eps_t, u)
+            mu.append(stage1_passes("mu", 1, u + 1))
+            next_stage2(1)
+        z_planes = work.tile([P, Z_TILES, BANK], BF16)
+        for t in range(Z_TILES):
+            if t == 1:
+                mu.append(stage1_passes("mu", 1, 3))
+            add_z(z_planes, mu[t], noise, t)
+            next_stage2(1)
+        z_grouped = regroup_z(z_planes)
+        next_stage2(1)
+        quantise_z(z_grouped, 1, 0, HALF_TILES)
+        next_stage2(len(first_half))
         for j in range(HALF_TILES, BATCH_TILES):
             for chunk in range(OUT_CHUNKS):
                 stage2(j, chunk)

@@ -33,7 +33,7 @@ def tile_vae_pa_kernel(tc, h, W_mu_e, b_mu_e, W_ls_e, b_ls_e, eps_z, W_in_d, b_i
         eps_sb = keep.tile([P, BATCH_TILES, 512], BF16)
         w_sb = {"mu": keep.tile([P, 2, 2, 1024], BF16, name="wmu_sb"),
                 "ls": keep.tile([P, 2, 2, 1024], BF16, name="wls_sb")}
-        wd_sb = keep.tile([P, 16, 512], BF16)
+        wd_sb = keep.tile([P, 8, 2, 512], BF16)
         bd_sb = keep.tile([P, 2048], BF16)
         bias_rows = keep.tile([P, P], F32)
         ident = keep.tile([P, P], F32)
@@ -58,7 +58,7 @@ def tile_vae_pa_kernel(tc, h, W_mu_e, b_mu_e, W_ls_e, b_ls_e, eps_z, W_in_d, b_i
         eps_v = eps_z.rearrange("(r j) z -> r j z", j=BATCH_TILES)
         w_v = {"mu": W_mu_e.rearrange("(u p e) k -> p u e k", u=2, e=2),
                "ls": W_ls_e.rearrange("(u p e) k -> p u e k", u=2, e=2)}
-        wd_v = W_in_d.rearrange("(i p) k -> p i k", p=P)
+        wd_v = W_in_d.rearrange("(q p a) k -> p q a k", p=P, a=2)
         out_v = out.rearrange("(r j) n -> r j n", j=BATCH_TILES)
 
         def load_h(first, tiles):
@@ -72,15 +72,16 @@ def tile_vae_pa_kernel(tc, h, W_mu_e, b_mu_e, W_ls_e, b_ls_e, eps_z, W_in_d, b_i
             nc.sync.dma_start(out=w_sb[m][:, u], in_=w_v[m][:, u])
 
         def load_wd(quarter):
-            nc.sync.dma_start(out=wd_sb[:, 4 * quarter:4 * quarter + 4, :], in_=wd_v[:, 4 * quarter:4 * quarter + 4, :])
+            pairs = slice(2 * quarter, 2 * quarter + 2)
+            nc.sync.dma_start(out=wd_sb[:, pairs], in_=wd_v[:, pairs])
 
         load_h(0, 1)
         load_h(1, 1)
+        nc.sync.dma_start(out=bias_rows[0:2, :].bitcast(BF16), in_=b_mu_e.rearrange("(u w) -> u w", u=2))
+        nc.sync.dma_start(out=bias_rows[2:4, :].bitcast(BF16), in_=b_ls_e.rearrange("(u w) -> u w", u=2))
         load_h(2, 2)
         load_w("ls", 0)
         load_w("ls", 1)
-        nc.sync.dma_start(out=bias_rows[0:2, :].bitcast(BF16), in_=b_mu_e.rearrange("(u w) -> u w", u=2))
-        nc.sync.dma_start(out=bias_rows[2:4, :].bitcast(BF16), in_=b_ls_e.rearrange("(u w) -> u w", u=2))
         load_w("mu", 0)
         load_w("mu", 1)
         load_eps(0)
@@ -97,13 +98,17 @@ def tile_vae_pa_kernel(tc, h, W_mu_e, b_mu_e, W_ls_e, b_ls_e, eps_z, W_in_d, b_i
             bank = psum.tile(shape, F32, tag="bank", bufs=6)
             return bank
 
-        def transpose_and_regroup(word_blocks):
+        def transpose_and_regroup(word_blocks, rows_alternate=False):
             bank = new_bank([P, 4, P])
             for n, words in enumerate(word_blocks):
                 nc.tensor.transpose(bank[:, n, :], words, ident[:])
             grouped = work.tile([P, 2 * BANK], BF16, align_bytes=64, bufs=8)
-            nc.scalar.copy(out=grouped[:].bitcast(F32).rearrange("p (a r u) -> p a r u", a=2, u=2),
-                           in_=bank[:].rearrange("p (a u) r -> p a r u", u=2))
+            if rows_alternate:
+                nc.scalar.copy(out=grouped[:].bitcast(F32).rearrange("p (r a u) -> p r a u", a=2, u=2),
+                               in_=bank[:].rearrange("p (a u) r -> p r a u", u=2))
+            else:
+                nc.scalar.copy(out=grouped[:].bitcast(F32).rearrange("p (a r u) -> p a r u", a=2, u=2),
+                               in_=bank[:].rearrange("p (a u) r -> p a r u", u=2))
             return grouped
 
         def prepare_h(j):
@@ -124,8 +129,8 @@ def tile_vae_pa_kernel(tc, h, W_mu_e, b_mu_e, W_ls_e, b_ls_e, eps_z, W_in_d, b_i
                                                  in_=grouped[:])
 
         def prepare_wd(pair):
-            blocks = [wd_sb[:, 2 * pair + n // 2, :].bitcast(F32)[:, P * (n % 2):P * (n % 2 + 1)] for n in range(4)]
-            grouped = transpose_and_regroup(blocks)
+            blocks = [wd_sb[:, pair, n // 2, :].bitcast(F32)[:, P * (n % 2):P * (n % 2 + 1)] for n in range(4)]
+            grouped = transpose_and_regroup(blocks, rows_alternate=True)
             cols = slice(2 * P * pair, 2 * P * (pair + 1))
             return lambda: nc.vector.quantize_mx(out=d_codes[:, cols].bitcast(FP8X4), scales=d_scales[:, cols],
                                                  in_=grouped[:])
@@ -188,31 +193,39 @@ def tile_vae_pa_kernel(tc, h, W_mu_e, b_mu_e, W_ls_e, b_ls_e, eps_z, W_in_d, b_i
 
         results = {}
 
-        def stage2(j, chunk):
-            cols = slice(BANK * chunk, BANK * (chunk + 1))
+        def stage2_columns(j, first, width):
+            cols = slice(first, first + width)
             acc = new_bank([P, BANK])
-            nc.tensor.matmul_mx(out=acc[:],
+            nc.tensor.matmul_mx(out=acc[:, 0:width],
                                 lhsT=z_codes[:, P * j:P * (j + 1)].bitcast(FP8X4),
                                 lhsT_scale=z_scales[:, P * j:P * (j + 1)],
                                 rhs=d_codes[:, cols].bitcast(FP8X4),
                                 rhs_scale=d_scales[:, cols],
                                 start=True, stop=True)
             biased = work.tile([P, BANK], F32, bufs=6)
-            nc.vector.tensor_tensor(out=biased[:], in0=acc[:], in1=bd_sb[:, cols], op=ALU.add)
-            if chunk % 2 == 0:
+            nc.vector.tensor_tensor(out=biased[:, 0:width], in0=acc[:, 0:width], in1=bd_sb[:, cols], op=ALU.add)
+            if first % (2 * BANK) == 0:
                 result = work.tile([P, 2 * BANK], F32, bufs=6)
                 results[j] = result
-            n = chunk % 2
-            nc.scalar.activation(out=results[j][:, BANK * n:BANK * (n + 1)], in_=biased[:], func=ACT.Tanh)
-            if n == 1:
-                nc.sync.dma_start(out=out_v[:, j, BANK * (chunk - 1):BANK * (chunk + 1)], in_=results[j][:])
+            at = first % (2 * BANK)
+            nc.scalar.activation(out=results[j][:, at:at + width], in_=biased[:, 0:width], func=ACT.Tanh)
+
+        def store(j, first, width):
+            at = first % (2 * BANK)
+            nc.sync.dma_start(out=out_v[:, j, first:first + width], in_=results[j][:, at:at + width])
+
+        def stage2(j, chunk):
+            stage2_columns(j, BANK * chunk, BANK)
+            if chunk % 2 == 1:
+                store(j, BANK * (chunk - 1), 2 * BANK)
 
         ctx.enter_context(tc.manual_schedule())
         for j in range(HALF_TILES):
             prepare_h(j)()
         for t in range(Z_TILES):
             prepare_w("ls", t)()
-        prepare_biases()
+            if t == 1:
+                prepare_biases()
         sd = deviations(0)
         quantise = [prepare_w("mu", t) for t in range(2)]
         eps_t = transposed_eps(0)
@@ -269,6 +282,12 @@ def tile_vae_pa_kernel(tc, h, W_mu_e, b_mu_e, W_ls_e, b_ls_e, eps_z, W_in_d, b_i
         next_stage2(1)
         quantise_z(z_grouped, 1, 0, HALF_TILES)
         next_stage2(len(first_half))
-        for j in range(HALF_TILES, BATCH_TILES):
+        last = BATCH_TILES - 1
+        for j in range(HALF_TILES, last):
             for chunk in range(OUT_CHUNKS):
                 stage2(j, chunk)
+        stage2(last, 0)
+        stage2(last, 1)
+        for first, width in ((2 * BANK, BANK), (3 * BANK, BANK // 2), (3 * BANK + BANK // 2, BANK // 2)):
+            stage2_columns(last, first, width)
+            store(last, first, width)

@@ -265,23 +265,25 @@ def tile_vae_pa_kernel(tc, h, W_mu_e, b_mu_e, W_ls_e, b_ls_e, eps_z, W_in_d, b_i
                 first_half.remove(block)
                 stage2(*block)
 
-        next_stage2(2)
         noise = work.tile([P, Z_TILES, BANK], F32, bufs=2)
-        mu = [stage1_passes("mu", 1, 0)]
+        mu_sb = work.tile([P, Z_TILES, BANK], F32, bufs=1)
+        z_planes = work.tile([P, Z_TILES, BANK], BF16)
         for u in range(2):
             multiply_noise(noise, sd, eps_t, u)
-            mu.append(stage1_passes("mu", 1, u + 1))
-            next_stage2(1)
-        z_planes = work.tile([P, Z_TILES, BANK], BF16)
-        for t in range(Z_TILES):
-            if t == 1:
-                mu.append(stage1_passes("mu", 1, 3))
-            add_z(z_planes, mu[t], noise, t)
-            next_stage2(1)
-        z_grouped = regroup_z(z_planes)
-        next_stage2(1)
-        quantise_z(z_grouped, 1, 0, HALF_TILES)
-        next_stage2(len(first_half))
+            for t in (2 * u, 2 * u + 1):
+                mu = stage1_passes("mu", 1, t)
+                nc.scalar.activation(out=mu_sb[:, t, :], in_=mu[:], func=ACT.Identity, bias=b_mu[:, t:t + 1])
+            for t in (2 * u, 2 * u + 1):
+                nc.gpsimd.tensor_tensor(out=z_planes[:, t, :], in0=mu_sb[:, t, :], in1=noise[:, t, :], op=ALU.add)
+        z_grouped = work.tile([P, BANK, Z_TILES], BF16, align_bytes=64, bufs=2)
+        for n in range(2):
+            rows = slice(2 * P * n, 2 * P * (n + 1))
+            nc.gpsimd.tensor_scalar(out=z_grouped[:, rows, :], in0=z_planes[:, :, rows].rearrange("p t b -> p b t"),
+                                    scalar1=1.0, scalar2=0.0, op0=ALU.mult, op1=ALU.add)
+        next_stage2(14)
+        quantise_z(z_grouped, 1, 0, 2)
+        next_stage2(2)
+        quantise_z(z_grouped, 1, 2, 2)
         last = BATCH_TILES - 1
         for j in range(HALF_TILES, last):
             for chunk in range(OUT_CHUNKS):

@@ -33,7 +33,7 @@ def tile_vae_pa_kernel(tc, h, W_mu_e, b_mu_e, W_ls_e, b_ls_e, eps_z, W_in_d, b_i
         eps_sb = keep.tile([P, BATCH_TILES, 512], BF16)
         w_sb = {"mu": keep.tile([P, 2, 2, 1024], BF16, name="wmu_sb"),
                 "ls": keep.tile([P, 2, 2, 1024], BF16, name="wls_sb")}
-        wd_sb = keep.tile([P, 8, 2, 512], BF16)
+        wd_sb = keep.tile([P, OUT_CHUNKS, 4, 512], BF16)
         bd_sb = keep.tile([P, 2048], BF16)
         bias_rows = keep.tile([P, P], F32)
         ident = keep.tile([P, P], F32)
@@ -58,7 +58,7 @@ def tile_vae_pa_kernel(tc, h, W_mu_e, b_mu_e, W_ls_e, b_ls_e, eps_z, W_in_d, b_i
         eps_v = eps_z.rearrange("(r j) z -> r j z", j=BATCH_TILES)
         w_v = {"mu": W_mu_e.rearrange("(u p e) k -> p u e k", u=2, e=2),
                "ls": W_ls_e.rearrange("(u p e) k -> p u e k", u=2, e=2)}
-        wd_v = W_in_d.rearrange("(q p a) k -> p q a k", p=P, a=2)
+        wd_v = W_in_d.rearrange("(c p a) k -> p c a k", p=P, a=4)
         out_v = out.rearrange("(r j) n -> r j n", j=BATCH_TILES)
 
         def load_h(first, tiles):
@@ -71,9 +71,8 @@ def tile_vae_pa_kernel(tc, h, W_mu_e, b_mu_e, W_ls_e, b_ls_e, eps_z, W_in_d, b_i
         def load_w(m, u):
             nc.sync.dma_start(out=w_sb[m][:, u], in_=w_v[m][:, u])
 
-        def load_wd(quarter):
-            pairs = slice(2 * quarter, 2 * quarter + 2)
-            nc.sync.dma_start(out=wd_sb[:, pairs], in_=wd_v[:, pairs])
+        def load_wd(chunk):
+            nc.sync.dma_start(out=wd_sb[:, chunk], in_=wd_v[:, chunk])
 
         load_h(0, 1)
         load_h(1, 1)
@@ -98,17 +97,13 @@ def tile_vae_pa_kernel(tc, h, W_mu_e, b_mu_e, W_ls_e, b_ls_e, eps_z, W_in_d, b_i
             bank = psum.tile(shape, F32, tag="bank", bufs=6)
             return bank
 
-        def transpose_and_regroup(word_blocks, rows_alternate=False):
+        def transpose_and_regroup(word_blocks):
             bank = new_bank([P, 4, P])
             for n, words in enumerate(word_blocks):
                 nc.tensor.transpose(bank[:, n, :], words, ident[:])
             grouped = work.tile([P, 2 * BANK], BF16, align_bytes=64, bufs=8)
-            if rows_alternate:
-                nc.scalar.copy(out=grouped[:].bitcast(F32).rearrange("p (r a u) -> p r a u", a=2, u=2),
-                               in_=bank[:].rearrange("p (a u) r -> p r a u", u=2))
-            else:
-                nc.scalar.copy(out=grouped[:].bitcast(F32).rearrange("p (a r u) -> p a r u", a=2, u=2),
-                               in_=bank[:].rearrange("p (a u) r -> p a r u", u=2))
+            nc.scalar.copy(out=grouped[:].bitcast(F32).rearrange("p (a r u) -> p a r u", a=2, u=2),
+                           in_=bank[:].rearrange("p (a u) r -> p a r u", u=2))
             return grouped
 
         def prepare_h(j):
@@ -129,8 +124,9 @@ def tile_vae_pa_kernel(tc, h, W_mu_e, b_mu_e, W_ls_e, b_ls_e, eps_z, W_in_d, b_i
                                                  in_=grouped[:])
 
         def prepare_wd(pair):
-            blocks = [wd_sb[:, pair, n // 2, :].bitcast(F32)[:, P * (n % 2):P * (n % 2 + 1)] for n in range(4)]
-            grouped = transpose_and_regroup(blocks, rows_alternate=True)
+            blocks = [wd_sb[:, pair // 2, 2 * (pair % 2) + n // 2, :].bitcast(F32)[:, P * (n % 2):P * (n % 2 + 1)]
+                      for n in range(4)]
+            grouped = transpose_and_regroup(blocks)
             cols = slice(2 * P * pair, 2 * P * (pair + 1))
             return lambda: nc.vector.quantize_mx(out=d_codes[:, cols].bitcast(FP8X4), scales=d_scales[:, cols],
                                                  in_=grouped[:])
@@ -193,31 +189,28 @@ def tile_vae_pa_kernel(tc, h, W_mu_e, b_mu_e, W_ls_e, b_ls_e, eps_z, W_in_d, b_i
 
         results = {}
 
-        def stage2_columns(j, first, width):
-            cols = slice(first, first + width)
+        def stage2(j, chunk):
+            cols = slice(BANK * chunk, BANK * (chunk + 1))
             acc = new_bank([P, BANK])
-            nc.tensor.matmul_mx(out=acc[:, 0:width],
+            nc.tensor.matmul_mx(out=acc[:],
                                 lhsT=z_codes[:, P * j:P * (j + 1)].bitcast(FP8X4),
                                 lhsT_scale=z_scales[:, P * j:P * (j + 1)],
                                 rhs=d_codes[:, cols].bitcast(FP8X4),
                                 rhs_scale=d_scales[:, cols],
                                 start=True, stop=True)
             biased = work.tile([P, BANK], F32, bufs=6)
-            nc.vector.tensor_tensor(out=biased[:, 0:width], in0=acc[:, 0:width], in1=bd_sb[:, cols], op=ALU.add)
-            if first % (2 * BANK) == 0:
-                result = work.tile([P, 2 * BANK], F32, bufs=6)
+            nc.vector.tensor_tensor(out=biased[:].rearrange("p (r a) -> p r a", a=4),
+                                    in0=acc[:].rearrange("p (a r) -> p r a", a=4),
+                                    in1=bd_sb[:, cols].rearrange("p (r a) -> p r a", a=4), op=ALU.add)
+            if chunk == 0:
+                result = work.tile([P, OUT_CHUNKS * BANK], F32, bufs=4)
                 results[j] = result
-            at = first % (2 * BANK)
-            nc.scalar.activation(out=results[j][:, at:at + width], in_=biased[:, 0:width], func=ACT.Tanh)
-
-        def store(j, first, width):
-            at = first % (2 * BANK)
-            nc.sync.dma_start(out=out_v[:, j, first:first + width], in_=results[j][:, at:at + width])
-
-        def stage2(j, chunk):
-            stage2_columns(j, BANK * chunk, BANK)
-            if chunk % 2 == 1:
-                store(j, BANK * (chunk - 1), 2 * BANK)
+            nc.scalar.activation(out=results[j][:, cols], in_=biased[:], func=ACT.Tanh)
+            stores = {0: (2, 4), BATCH_TILES - 2: (2, 4), BATCH_TILES - 1: (2, 3, 4)}.get(j, (4,))
+            if chunk + 1 in stores:
+                first = max([0] + [end for end in stores if end <= chunk])
+                done = slice(BANK * first, BANK * (chunk + 1))
+                nc.sync.dma_start(out=out_v[:, j, done], in_=results[j][:, done])
 
         ctx.enter_context(tc.manual_schedule())
         for j in range(HALF_TILES):
@@ -257,7 +250,7 @@ def tile_vae_pa_kernel(tc, h, W_mu_e, b_mu_e, W_ls_e, b_ls_e, eps_z, W_in_d, b_i
 
         eps_t = transposed_eps(1)
         sd = deviations(1)
-        first_half = [(j, chunk) for chunks in ((0, 1), (2, 3)) for j in range(HALF_TILES) for chunk in chunks]
+        first_half = [(j, chunk) for j in range(HALF_TILES) for chunk in range(OUT_CHUNKS)]
 
         def next_stage2(count):
             for n in range(count):
@@ -284,12 +277,6 @@ def tile_vae_pa_kernel(tc, h, W_mu_e, b_mu_e, W_ls_e, b_ls_e, eps_z, W_in_d, b_i
         quantise_z(z_grouped, 1, 0, 2)
         next_stage2(2)
         quantise_z(z_grouped, 1, 2, 2)
-        last = BATCH_TILES - 1
-        for j in range(HALF_TILES, last):
+        for j in range(HALF_TILES, BATCH_TILES):
             for chunk in range(OUT_CHUNKS):
                 stage2(j, chunk)
-        stage2(last, 0)
-        stage2(last, 1)
-        for first, width in ((2 * BANK, BANK), (3 * BANK, BANK // 2), (3 * BANK + BANK // 2, BANK // 2)):
-            stage2_columns(last, first, width)
-            store(last, first, width)

@@ -202,15 +202,16 @@ def tile_vae_pa_kernel(tc, h, W_mu_e, b_mu_e, W_ls_e, b_ls_e, eps_z, W_in_d, b_i
             nc.vector.tensor_tensor(out=biased[:].rearrange("p (r a) -> p r a", a=4),
                                     in0=acc[:].rearrange("p (a r) -> p r a", a=4),
                                     in1=bd_sb[:, cols].rearrange("p (r a) -> p r a", a=4), op=ALU.add)
-            if chunk == 0:
-                result = work.tile([P, OUT_CHUNKS * BANK], F32, bufs=4)
+            if chunk % 2 == 0:
+                result = work.tile([P, 2 * BANK], F32, bufs=6)
                 results[j] = result
-            nc.scalar.activation(out=results[j][:, cols], in_=biased[:], func=ACT.Tanh)
-            stores = {0: (2, 4), BATCH_TILES - 2: (2, 4), BATCH_TILES - 1: (2, 3, 4)}.get(j, (4,))
-            if chunk + 1 in stores:
-                first = max([0] + [end for end in stores if end <= chunk])
-                done = slice(BANK * first, BANK * (chunk + 1))
-                nc.sync.dma_start(out=out_v[:, j, done], in_=results[j][:, done])
+            n = chunk % 2
+            nc.scalar.activation(out=results[j][:, BANK * n:BANK * (n + 1)], in_=biased[:], func=ACT.Tanh)
+            alone = j == BATCH_TILES - 1 and chunk >= OUT_CHUNKS - 2
+            if alone or n == 1:
+                start = n if alone else 0
+                nc.sync.dma_start(out=out_v[:, j, BANK * (chunk - n + start):BANK * (chunk + 1)],
+                                  in_=results[j][:, BANK * start:BANK * (n + 1)])
 
         ctx.enter_context(tc.manual_schedule())
         for j in range(HALF_TILES):
@@ -250,7 +251,7 @@ def tile_vae_pa_kernel(tc, h, W_mu_e, b_mu_e, W_ls_e, b_ls_e, eps_z, W_in_d, b_i
 
         eps_t = transposed_eps(1)
         sd = deviations(1)
-        first_half = [(j, chunk) for j in range(HALF_TILES) for chunk in range(OUT_CHUNKS)]
+        first_half = [(j, chunk) for chunks in ((0, 1), (2, 3)) for j in range(HALF_TILES) for chunk in chunks]
 
         def next_stage2(count):
             for n in range(count):

from contextlib import ExitStack

import concourse.mybir as mybir
from concourse.masks import make_identity

FLOPS = 2 * 1024 * 1024 * 1024 + 2 * 1024 * 512 * 2048

F32 = mybir.dt.float32
BF16 = mybir.dt.bfloat16
U32 = mybir.dt.uint32
U8 = mybir.dt.uint8
FP8X4 = mybir.dt.float8_e4m3fn_x4
ACT = mybir.ActivationFunctionType
ALU = mybir.AluOpType

P = 128
BANK = 512
BATCH_TILES = 8
HALF_TILES = 4
Z_TILES = 4
PASSES_1 = 2
OUT_CHUNKS = 4


def tile_vae_pa_kernel(tc, h, W_mu_e, b_mu_e, W_ls_e, b_ls_e, eps_z, W_in_d, b_in_d, out):
    nc = tc.nc
    with ExitStack() as ctx:
        keep = ctx.enter_context(tc.tile_pool(name="keep", bufs=1))
        work = ctx.enter_context(tc.tile_pool(name="work", bufs=2))
        psum = ctx.enter_context(tc.psum_pool(name="psum", bufs=2))

        h_sb = keep.tile([P, BATCH_TILES, 1024], BF16)
        eps_sb = keep.tile([P, BATCH_TILES, 512], BF16)
        w_sb = {"mu": keep.tile([P, 2, 2, 1024], BF16, name="wmu_sb"),
                "ls": keep.tile([P, 2, 2, 1024], BF16, name="wls_sb")}
        wd_sb = keep.tile([P, OUT_CHUNKS, 4, 512], BF16)
        bd_sb = keep.tile([P, 2048], BF16)
        bias_rows = keep.tile([P, P], F32)
        ident = keep.tile([P, P], F32)
        b_mu = keep.tile([P, Z_TILES], F32)
        half_b_ls = keep.tile([P, Z_TILES], F32)

        h_codes = keep.tile([P, PASSES_1, 1024], U32, align_bytes=64)
        h_scales = keep.tile([P, PASSES_1, 1024], U8, align_bytes=64)
        w_codes = {"mu": keep.tile([P, Z_TILES, PASSES_1 * P], U32, align_bytes=64, name="wmu_codes"),
                   "ls": keep.tile([P, Z_TILES, PASSES_1 * P], U32, align_bytes=64, name="wls_codes")}
        w_scales = {"mu": keep.tile([P, Z_TILES, PASSES_1 * P], U8, align_bytes=64, name="wmu_scales"),
                    "ls": keep.tile([P, Z_TILES, PASSES_1 * P], U8, align_bytes=64, name="wls_scales")}
        d_codes = keep.tile([P, 2048], U32, align_bytes=64)
        d_scales = keep.tile([P, 2048], U8, align_bytes=64)
        z_codes = keep.tile([P, 1024], U32, align_bytes=64)
        z_scales = keep.tile([P, 1024], U8, align_bytes=64)

        nc.vector.memset(bias_rows[:], 0.0)
        make_identity(nc, ident[:])

        h_v = h.rearrange("(r j) k -> r j k", j=BATCH_TILES)
        eps_v = eps_z.rearrange("(r j) z -> r j z", j=BATCH_TILES)
        w_v = {"mu": W_mu_e.rearrange("(u p e) k -> p u e k", u=2, e=2),
               "ls": W_ls_e.rearrange("(u p e) k -> p u e k", u=2, e=2)}
        wd_v = W_in_d.rearrange("(c p a) k -> p c a k", p=P, a=4)
        out_v = out.rearrange("(r j) n -> r j n", j=BATCH_TILES)

        def load_h(first, tiles):
            nc.sync.dma_start(out=h_sb[:, first:first + tiles, :], in_=h_v[:, first:first + tiles, :])

        def load_eps(half):
            tiles = slice(HALF_TILES * half, HALF_TILES * (half + 1))
            nc.sync.dma_start(out=eps_sb[:, tiles, :], in_=eps_v[:, tiles, :])

        def load_w(m, u):
            nc.sync.dma_start(out=w_sb[m][:, u], in_=w_v[m][:, u])

        def load_wd(chunk):
            nc.sync.dma_start(out=wd_sb[:, chunk], in_=wd_v[:, chunk])

        load_h(0, 1)
        load_h(1, 1)
        nc.sync.dma_start(out=bias_rows[0:2, :].bitcast(BF16), in_=b_mu_e.rearrange("(u w) -> u w", u=2))
        nc.sync.dma_start(out=bias_rows[2:4, :].bitcast(BF16), in_=b_ls_e.rearrange("(u w) -> u w", u=2))
        load_h(2, 2)
        load_w("ls", 0)
        load_w("ls", 1)
        load_w("mu", 0)
        load_w("mu", 1)
        load_eps(0)
        load_wd(0)
        load_wd(1)
        load_h(4, 2)
        load_h(6, 2)
        load_wd(2)
        load_wd(3)
        load_eps(1)
        nc.sync.dma_start(out=bd_sb[:], in_=b_in_d.partition_broadcast(P))

        def new_bank(shape):
            bank = psum.tile(shape, F32, tag="bank", bufs=6)
            return bank

        def transpose_and_regroup(word_blocks):
            bank = new_bank([P, 4, P])
            for n, words in enumerate(word_blocks):
                nc.tensor.transpose(bank[:, n, :], words, ident[:])
            grouped = work.tile([P, 2 * BANK], BF16, align_bytes=64, bufs=8)
            nc.scalar.copy(out=grouped[:].bitcast(F32).rearrange("p (a r u) -> p a r u", a=2, u=2),
                           in_=bank[:].rearrange("p (a u) r -> p a r u", u=2))
            return grouped

        def prepare_h(j):
            words = h_sb[:, j, :].bitcast(F32)
            grouped = transpose_and_regroup([words[:, P * n:P * (n + 1)] for n in range(4)])
            rows = slice(P * j, P * (j + 1))

            def quantise():
                for g in range(PASSES_1):
                    nc.vector.quantize_mx(out=h_codes[:, g, rows].bitcast(FP8X4), scales=h_scales[:, g, rows],
                                          in_=grouped[:, BANK * g:BANK * (g + 1)])
            return quantise

        def prepare_w(m, t):
            words = w_sb[m][:, t // 2, t % 2, :].bitcast(F32)
            grouped = transpose_and_regroup([words[:, P * n:P * (n + 1)] for n in range(4)])
            return lambda: nc.vector.quantize_mx(out=w_codes[m][:, t, :].bitcast(FP8X4), scales=w_scales[m][:, t, :],
                                                 in_=grouped[:])

        def prepare_wd(pair):
            blocks = [wd_sb[:, pair // 2, 2 * (pair % 2) + n // 2, :].bitcast(F32)[:, P * (n % 2):P * (n % 2 + 1)]
                      for n in range(4)]
            grouped = transpose_and_regroup(blocks)
            cols = slice(2 * P * pair, 2 * P * (pair + 1))
            return lambda: nc.vector.quantize_mx(out=d_codes[:, cols].bitcast(FP8X4), scales=d_scales[:, cols],
                                                 in_=grouped[:])

        def prepare_biases():
            bank = new_bank([P, 4, P])
            nc.tensor.transpose(bank[:, 0, :], bias_rows[:], ident[:])
            pairs = bank[:, 0, :].bitcast(BF16)
            nc.vector.tensor_copy(out=b_mu[:], in_=pairs[:, 0:Z_TILES])
            nc.vector.tensor_scalar(out=half_b_ls[:], in0=pairs[:, Z_TILES:2 * Z_TILES], scalar1=0.5, scalar2=0.0,
                                    op0=ALU.mult, op1=ALU.add)

        def stage1_passes(m, half, t):
            cols = slice(BANK * half, BANK * (half + 1))
            acc = new_bank([P, BANK])
            for g in range(PASSES_1):
                nc.tensor.matmul_mx(out=acc[:],
                                    lhsT=w_codes[m][:, t, P * g:P * (g + 1)].bitcast(FP8X4),
                                    lhsT_scale=w_scales[m][:, t, P * g:P * (g + 1)],
                                    rhs=h_codes[:, g, cols].bitcast(FP8X4),
                                    rhs_scale=h_scales[:, g, cols],
                                    start=(g == 0), stop=(g == PASSES_1 - 1))
            return acc

        def transposed_eps(half):
            banks = []
            for u in range(2):
                bank = psum.tile([P, BANK], F32, tag="eps", bufs=2)
                for n in range(HALF_TILES):
                    nc.tensor.transpose(bank[:, P * n:P * (n + 1)],
                                        eps_sb[:, HALF_TILES * half + n, :].bitcast(F32)[:, P * u:P * (u + 1)], ident[:])
                banks.append(bank)
            return banks

        def deviations(half):
            sd = work.tile([P, Z_TILES, BANK], F32, bufs=2)
            for t in range(Z_TILES):
                ls = stage1_passes("ls", half, t)
                nc.scalar.activation(out=sd[:, t, :], in_=ls[:], func=ACT.Exp, bias=half_b_ls[:, t:t + 1], scale=0.5)
            return sd

        def multiply_noise(noise, sd, eps_t, u):
            nc.vector.tensor_tensor(out=noise[:, 2 * u:2 * u + 2, :], in0=sd[:, 2 * u:2 * u + 2, :],
                                    in1=eps_t[u][:].bitcast(BF16).rearrange("p (b e) -> p e b", e=2), op=ALU.mult)

        def add_z(z_planes, mu, noise, t):
            nc.vector.scalar_tensor_tensor(out=z_planes[:, t, :], in0=mu[:], scalar=b_mu[:, t:t + 1],
                                           in1=noise[:, t, :], op0=ALU.add, op1=ALU.add)

        def regroup_z(z_planes):
            z_grouped = work.tile([P, BANK, Z_TILES], BF16, align_bytes=64, bufs=2)
            nc.vector.tensor_copy(out=z_grouped[:].rearrange("p (c i) t -> p c t i", i=4),
                                  in_=z_planes[:].rearrange("p t (c i) -> p c t i", i=4))
            return z_grouped

        def quantise_z(z_grouped, half, first, tiles):
            cols = slice(BANK * half + P * first, BANK * half + P * (first + tiles))
            nc.vector.quantize_mx(out=z_codes[:, cols].bitcast(FP8X4), scales=z_scales[:, cols],
                                  in_=z_grouped[:, P * first:P * (first + tiles), :].rearrange("p b t -> p (b t)"))

        results = {}

        def stage2(j, chunk):
            cols = slice(BANK * chunk, BANK * (chunk + 1))
            acc = new_bank([P, BANK])
            nc.tensor.matmul_mx(out=acc[:],
                                lhsT=z_codes[:, P * j:P * (j + 1)].bitcast(FP8X4),
                                lhsT_scale=z_scales[:, P * j:P * (j + 1)],
                                rhs=d_codes[:, cols].bitcast(FP8X4),
                                rhs_scale=d_scales[:, cols],
                                start=True, stop=True)
            biased = work.tile([P, BANK], F32, bufs=6)
            nc.vector.tensor_tensor(out=biased[:].rearrange("p (r a) -> p r a", a=4),
                                    in0=acc[:].rearrange("p (a r) -> p r a", a=4),
                                    in1=bd_sb[:, cols].rearrange("p (r a) -> p r a", a=4), op=ALU.add)
            if chunk % 2 == 0:
                result = work.tile([P, 2 * BANK], F32, bufs=6)
                results[j] = result
            n = chunk % 2
            nc.scalar.activation(out=results[j][:, BANK * n:BANK * (n + 1)], in_=biased[:], func=ACT.Tanh)
            alone = j == BATCH_TILES - 1 and chunk >= OUT_CHUNKS - 2
            if alone or n == 1:
                start = n if alone else 0
                nc.sync.dma_start(out=out_v[:, j, BANK * (chunk - n + start):BANK * (chunk + 1)],
                                  in_=results[j][:, BANK * start:BANK * (n + 1)])

        ctx.enter_context(tc.manual_schedule())
        for j in range(HALF_TILES):
            prepare_h(j)()
        for t in range(Z_TILES):
            prepare_w("ls", t)()
            if t == 1:
                prepare_biases()
        sd = deviations(0)
        quantise = [prepare_w("mu", t) for t in range(2)]
        eps_t = transposed_eps(0)
        noise = work.tile([P, Z_TILES, BANK], F32, bufs=2)
        for u in range(2):
            multiply_noise(noise, sd, eps_t, u)
        for t in range(2):
            quantise[t]()
        for t in range(2, Z_TILES):
            prepare_w("mu", t)()

        quantise = prepare_wd(0)
        for prepare, index in ((prepare_wd, 1), (prepare_h, 4), (prepare_h, 5), (prepare_h, 6), (prepare_h, 7)):
            following = prepare(index)
            quantise()
            quantise = following
        z_planes = work.tile([P, Z_TILES, BANK], BF16)
        for t in range(Z_TILES):
            add_z(z_planes, stage1_passes("mu", 0, t), noise, t)
        for pair in range(2, 8):
            following = prepare_wd(pair)
            quantise()
            quantise = following
            if pair == 2:
                z_grouped = regroup_z(z_planes)
            if pair == 3:
                quantise_z(z_grouped, 0, 0, HALF_TILES)
        quantise()

        eps_t = transposed_eps(1)
        sd = deviations(1)
        first_half = [(j, chunk) for chunks in ((0, 1), (2, 3)) for j in range(HALF_TILES) for chunk in chunks]

        def next_stage2(count):
            for n in range(count):
                block = first_half[0]
                first_half.remove(block)
                stage2(*block)

        noise = work.tile([P, Z_TILES, BANK], F32, bufs=2)
        mu_sb = work.tile([P, Z_TILES, BANK], F32, bufs=1)
        z_planes = work.tile([P, Z_TILES, BANK], BF16)
        for u in range(2):
            multiply_noise(noise, sd, eps_t, u)
            for t in (2 * u, 2 * u + 1):
                mu = stage1_passes("mu", 1, t)
                nc.scalar.activation(out=mu_sb[:, t, :], in_=mu[:], func=ACT.Identity, bias=b_mu[:, t:t + 1])
            for t in (2 * u, 2 * u + 1):
                nc.gpsimd.tensor_tensor(out=z_planes[:, t, :], in0=mu_sb[:, t, :], in1=noise[:, t, :], op=ALU.add)
        z_grouped = work.tile([P, BANK, Z_TILES], BF16, align_bytes=64, bufs=2)
        for n in range(2):
            rows = slice(2 * P * n, 2 * P * (n + 1))
            nc.gpsimd.tensor_scalar(out=z_grouped[:, rows, :], in0=z_planes[:, :, rows].rearrange("p t b -> p b t"),
                                    scalar1=1.0, scalar2=0.0, op0=ALU.mult, op1=ALU.add)
        next_stage2(14)
        quantise_z(z_grouped, 1, 0, 2)
        next_stage2(2)
        quantise_z(z_grouped, 1, 2, 2)
        for j in range(HALF_TILES, BATCH_TILES):
            for chunk in range(OUT_CHUNKS):
                stage2(j, chunk)
